import numpy as np
import ml_dtypes


def mxq(x, axis, fmt="e4m3"):
    dtype, down = {"e4m3": (ml_dtypes.float8_e4m3fn, 7), "e5m2": (ml_dtypes.float8_e5m2, 14)}[fmt]
    v = np.moveaxis(np.asarray(x, np.float32).astype(ml_dtypes.bfloat16).astype(np.float64), axis, -1)
    blocks = v.reshape(v.shape[:-1] + (-1, 32))
    amax = np.abs(blocks).max(-1, keepdims=True)
    byte = np.maximum(np.where(amax > 0, np.frexp(amax)[1] - 1 + 127, 0) - down, 1)
    scale = np.exp2(byte - 127.0)
    codes = (blocks / scale).astype(np.float32).astype(dtype).astype(np.float64)
    return np.moveaxis((codes * scale).reshape(v.shape), -1, axis)


WIDE = False


def mx_kscale(k):
    if not WIDE:
        return np.ones(k)
    levels = np.array([10, -10, 5, -5, 0])
    if k % 512:
        return np.exp2(np.random.permutation(np.resize(levels, k // 32))).repeat(32)
    a = np.empty((k // 512, 16))
    for p in range(k // 512):
        a[p, :8] = np.random.permutation(np.resize(levels, 8))
        for g in range(8):
            far = levels[np.abs(levels - a[p, g]) >= 10]
            a[p, g + 8] = far[np.random.randint(len(far))]
    return np.exp2(a.ravel()).repeat(32)


BF16 = ml_dtypes.bfloat16


def bf(x):
    return np.asarray(x, np.float32).astype(BF16)


def f64(x):
    return np.asarray(x).astype(np.float64)


B, S, D = 1, 1024, 1024


def sigmoid(z):
    return 1.0 / (1.0 + np.exp(-z))


def draw0():
    s, t = mx_kscale(D), mx_kscale(D)
    return {
        'x': bf(np.random.standard_normal((B, S, D)) * s),
        'wq_w': bf(np.random.standard_normal((D, D)) / np.sqrt(D) / s),
        'wq_b': bf(np.random.standard_normal(D) * 0.1),
        'r_aft': bf(np.random.standard_normal((B, S, D)) * 6.0 / np.sqrt(S) * t),
        'out_w': bf(np.random.standard_normal((D, D)) * 6.0 / np.sqrt(D) / t),
        'out_b': bf(np.random.standard_normal(D) * 0.1),
    }


def core(x, wq_w, wq_b, r_aft, out_w, out_b):
    q = (mxq(f64(x), 2, 'e4m3') @ mxq(f64(wq_w), 1, 'e4m3').T) + f64(wq_b)
    y = sigmoid(q) * f64(r_aft)
    return (mxq(y, 2, 'e4m3') @ mxq(f64(out_w), 1, 'e4m3').T) + f64(out_b)


def e4m3fn_bytes(y):
    return np.clip(np.asarray(y, np.float64), -448.0, 448.0).astype(np.float32).astype(ml_dtypes.float8_e4m3fn).view(np.uint8)


def e4m3fn_values(b):
    return np.asarray(b, np.uint8).view(ml_dtypes.float8_e4m3fn).astype(np.float64)


def setup_inputs():
    d = draw0()
    x0 = np.asarray(d['x']).astype(np.float64)
    s = (np.max(np.abs(x0), axis=(0, 1), keepdims=True) / 448.0).astype(np.float32)
    out = {}
    for k, v in d.items():
        if k == 'x':
            out['x_bytes'] = e4m3fn_bytes(x0 / s.astype(np.float64))
            out['x_scale'] = s
        else:
            out[k] = v
    return out


def reference(x_bytes, x_scale, wq_w, wq_b, r_aft, out_w, out_b):
    return core(e4m3fn_values(x_bytes) * x_scale.astype(np.float64), wq_w, wq_b, r_aft, out_w, out_b)

@@ -1,0 +1,298 @@
+from contextlib import ExitStack
+
+import concourse.mybir as mybir
+from concourse.masks import make_identity
+
+F32 = mybir.dt.float32
+BF16 = mybir.dt.bfloat16
+U32 = mybir.dt.uint32
+U8 = mybir.dt.uint8
+FP8 = mybir.dt.float8_e4m3fn
+FP8X4 = mybir.dt.float8_e4m3fn_x4
+MULT = mybir.AluOpType.mult
+ADD = mybir.AluOpType.add
+SIGMOID = mybir.ActivationFunctionType.Sigmoid
+
+P = 128
+TOKENS = 1024
+D = 1024
+FLOPS = 2 * 2 * TOKENS * D * D
+BLOCKS = 4
+TB = TOKENS // BLOCKS
+J = TB // P
+HALF = 512
+
+ORDER = (
+    "C0 C2 W1 X01 X00 W0 w0 x0 X20 W2 W3 X21 C1 W5 w1 W4 C3 w2 M000 "
+    "X10 X11 x1 W6 W7 M001 M010 X30 X31 O03 O02 M101 R00 w3 R01 O01 G00 O00 "
+    "M011 x2 M100 R10 o0 O10 O12 R11 M110 M111 G01 G10 M211 M210 "
+    "R31 O11 O13 Y0 R21 G11 x3 Y1 o1 R20 G21 P000 M200 P100 M201 P111 G20 "
+    "P110 M310 P010 P101 Y2 S10 M311 P011 M300 M301 S11 G31 S01 P001 y31 P201 S00 "
+    "R30 P210 G30 P200 y30 P211 P310 S20 P311 P300 S21 s310 s311 P301 s300 s301"
+)
+
+WIDENED_BY_VECTOR = ((0, 0), (2, 1))
+BIASED_BY_GPSIMD = ((0, 0, 0), (0, 1, 1), (1, 0, 0), (1, 1, 0), (2, 0, 1), (2, 1, 0))
+WARM_UP = 5
+
+
+def tile_aft_full_pb_kernel(tc, x_bytes, x_scale, wq_w, wq_b, r_aft, out_w, out_b, out):
+    nc = tc.nc
+    x_hbm = x_bytes[0, :, :].rearrange("(b p j) k -> b p j k", b=BLOCKS, p=P)
+    r_hbm = r_aft[0, :, :].rearrange("(b p j) k -> b p j k", b=BLOCKS, p=P)
+    out_hbm = out[0, :, :].rearrange("(b p j) n -> b p j n", b=BLOCKS, p=P)
+    wq_hbm = wq_w.rearrange("(f m t) k -> f m t k", f=2, m=P)
+    ow_hbm = out_w.rearrange("(c s m) k -> c m s k", c=2, m=P)
+
+    with ExitStack() as ctx:
+        keep = ctx.enter_context(tc.tile_pool(name="keep", bufs=1))
+        token_banks = ctx.enter_context(tc.psum_pool(name="token_banks", bufs=3))
+        row_banks = ctx.enter_context(tc.psum_pool(name="row_banks", bufs=2))
+        query_banks = ctx.enter_context(tc.psum_pool(name="query_banks", bufs=3))
+        ctx.enter_context(tc.manual_schedule())
+
+        x_mult = keep.tile([P, 2, 4], F32)
+        query_bias = keep.tile([P, 2, 4], BF16)
+        out_bias = keep.tile([P, D], BF16)
+        identity = keep.tile([P, P], F32)
+        zeros = keep.tile([P, HALF], BF16)
+        one_column = keep.tile([P, 1], F32)
+        x_raw = keep.tile([P, BLOCKS, J, D], U8, align_bytes=64)
+        x_wide = keep.tile([P, BLOCKS, J, D], BF16, align_bytes=64)
+        r_raw = keep.tile([P, BLOCKS, J, D], BF16, align_bytes=64)
+        wq_raw = keep.tile([P, 8, D], BF16, align_bytes=64)
+        ow_raw = keep.tile([P, 2, 4, D], BF16, align_bytes=64)
+        x_kin = keep.tile([P, BLOCKS, 2, TB * 4], BF16, align_bytes=64)
+        x_codes = keep.tile([P, BLOCKS, 2, TB], U32, align_bytes=64)
+        x_scales = keep.tile([P, BLOCKS, 2, TB], U8, align_bytes=64)
+        wq_kin = keep.tile([P, 8, 2, P * 4], BF16, align_bytes=64)
+        wq_codes = keep.tile([P, 8, 2, P], U32, align_bytes=64)
+        wq_scales = keep.tile([P, 8, 2, P], U8, align_bytes=64)
+        ow_kin = keep.tile([P, 2, 2, 4, P * 4], BF16, align_bytes=64)
+        ow_codes = keep.tile([P, 2, 2, HALF], U32, align_bytes=64)
+        ow_scales = keep.tile([P, 2, 2, HALF], U8, align_bytes=64)
+        gate_sig = keep.tile([P, 2, 2, 4, TB], F32, align_bytes=64)
+        y_kin = keep.tile([P, BLOCKS, 2, TB * 4], BF16, align_bytes=64)
+        y_codes = keep.tile([P, BLOCKS, 2, TB], U32, align_bytes=64)
+        y_scales = keep.tile([P, BLOCKS, 2, TB], U8, align_bytes=64)
+        result = keep.tile([P, BLOCKS, J, D], F32, align_bytes=64)
+
+        x_words = x_wide[:].bitcast(F32)
+        r_words = r_raw[:].bitcast(F32)
+        wq_words = wq_raw[:].bitcast(F32)
+        ow_words = ow_raw[:].bitcast(F32)
+        wq_kin_words = wq_kin[:].bitcast(F32)
+        ow_kin_words = ow_kin[:].bitcast(F32)
+        bank = {}
+
+        def load_x(b):
+            nc.sync.dma_start(out=x_raw[:, b], in_=x_hbm[b])
+
+        def load_wq(first, count):
+            f, t = first // 4, first % 4
+            nc.sync.dma_start(out=wq_raw[:, first : first + count, :], in_=wq_hbm[f][:, t : t + count, :])
+
+        def load_ow(c, s):
+            nc.sync.dma_start(out=ow_raw[:, c, s : s + 2, :], in_=ow_hbm[c][:, s : s + 2, :])
+
+        def load_r(b):
+            nc.sync.dma_start(out=r_raw[:, b], in_=r_hbm[b])
+
+        def widen(b):
+            for j in range(J):
+                codes = x_raw[:, b, j, :].bitcast(FP8)
+                if (b, j) in WIDENED_BY_VECTOR:
+                    nc.vector.tensor_copy(out=x_wide[:, b, j, :], in_=codes)
+                else:
+                    nc.scalar.copy(out=x_wide[:, b, j, :], in_=codes)
+
+        def turn_tokens(words, b, g):
+            turned = token_banks.tile([P, 2, TB], F32, name="turned")
+            for u in range(2):
+                for j in range(J):
+                    nc.tensor.transpose(
+                        turned[:, u, j * P : (j + 1) * P],
+                        words[:, b, j, 256 * g + u : 256 * (g + 1) : 2],
+                        identity[:],
+                    )
+            return turned
+
+        def turn_rows(row_words):
+            rows = row_banks.tile([P, 4, P], F32, name="rows")
+            for i in range(4):
+                g, u = i // 2, i % 2
+                nc.tensor.transpose(rows[:, i, :], row_words[:, 256 * g + u : 256 * (g + 1) : 2], identity[:])
+            return rows
+
+        def by_k(flat):
+            return flat.rearrange("p (c u e) -> p c u e", u=2, e=2)
+
+        def bank_by_k(turned):
+            return turned[:].bitcast(BF16).rearrange("p u (c e) -> p c u e", e=2)
+
+        def turn_x(b, g):
+            turned = turn_tokens(x_words, b, g)
+            scale = x_mult[:, g, :].rearrange("p (u e) -> p u e", u=2).unsqueeze(1).to_broadcast([P, TB, 2, 2])
+            nc.vector.tensor_tensor(out=by_k(x_kin[:, b, g, :]), in0=bank_by_k(turned), in1=scale, op=MULT)
+
+        def quantise_x(b):
+            nc.vector.quantize_mx(
+                out=x_codes[:, b].rearrange("p g c -> p (g c)").bitcast(FP8X4),
+                scales=x_scales[:, b].rearrange("p g c -> p (g c)"),
+                in_=x_kin[:, b].rearrange("p g c -> p (g c)"),
+            )
+
+        def turn_wq(i):
+            rows = turn_rows(wq_words[:, i, :])
+            nc.scalar.copy(
+                out=wq_kin_words[:, i].rearrange("p g (m u) -> p g m u", u=2),
+                in_=rows[:].rearrange("p (g u) m -> p g m u", u=2),
+            )
+
+        def quantise_wq(i):
+            pair = slice(2 * i, 2 * i + 2)
+            nc.vector.quantize_mx(
+                out=wq_codes[:, pair].rearrange("p s g m -> p (s g m)").bitcast(FP8X4),
+                scales=wq_scales[:, pair].rearrange("p s g m -> p (s g m)"),
+                in_=wq_kin[:, pair].rearrange("p s g m -> p (s g m)"),
+            )
+
+        def turn_ow(c, s):
+            rows = turn_rows(ow_words[:, c, s, :])
+            nc.scalar.copy(
+                out=ow_kin_words[:, c, :, s, :].rearrange("p g (m u) -> p g m u", u=2),
+                in_=rows[:].rearrange("p (g u) m -> p g m u", u=2),
+            )
+
+        def quantise_ow(c):
+            for g in range(2):
+                nc.vector.quantize_mx(
+                    out=ow_codes[:, c, g, :].bitcast(FP8X4),
+                    scales=ow_scales[:, c, g, :],
+                    in_=ow_kin[:, c, g].rearrange("p s m -> p (s m)"),
+                )
+
+        def turn_r(b, f):
+            bank["r", b, f] = turn_tokens(r_words, b, f)
+
+        def query(b, f, h):
+            q = query_banks.tile([P, 2, TB], F32, name="q")
+            for i in range(2):
+                for g in range(2):
+                    nc.tensor.matmul_mx(
+                        out=q[:, i, :],
+                        lhsT=wq_codes[:, 4 * f + 2 * h + i, g, :].bitcast(FP8X4),
+                        lhsT_scale=wq_scales[:, 4 * f + 2 * h + i, g, :],
+                        rhs=x_codes[:, b, g, :].bitcast(FP8X4),
+                        rhs_scale=x_scales[:, b, g, :],
+                        start=(g == 0),
+                        stop=(g == 1),
+                    )
+            for i in range(2):
+                t = 2 * h + i
+                nc.scalar.activation(
+                    out=gate_sig[:, b % 2, f, t, :], in_=q[:, i, :], func=SIGMOID, bias=query_bias[:, f, t : t + 1]
+                )
+
+        def gate(b, f):
+            nc.vector.tensor_tensor(
+                out=by_k(y_kin[:, b, f, :]),
+                in0=bank_by_k(bank["r", b, f]),
+                in1=gate_sig[:, b % 2, f].rearrange("p (u e) c -> p c u e", u=2),
+                op=MULT,
+            )
+
+        def quantise_y(b):
+            nc.vector.quantize_mx(
+                out=y_codes[:, b].rearrange("p f c -> p (f c)").bitcast(FP8X4),
+                scales=y_scales[:, b].rearrange("p f c -> p (f c)"),
+                in_=y_kin[:, b].rearrange("p f c -> p (f c)"),
+            )
+
+        def quantise_y_half(b, f):
+            nc.vector.quantize_mx(
+                out=y_codes[:, b, f, :].bitcast(FP8X4), scales=y_scales[:, b, f, :], in_=y_kin[:, b, f, :]
+            )
+
+        def project(b, j, c):
+            rows = row_banks.tile([P, HALF], F32, name="rows")
+            for g in range(2):
+                nc.tensor.matmul_mx(
+                    out=rows[:],
+                    lhsT=y_codes[:, b, g, j * P : (j + 1) * P].bitcast(FP8X4),
+                    lhsT_scale=y_scales[:, b, g, j * P : (j + 1) * P],
+                    rhs=ow_codes[:, c, g, :].bitcast(FP8X4),
+                    rhs_scale=ow_scales[:, c, g, :],
+                    start=(g == 0),
+                    stop=(g == 1),
+                )
+            if (b, j, c) in BIASED_BY_GPSIMD:
+                columns = slice(HALF * c, HALF * (c + 1))
+                nc.scalar.copy(out=result[:, b, j, columns], in_=rows[:])
+                for first in (HALF * c, HALF * c + HALF // 2):
+                    part = slice(first, first + HALF // 2)
+                    nc.gpsimd.tensor_tensor(
+                        out=result[:, b, j, part], in0=result[:, b, j, part], in1=out_bias[:, part], op=ADD
+                    )
+            else:
+                columns = slice(HALF * c, HALF * (c + 1))
+                nc.vector.tensor_tensor(
+                    out=result[:, b, j, columns], in0=rows[:], in1=out_bias[:, columns], op=ADD
+                )
+
+        def store(b, j):
+            nc.sync.dma_start(out=out_hbm[b][:, j, :], in_=result[:, b, j, :])
+
+        def store_half(b, j, c):
+            columns = slice(HALF * c, HALF * (c + 1))
+            nc.sync.dma_start(out=out_hbm[b][:, j, columns], in_=result[:, b, j, columns])
+
+        nc.scalar.dma_start(out=x_mult[:], in_=x_scale[0, :, :].rearrange("o (g p t) -> p (o g) t", p=P, t=4))
+        nc.scalar.dma_start(out=query_bias[:], in_=wq_b.rearrange("(f p t) -> p f t", p=P, t=4))
+        make_identity(nc, identity[:])
+        nc.vector.memset(zeros[:], 0.0)
+        nc.vector.memset(one_column[:], 0.0)
+        nc.scalar.activation(out=one_column[:], in_=one_column[:], func=SIGMOID)
+
+        load_x(0)
+        load_wq(1, 1)
+        load_x(2)
+        load_wq(0, 1)
+        load_wq(2, 2)
+        load_x(1)
+        load_wq(4, 2)
+        load_x(3)
+        load_wq(6, 2)
+        load_ow(0, 2)
+        load_ow(1, 0)
+        load_ow(0, 0)
+        load_r(0)
+        load_r(1)
+        load_ow(1, 2)
+        load_r(3)
+        load_r(2)
+        nc.sync.dma_start(out=out_bias[:], in_=out_b.partition_broadcast(P))
+
+        warm = query_banks.tile([P, HALF], F32, name="q")
+        for i in range(WARM_UP):
+            nc.tensor.matmul(warm[:], lhsT=zeros[:, :P], rhs=zeros[:], start=True, stop=True)
+
+        steps = {
+            "C": widen,
+            "X": turn_x,
+            "x": quantise_x,
+            "W": turn_wq,
+            "w": quantise_wq,
+            "O": turn_ow,
+            "o": quantise_ow,
+            "R": turn_r,
+            "M": query,
+            "G": gate,
+            "Y": quantise_y,
+            "y": quantise_y_half,
+            "P": project,
+            "S": store,
+            "s": store_half,
+        }
+        for step in ORDER.split():
+            steps[step[0]](*[int(digit) for digit in step[1:]])

@@ -21,19 +21,10 @@ BLOCKS = 4
 TB = TOKENS // BLOCKS
 J = TB // P
 HALF = 512
-
-ORDER = (
-    "C0 C2 W1 X01 X00 W0 w0 x0 X20 W2 W3 X21 C1 W5 w1 W4 C3 w2 M000 "
-    "X10 X11 x1 W6 W7 M001 M010 X30 X31 O03 O02 M101 R00 w3 R01 O01 G00 O00 "
-    "M011 x2 M100 R10 o0 O10 O12 R11 M110 M111 G01 G10 M211 M210 "
-    "R31 O11 O13 Y0 R21 G11 x3 Y1 o1 R20 G21 P000 M200 P100 M201 P111 G20 "
-    "P110 M310 P010 P101 Y2 S10 M311 P011 M300 M301 S11 G31 S01 P001 y31 P201 S00 "
-    "R30 P210 G30 P200 y30 P211 P310 S20 P311 P300 S21 s310 s311 P301 s300 s301"
-)
-
-WIDENED_BY_VECTOR = ((0, 0), (2, 1))
-BIASED_BY_GPSIMD = ((0, 0, 0), (0, 1, 1), (1, 0, 0), (1, 1, 0), (2, 0, 1), (2, 1, 0))
-WARM_UP = 5
+WORDS = HALF // 2
+SORT_BUFS = 4
+KIN_BUFS = 12
+RESULT_BUFS = 8
 
 
 def tile_aft_full_pb_kernel(tc, x_bytes, x_scale, wq_w, wq_b, r_aft, out_w, out_b, out):
@@ -41,258 +32,272 @@ def tile_aft_full_pb_kernel(tc, x_bytes, x_scale, wq_w, wq_b, r_aft, out_w, out_
     x_hbm = x_bytes[0, :, :].rearrange("(b p j) k -> b p j k", b=BLOCKS, p=P)
     r_hbm = r_aft[0, :, :].rearrange("(b p j) k -> b p j k", b=BLOCKS, p=P)
     out_hbm = out[0, :, :].rearrange("(b p j) n -> b p j n", b=BLOCKS, p=P)
-    wq_hbm = wq_w.rearrange("(f m t) k -> f m t k", f=2, m=P)
-    ow_hbm = out_w.rearrange("(c s m) k -> c m s k", c=2, m=P)
+    wq_hbm = wq_w.rearrange("(f m h s) k -> f h m s k", f=2, m=P, h=2)
+    ow_hbm = out_w.rearrange("(i s m) k -> i m s k", i=4, m=P)
 
     with ExitStack() as ctx:
         keep = ctx.enter_context(tc.tile_pool(name="keep", bufs=1))
-        token_banks = ctx.enter_context(tc.psum_pool(name="token_banks", bufs=3))
-        row_banks = ctx.enter_context(tc.psum_pool(name="row_banks", bufs=2))
-        query_banks = ctx.enter_context(tc.psum_pool(name="query_banks", bufs=3))
+        flow = ctx.enter_context(tc.tile_pool(name="flow", bufs=4))
+        banks = ctx.enter_context(tc.psum_pool(name="banks", bufs=6))
+        gate_banks = ctx.enter_context(tc.psum_pool(name="gate_banks", bufs=2))
         ctx.enter_context(tc.manual_schedule())
 
         x_mult = keep.tile([P, 2, 4], F32)
+        x_mult_rows = [keep.tile([P, HALF], F32, name="x_mult_rows%d" % g) for g in range(2)]
         query_bias = keep.tile([P, 2, 4], BF16)
         out_bias = keep.tile([P, D], BF16)
         identity = keep.tile([P, P], F32)
-        zeros = keep.tile([P, HALF], BF16)
         one_column = keep.tile([P, 1], F32)
-        x_raw = keep.tile([P, BLOCKS, J, D], U8, align_bytes=64)
-        x_wide = keep.tile([P, BLOCKS, J, D], BF16, align_bytes=64)
-        r_raw = keep.tile([P, BLOCKS, J, D], BF16, align_bytes=64)
-        wq_raw = keep.tile([P, 8, D], BF16, align_bytes=64)
-        ow_raw = keep.tile([P, 2, 4, D], BF16, align_bytes=64)
-        x_kin = keep.tile([P, BLOCKS, 2, TB * 4], BF16, align_bytes=64)
-        x_codes = keep.tile([P, BLOCKS, 2, TB], U32, align_bytes=64)
-        x_scales = keep.tile([P, BLOCKS, 2, TB], U8, align_bytes=64)
-        wq_kin = keep.tile([P, 8, 2, P * 4], BF16, align_bytes=64)
-        wq_codes = keep.tile([P, 8, 2, P], U32, align_bytes=64)
-        wq_scales = keep.tile([P, 8, 2, P], U8, align_bytes=64)
-        ow_kin = keep.tile([P, 2, 2, 4, P * 4], BF16, align_bytes=64)
-        ow_codes = keep.tile([P, 2, 2, HALF], U32, align_bytes=64)
-        ow_scales = keep.tile([P, 2, 2, HALF], U8, align_bytes=64)
-        gate_sig = keep.tile([P, 2, 2, 4, TB], F32, align_bytes=64)
-        y_kin = keep.tile([P, BLOCKS, 2, TB * 4], BF16, align_bytes=64)
-        y_codes = keep.tile([P, BLOCKS, 2, TB], U32, align_bytes=64)
-        y_scales = keep.tile([P, BLOCKS, 2, TB], U8, align_bytes=64)
-        result = keep.tile([P, BLOCKS, J, D], F32, align_bytes=64)
 
-        x_words = x_wide[:].bitcast(F32)
-        r_words = r_raw[:].bitcast(F32)
-        wq_words = wq_raw[:].bitcast(F32)
-        ow_words = ow_raw[:].bitcast(F32)
-        wq_kin_words = wq_kin[:].bitcast(F32)
-        ow_kin_words = ow_kin[:].bitcast(F32)
-        bank = {}
+        def kept(name, count, shape, dtype):
+            return [keep.tile(shape, dtype, name="%s%d" % (name, i), align_bytes=64) for i in range(count)]
 
-        def load_x(b):
-            nc.sync.dma_start(out=x_raw[:, b], in_=x_hbm[b])
+        x_raw = kept("x_raw", BLOCKS, [P, J, D], U8)
+        r_raw = kept("r_raw", BLOCKS, [P, J, D], BF16)
+        wq_raw = kept("wq_raw", 4, [P, 2, D], BF16)
+        ow_raw = kept("ow_raw", 4, [P, 2, D], BF16)
+        x_codes = kept("x_codes", BLOCKS, [P, 2, TB], U32)
+        x_scales = kept("x_scales", BLOCKS, [P, 2, TB], U8)
+        wq_codes = kept("wq_codes", 4, [P, 2, 2, P], U32)
+        wq_scales = kept("wq_scales", 4, [P, 2, 2, P], U8)
+        ow_codes = kept("ow_codes", 2, [P, 2, HALF], U32)
+        ow_scales = kept("ow_scales", 2, [P, 2, HALF], U8)
+        y_codes = kept("y_codes", BLOCKS, [P, 2, TB], U32)
+        y_scales = kept("y_scales", BLOCKS, [P, 2, TB], U8)
+        gate_sig = kept("gate_sig", 2 * BLOCKS, [P, 4, TB], F32)
+        held = {}
 
-        def load_wq(first, count):
-            f, t = first // 4, first % 4
-            nc.sync.dma_start(out=wq_raw[:, first : first + count, :], in_=wq_hbm[f][:, t : t + count, :])
+        def quantise(codes, scales, values):
+            nc.vector.quantize_mx(out=codes.bitcast(FP8X4), scales=scales, in_=values)
 
-        def load_ow(c, s):
-            nc.sync.dma_start(out=ow_raw[:, c, s : s + 2, :], in_=ow_hbm[c][:, s : s + 2, :])
+        def strided(words, g, u):
+            return words[:, WORDS * g + u : WORDS * (g + 1) : 2]
 
-        def load_r(b):
-            nc.sync.dma_start(out=r_raw[:, b], in_=r_hbm[b])
+        def presorted(words, g, u):
+            return words[:, WORDS * g + P * u : WORDS * g + P * (u + 1)]
 
-        def widen(b):
-            for j in range(J):
-                codes = x_raw[:, b, j, :].bitcast(FP8)
-                if (b, j) in WIDENED_BY_VECTOR:
-                    nc.vector.tensor_copy(out=x_wide[:, b, j, :], in_=codes)
-                else:
-                    nc.scalar.copy(out=x_wide[:, b, j, :], in_=codes)
+        def sort_rows(key, row, engine):
+            ordered = flow.tile([P, HALF], F32, name="ordered", align_bytes=64, bufs=SORT_BUFS)
+            held["sorted", key] = ordered
+            dst = ordered[:].rearrange("p (g u m) -> p g u m", g=2, u=2)
+            src = row.bitcast(F32).rearrange("p (g m u) -> p g u m", g=2, u=2)
+            if engine == "S":
+                nc.scalar.copy(out=dst, in_=src)
+            else:
+                nc.vector.tensor_copy(out=dst, in_=src)
 
-        def turn_tokens(words, b, g):
-            turned = token_banks.tile([P, 2, TB], F32, name="turned")
-            for u in range(2):
-                for j in range(J):
-                    nc.tensor.transpose(
-                        turned[:, u, j * P : (j + 1) * P],
-                        words[:, b, j, 256 * g + u : 256 * (g + 1) : 2],
-                        identity[:],
-                    )
-            return turned
+        def picker(key, row):
+            if ("sorted", key) in held:
+                words = held["sorted", key][:]
+                return lambda g, u: presorted(words, g, u)
+            words = row.bitcast(F32)
+            return lambda g, u: strided(words, g, u)
 
-        def turn_rows(row_words):
-            rows = row_banks.tile([P, 4, P], F32, name="rows")
+        def turn_rows(pick, kin_words):
+            rows = banks.tile([P, 4, P], F32, name="bank")
             for i in range(4):
-                g, u = i // 2, i % 2
-                nc.tensor.transpose(rows[:, i, :], row_words[:, 256 * g + u : 256 * (g + 1) : 2], identity[:])
-            return rows
-
-        def by_k(flat):
-            return flat.rearrange("p (c u e) -> p c u e", u=2, e=2)
-
-        def bank_by_k(turned):
-            return turned[:].bitcast(BF16).rearrange("p u (c e) -> p c u e", e=2)
-
-        def turn_x(b, g):
-            turned = turn_tokens(x_words, b, g)
-            scale = x_mult[:, g, :].rearrange("p (u e) -> p u e", u=2).unsqueeze(1).to_broadcast([P, TB, 2, 2])
-            nc.vector.tensor_tensor(out=by_k(x_kin[:, b, g, :]), in0=bank_by_k(turned), in1=scale, op=MULT)
-
-        def quantise_x(b):
-            nc.vector.quantize_mx(
-                out=x_codes[:, b].rearrange("p g c -> p (g c)").bitcast(FP8X4),
-                scales=x_scales[:, b].rearrange("p g c -> p (g c)"),
-                in_=x_kin[:, b].rearrange("p g c -> p (g c)"),
-            )
-
-        def turn_wq(i):
-            rows = turn_rows(wq_words[:, i, :])
+                nc.tensor.transpose(rows[:, i, :], pick(i // 2, i % 2), identity[:])
             nc.scalar.copy(
-                out=wq_kin_words[:, i].rearrange("p g (m u) -> p g m u", u=2),
+                out=kin_words.rearrange("p g (m u) -> p g m u", u=2),
                 in_=rows[:].rearrange("p (g u) m -> p g m u", u=2),
             )
 
-        def quantise_wq(i):
-            pair = slice(2 * i, 2 * i + 2)
-            nc.vector.quantize_mx(
-                out=wq_codes[:, pair].rearrange("p s g m -> p (s g m)").bitcast(FP8X4),
-                scales=wq_scales[:, pair].rearrange("p s g m -> p (s g m)"),
-                in_=wq_kin[:, pair].rearrange("p s g m -> p (s g m)"),
-            )
+        def spread_scale(g):
+            spread = gate_banks.tile([P, 4, P], F32, name="turned")
+            for t in range(4):
+                nc.tensor.transpose(spread[:, t, :], x_mult[:, g, t : t + 1].to_broadcast([P, P]), identity[:])
+            nc.scalar.copy(out=x_mult_rows[g][:].rearrange("p (m t) -> p m t", t=4), in_=spread[:].rearrange("p t m -> p m t"))
 
-        def turn_ow(c, s):
-            rows = turn_rows(ow_words[:, c, s, :])
-            nc.scalar.copy(
-                out=ow_kin_words[:, c, :, s, :].rearrange("p g (m u) -> p g m u", u=2),
-                in_=rows[:].rearrange("p (g u) m -> p g m u", u=2),
-            )
-
-        def quantise_ow(c):
+        def scale_x(b, j):
+            wide = flow.tile([P, D], BF16, name="x_wide", align_bytes=64, bufs=8)
+            held["x_wide", b, j] = wide
             for g in range(2):
-                nc.vector.quantize_mx(
-                    out=ow_codes[:, c, g, :].bitcast(FP8X4),
-                    scales=ow_scales[:, c, g, :],
-                    in_=ow_kin[:, c, g].rearrange("p s m -> p (s m)"),
+                half = slice(HALF * g, HALF * (g + 1))
+                nc.vector.tensor_tensor(
+                    out=wide[:, half], in0=x_raw[b][:, j, half].bitcast(FP8), in1=x_mult_rows[g][:], op=MULT
                 )
 
-        def turn_r(b, f):
-            bank["r", b, f] = turn_tokens(r_words, b, f)
+        def kin_tile(key):
+            if key not in held:
+                held[key] = flow.tile([P, 2, 4 * TB], BF16, name="kin", align_bytes=64, bufs=KIN_BUFS)
+            return held[key]
 
-        def query(b, f, h):
-            q = query_banks.tile([P, 2, TB], F32, name="q")
-            for i in range(2):
+        def turn_x(b, j):
+            kin = kin_tile(("x", b))
+            turn_rows(picker(("x", b, j), held["x_wide", b, j][:]), kin[:].bitcast(F32)[:, :, WORDS * j : WORDS * (j + 1)])
+
+        def quantise_x(b):
+            quantise(x_codes[b][:].rearrange("p g c -> p (g c)"), x_scales[b][:].rearrange("p g c -> p (g c)"),
+                     held["x", b][:].rearrange("p g c -> p (g c)"))
+
+        def turn_wq(i, s):
+            kin = kin_tile(("wq", i))
+            turn_rows(picker(("wq", i, s), wq_raw[i][:, s, :]), kin[:].bitcast(F32)[:, s, :].rearrange("p (g w) -> p g w", g=2))
+
+        def quantise_wq(i):
+            quantise(wq_codes[i][:].rearrange("p s g m -> p (s g m)"), wq_scales[i][:].rearrange("p s g m -> p (s g m)"),
+                     held["wq", i][:].rearrange("p s c -> p (s c)"))
+
+        def turn_ow(i, s):
+            kin = kin_tile(("ow", i))
+            turn_rows(picker(("ow", i, s), ow_raw[i][:, s, :]), kin[:].bitcast(F32)[:, :, WORDS * s : WORDS * (s + 1)])
+
+        def quantise_ow(i):
+            columns = slice(TB * (i % 2), TB * (i % 2 + 1))
+            for g in range(2):
+                quantise(ow_codes[i // 2][:, g, columns], ow_scales[i // 2][:, g, columns], held["ow", i][:, g, :])
+
+        def turn_r(b, f):
+            turned = gate_banks.tile([P, TB // 2, 2, 2], F32, name="turned")
+            held["r", b, f] = turned
+            for j in range(J):
+                pick = picker(("r", b, j), r_raw[b][:, j, :])
+                for u in range(2):
+                    nc.tensor.transpose(turned[:, 64 * j : 64 * (j + 1), u, :], pick(f, u), identity[:])
+
+        def query(b, i):
+            f, h = i // 2, i % 2
+            q = banks.tile([P, 2, TB], F32, name="bank")
+            for s in range(2):
                 for g in range(2):
                     nc.tensor.matmul_mx(
-                        out=q[:, i, :],
-                        lhsT=wq_codes[:, 4 * f + 2 * h + i, g, :].bitcast(FP8X4),
-                        lhsT_scale=wq_scales[:, 4 * f + 2 * h + i, g, :],
-                        rhs=x_codes[:, b, g, :].bitcast(FP8X4),
-                        rhs_scale=x_scales[:, b, g, :],
+                        out=q[:, s, :],
+                        lhsT=wq_codes[i][:, s, g, :].bitcast(FP8X4),
+                        lhsT_scale=wq_scales[i][:, s, g, :],
+                        rhs=x_codes[b][:, g, :].bitcast(FP8X4),
+                        rhs_scale=x_scales[b][:, g, :],
                         start=(g == 0),
                         stop=(g == 1),
                     )
-            for i in range(2):
-                t = 2 * h + i
+            for s in range(2):
+                t = 2 * h + s
                 nc.scalar.activation(
-                    out=gate_sig[:, b % 2, f, t, :], in_=q[:, i, :], func=SIGMOID, bias=query_bias[:, f, t : t + 1]
+                    out=gate_sig[2 * b + f][:, t, :], in_=q[:, s, :], func=SIGMOID, bias=query_bias[:, f, t : t + 1]
                 )
 
         def gate(b, f):
+            kin = kin_tile(("y", b))
             nc.vector.tensor_tensor(
-                out=by_k(y_kin[:, b, f, :]),
-                in0=bank_by_k(bank["r", b, f]),
-                in1=gate_sig[:, b % 2, f].rearrange("p (u e) c -> p c u e", u=2),
+                out=kin[:, f, :].rearrange("p (c i u e) -> p c u e i", i=2, u=2, e=2),
+                in0=held["r", b, f][:].bitcast(BF16).rearrange("p c u (i e) -> p c u e i", e=2),
+                in1=gate_sig[2 * b + f][:].rearrange("p (u e) (c i) -> p c u e i", u=2, i=2),
                 op=MULT,
             )
 
-        def quantise_y(b):
-            nc.vector.quantize_mx(
-                out=y_codes[:, b].rearrange("p f c -> p (f c)").bitcast(FP8X4),
-                scales=y_scales[:, b].rearrange("p f c -> p (f c)"),
-                in_=y_kin[:, b].rearrange("p f c -> p (f c)"),
-            )
-
-        def quantise_y_half(b, f):
-            nc.vector.quantize_mx(
-                out=y_codes[:, b, f, :].bitcast(FP8X4), scales=y_scales[:, b, f, :], in_=y_kin[:, b, f, :]
-            )
+        def quantise_y(b, f):
+            quantise(y_codes[b][:, f, :], y_scales[b][:, f, :], held["y", b][:, f, :])
 
         def project(b, j, c):
-            rows = row_banks.tile([P, HALF], F32, name="rows")
+            rows = banks.tile([P, HALF], F32, name="bank")
+            held["out", b, j, c] = rows
             for g in range(2):
                 nc.tensor.matmul_mx(
                     out=rows[:],
-                    lhsT=y_codes[:, b, g, j * P : (j + 1) * P].bitcast(FP8X4),
-                    lhsT_scale=y_scales[:, b, g, j * P : (j + 1) * P],
-                    rhs=ow_codes[:, c, g, :].bitcast(FP8X4),
-                    rhs_scale=ow_scales[:, c, g, :],
+                    lhsT=y_codes[b][:, g, j * P : (j + 1) * P].bitcast(FP8X4),
+                    lhsT_scale=y_scales[b][:, g, j * P : (j + 1) * P],
+                    rhs=ow_codes[c][:, g, :].bitcast(FP8X4),
+                    rhs_scale=ow_scales[c][:, g, :],
                     start=(g == 0),
                     stop=(g == 1),
                 )
-            if (b, j, c) in BIASED_BY_GPSIMD:
-                columns = slice(HALF * c, HALF * (c + 1))
-                nc.scalar.copy(out=result[:, b, j, columns], in_=rows[:])
-                for first in (HALF * c, HALF * c + HALF // 2):
-                    part = slice(first, first + HALF // 2)
-                    nc.gpsimd.tensor_tensor(
-                        out=result[:, b, j, part], in0=result[:, b, j, part], in1=out_bias[:, part], op=ADD
-                    )
-            else:
-                columns = slice(HALF * c, HALF * (c + 1))
-                nc.vector.tensor_tensor(
-                    out=result[:, b, j, columns], in0=rows[:], in1=out_bias[:, columns], op=ADD
-                )
 
-        def store(b, j):
-            nc.sync.dma_start(out=out_hbm[b][:, j, :], in_=result[:, b, j, :])
-
-        def store_half(b, j, c):
+        def finish(b, j, c, engine):
             columns = slice(HALF * c, HALF * (c + 1))
-            nc.sync.dma_start(out=out_hbm[b][:, j, columns], in_=result[:, b, j, columns])
+            result = flow.tile([P, HALF], F32, name="result", align_bytes=64, bufs=RESULT_BUFS)
+            held["result", b, j, c] = result
+            if engine == "V":
+                nc.vector.tensor_tensor(out=result[:], in0=held["out", b, j, c][:], in1=out_bias[:, columns], op=ADD)
+                store(b, j, c)
+            else:
+                nc.scalar.copy(out=result[:], in_=held["out", b, j, c][:])
+                nc.gpsimd.tensor_tensor(out=result[:], in0=result[:], in1=out_bias[:, columns], op=ADD)
 
-        nc.scalar.dma_start(out=x_mult[:], in_=x_scale[0, :, :].rearrange("o (g p t) -> p (o g) t", p=P, t=4))
+        def store(b, j, c):
+            nc.sync.dma_start(out=out_hbm[b][:, j, HALF * c : HALF * (c + 1)], in_=held["result", b, j, c][:])
+
+        def load_x(b):
+            nc.sync.dma_start(out=x_raw[b][:], in_=x_hbm[b])
+
+        def load_r(b):
+            nc.sync.dma_start(out=r_raw[b][:], in_=r_hbm[b])
+
+        def load_wq(i):
+            nc.sync.dma_start(out=wq_raw[i][:], in_=wq_hbm[i // 2][i % 2])
+
+        def load_ow(i):
+            nc.sync.dma_start(out=ow_raw[i][:], in_=ow_hbm[i])
+
+        nc.sync.dma_start(out=x_mult[:], in_=x_scale[0, :, :].rearrange("o (g p t) -> p (o g) t", p=P, t=4))
         nc.scalar.dma_start(out=query_bias[:], in_=wq_b.rearrange("(f p t) -> p f t", p=P, t=4))
+        nc.gpsimd.memset(one_column[:], 0.0)
         make_identity(nc, identity[:])
-        nc.vector.memset(zeros[:], 0.0)
-        nc.vector.memset(one_column[:], 0.0)
         nc.scalar.activation(out=one_column[:], in_=one_column[:], func=SIGMOID)
 
+        load_wq(0)
         load_x(0)
-        load_wq(1, 1)
-        load_x(2)
-        load_wq(0, 1)
-        load_wq(2, 2)
+        load_wq(1)
         load_x(1)
-        load_wq(4, 2)
+        load_wq(2)
+        load_wq(3)
+        load_x(2)
+        load_ow(0)
         load_x(3)
-        load_wq(6, 2)
-        load_ow(0, 2)
-        load_ow(1, 0)
-        load_ow(0, 0)
+        load_ow(1)
         load_r(0)
+        load_ow(2)
+        load_ow(3)
         load_r(1)
-        load_ow(1, 2)
-        load_r(3)
-        load_r(2)
         nc.sync.dma_start(out=out_bias[:], in_=out_b.partition_broadcast(P))
+        load_r(2)
+        load_r(3)
 
-        warm = query_banks.tile([P, HALF], F32, name="q")
-        for i in range(WARM_UP):
-            nc.tensor.matmul(warm[:], lhsT=zeros[:, :P], rhs=zeros[:], start=True, stop=True)
+        for g in range(2):
+            spread_scale(g)
+        for b in range(BLOCKS):
+            for j in range(J):
+                scale_x(b, j)
+        weights = [(turn_wq, i) for i in range(4)] + [(turn_ow, i) for i in range(4)]
+        runs = weights[:2] + [(turn_x, 0)] + weights[2:4] + [(turn_x, 1), weights[4], (turn_x, 2), weights[5], (turn_x, 3)] + weights[6:]
+        for turn, i in runs:
+            for s in range(2):
+                turn(i, s)
+        quantise_wq(0)
+        quantise_x(0)
+        for i in range(1, 4):
+            quantise_wq(i)
+        quantise_x(1)
+        for i in range(4):
+            quantise_ow(i)
+        for b in range(2, BLOCKS):
+            quantise_x(b)
 
-        steps = {
-            "C": widen,
-            "X": turn_x,
-            "x": quantise_x,
-            "W": turn_wq,
-            "w": quantise_wq,
-            "O": turn_ow,
-            "o": quantise_ow,
-            "R": turn_r,
-            "M": query,
-            "G": gate,
-            "Y": quantise_y,
-            "y": quantise_y_half,
-            "P": project,
-            "S": store,
-            "s": store_half,
-        }
-        for step in ORDER.split():
-            steps[step[0]](*[int(digit) for digit in step[1:]])
+        tiles = [(j, c) for c in range(2) for j in range(J)]
+
+        def project_and_finish(b, some):
+            for j, c in some:
+                project(b, j, c)
+                finish(b, j, c, "V")
+
+        for i in range(4):
+            query(0, i)
+        last = BLOCKS - 1
+        for b in range(last):
+            for f in range(2):
+                turn_r(b, f)
+            for f in range(2):
+                gate(b, f)
+            for i in range(4):
+                query(b + 1, i)
+            for f in range(2):
+                quantise_y(b, f)
+            if b > 0:
+                project_and_finish(b - 1, tiles)
+        for f in range(2):
+            turn_r(last, f)
+        for f in range(2):
+            gate(last, f)
+            project_and_finish(last - 1, tiles[f : f + 1])
+        for f in range(2):
+            quantise_y(last, f)
+        project_and_finish(last - 1, tiles[2:])
+        project_and_finish(last, tiles)

@@ -23,8 +23,8 @@ J = TB // P
 HALF = 512
 WORDS = HALF // 2
 SORT_BUFS = 4
-KIN_BUFS = 12
-RESULT_BUFS = 8
+KIN_BUFS = 9
+RESULT_BUFS = 16
 
 
 def tile_aft_full_pb_kernel(tc, x_bytes, x_scale, wq_w, wq_b, r_aft, out_w, out_b, out):
@@ -54,7 +54,8 @@ def tile_aft_full_pb_kernel(tc, x_bytes, x_scale, wq_w, wq_b, r_aft, out_w, out_
 
         x_raw = kept("x_raw", BLOCKS, [P, J, D], U8)
         r_raw = kept("r_raw", BLOCKS, [P, J, D], BF16)
-        wq_raw = kept("wq_raw", 4, [P, 2, D], BF16)
+        wq_first = kept("wq_first", 2, [P, D], BF16)
+        wq_raw = [None] + kept("wq_raw", 3, [P, 2, D], BF16)
         ow_raw = kept("ow_raw", 4, [P, 2, D], BF16)
         x_codes = kept("x_codes", BLOCKS, [P, 2, TB], U32)
         x_scales = kept("x_scales", BLOCKS, [P, 2, TB], U8)
@@ -94,16 +95,14 @@ def tile_aft_full_pb_kernel(tc, x_bytes, x_scale, wq_w, wq_b, r_aft, out_w, out_
             return lambda g, u: strided(words, g, u)
 
         def turn_rows(pick, kin_words):
-            rows = banks.tile([P, 4, P], F32, name="bank")
-            for i in range(4):
-                nc.tensor.transpose(rows[:, i, :], pick(i // 2, i % 2), identity[:])
-            nc.scalar.copy(
-                out=kin_words.rearrange("p g (m u) -> p g m u", u=2),
-                in_=rows[:].rearrange("p (g u) m -> p g m u", u=2),
-            )
+            rows = banks.tile([P, 2, P // 2, 2, 2], F32, name="bank")
+            for g in range(2):
+                for u in range(2):
+                    nc.tensor.transpose(rows[:, g, :, u, :], pick(g, u), identity[:])
+            nc.scalar.copy(out=kin_words.rearrange("p g (c i u) -> p g c u i", i=2, u=2), in_=rows[:])
 
         def spread_scale(g):
-            spread = gate_banks.tile([P, 4, P], F32, name="turned")
+            spread = banks.tile([P, 4, P], F32, name="bank")
             for t in range(4):
                 nc.tensor.transpose(spread[:, t, :], x_mult[:, g, t : t + 1].to_broadcast([P, P]), identity[:])
             nc.scalar.copy(out=x_mult_rows[g][:].rearrange("p (m t) -> p m t", t=4), in_=spread[:].rearrange("p t m -> p m t"))
@@ -116,6 +115,35 @@ def tile_aft_full_pb_kernel(tc, x_bytes, x_scale, wq_w, wq_b, r_aft, out_w, out_
                 nc.vector.tensor_tensor(
                     out=wide[:, half], in0=x_raw[b][:, j, half].bitcast(FP8), in1=x_mult_rows[g][:], op=MULT
                 )
+
+        def widen(b, j, engine):
+            wide = flow.tile([P, D], BF16, name="x_wide", align_bytes=64, bufs=8)
+            held["x_wide", b, j] = wide
+            codes = x_raw[b][:, j, :].bitcast(FP8)
+            if engine == "V":
+                nc.vector.tensor_copy(out=wide[:], in_=codes)
+            elif engine == "S":
+                nc.scalar.copy(out=wide[:], in_=codes)
+            else:
+                nc.gpsimd.tensor_copy(out=wide[:], in_=codes)
+
+        def turn_wide(b, g):
+            turned = banks.tile([P, TB // 2, 2, 2], F32, name="bank")
+            held["turned", b, g] = turned
+            for j in range(J):
+                pick = picker(("x", b, j), held["x_wide", b, j][:])
+                for u in range(2):
+                    nc.tensor.transpose(turned[:, 64 * j : 64 * (j + 1), u, :], pick(g, u), identity[:])
+
+        def scale_turned(b, g):
+            kin = kin_tile(("x", b))
+            scale = x_mult[:, g, :].unsqueeze(1).unsqueeze(3).to_broadcast([P, TB // 2, 4, 2])
+            nc.vector.tensor_tensor(
+                out=kin[:, g, :].rearrange("p (c i u e) -> p c u e i", i=2, u=2, e=2),
+                in0=held["turned", b, g][:].bitcast(BF16).rearrange("p c u (i e) -> p c u e i", e=2),
+                in1=scale.rearrange("p c (u e) i -> p c u e i", u=2),
+                op=MULT,
+            )
 
         def kin_tile(key):
             if key not in held:
@@ -132,7 +160,7 @@ def tile_aft_full_pb_kernel(tc, x_bytes, x_scale, wq_w, wq_b, r_aft, out_w, out_
 
         def turn_wq(i, s):
             kin = kin_tile(("wq", i))
-            turn_rows(picker(("wq", i, s), wq_raw[i][:, s, :]), kin[:].bitcast(F32)[:, s, :].rearrange("p (g w) -> p g w", g=2))
+            turn_rows(picker(("wq", i, s), wq_raw[i][:, s, :] if i else wq_first[s][:]), kin[:].bitcast(F32)[:, s, :].rearrange("p (g w) -> p g w", g=2))
 
         def quantise_wq(i):
             quantise(wq_codes[i][:].rearrange("p s g m -> p (s g m)"), wq_scales[i][:].rearrange("p s g m -> p (s g m)"),
@@ -184,8 +212,30 @@ def tile_aft_full_pb_kernel(tc, x_bytes, x_scale, wq_w, wq_b, r_aft, out_w, out_
                 op=MULT,
             )
 
+        def gate_tokens(b, f, j):
+            kin = kin_tile(("y", b))
+            nc.vector.tensor_tensor(
+                out=kin[:, j, HALF * f : HALF * (f + 1)].rearrange("p (c i u e) -> p c u e i", i=2, u=2, e=2),
+                in0=held["r", b, f][:, 64 * j : 64 * (j + 1)].bitcast(BF16).rearrange("p c u (i e) -> p c u e i", e=2),
+                in1=gate_sig[2 * b + f][:, :, P * j : P * (j + 1)].rearrange("p (u e) (c i) -> p c u e i", u=2, i=2),
+                op=MULT,
+            )
+
+        def quantise_tokens(b, j):
+            held["by tokens", b] = True
+            quantise(y_codes[b][:, j, :], y_scales[b][:, j, :], held["y", b][:, j, :])
+
+        def quantise_block(b):
+            quantise(y_codes[b][:].rearrange("p f c -> p (f c)"), y_scales[b][:].rearrange("p f c -> p (f c)"),
+                     held["y", b][:].rearrange("p f c -> p (f c)"))
+
         def quantise_y(b, f):
             quantise(y_codes[b][:, f, :], y_scales[b][:, f, :], held["y", b][:, f, :])
+
+        def y_part(tiles, b, j, g):
+            if ("by tokens", b) in held:
+                return tiles[b][:, j, g * P : (g + 1) * P]
+            return tiles[b][:, g, j * P : (j + 1) * P]
 
         def project(b, j, c):
             rows = banks.tile([P, HALF], F32, name="bank")
@@ -193,8 +243,8 @@ def tile_aft_full_pb_kernel(tc, x_bytes, x_scale, wq_w, wq_b, r_aft, out_w, out_
             for g in range(2):
                 nc.tensor.matmul_mx(
                     out=rows[:],
-                    lhsT=y_codes[b][:, g, j * P : (j + 1) * P].bitcast(FP8X4),
-                    lhsT_scale=y_scales[b][:, g, j * P : (j + 1) * P],
+                    lhsT=y_part(y_codes, b, j, g).bitcast(FP8X4),
+                    lhsT_scale=y_part(y_scales, b, j, g),
                     rhs=ow_codes[c][:, g, :].bitcast(FP8X4),
                     rhs_scale=ow_scales[c][:, g, :],
                     start=(g == 0),
@@ -224,6 +274,9 @@ def tile_aft_full_pb_kernel(tc, x_bytes, x_scale, wq_w, wq_b, r_aft, out_w, out_
         def load_wq(i):
             nc.sync.dma_start(out=wq_raw[i][:], in_=wq_hbm[i // 2][i % 2])
 
+        def load_wq_first(s):
+            nc.sync.dma_start(out=wq_first[s][:], in_=wq_hbm[0][0][:, s, :])
+
         def load_ow(i):
             nc.sync.dma_start(out=ow_raw[i][:], in_=ow_hbm[i])
 
@@ -232,72 +285,144 @@ def tile_aft_full_pb_kernel(tc, x_bytes, x_scale, wq_w, wq_b, r_aft, out_w, out_
         nc.gpsimd.memset(one_column[:], 0.0)
         make_identity(nc, identity[:])
         nc.scalar.activation(out=one_column[:], in_=one_column[:], func=SIGMOID)
-
-        load_wq(0)
+        load_wq_first(0)
         load_x(0)
+        load_wq_first(1)
         load_wq(1)
         load_x(1)
         load_wq(2)
         load_wq(3)
-        load_x(2)
         load_ow(0)
-        load_x(3)
+        load_x(2)
         load_ow(1)
+        load_x(3)
         load_r(0)
+        load_r(1)
         load_ow(2)
         load_ow(3)
-        load_r(1)
         nc.sync.dma_start(out=out_bias[:], in_=out_b.partition_broadcast(P))
         load_r(2)
         load_r(3)
-
-        for g in range(2):
-            spread_scale(g)
-        for b in range(BLOCKS):
-            for j in range(J):
-                scale_x(b, j)
-        weights = [(turn_wq, i) for i in range(4)] + [(turn_ow, i) for i in range(4)]
-        runs = weights[:2] + [(turn_x, 0)] + weights[2:4] + [(turn_x, 1), weights[4], (turn_x, 2), weights[5], (turn_x, 3)] + weights[6:]
-        for turn, i in runs:
-            for s in range(2):
-                turn(i, s)
+        spread_scale(0)
+        spread_scale(1)
+        scale_x(0, 0)
+        scale_x(0, 1)
+        turn_wq(0, 0)
+        turn_wq(0, 1)
+        turn_x(0, 0)
+        scale_x(1, 0)
+        scale_x(1, 1)
+        turn_wq(1, 0)
+        turn_wq(1, 1)
+        turn_x(0, 1)
         quantise_wq(0)
+        turn_wq(2, 0)
+        turn_wq(2, 1)
         quantise_x(0)
-        for i in range(1, 4):
-            quantise_wq(i)
+        scale_x(2, 0)
+        turn_wq(3, 0)
+        turn_wq(3, 1)
+        quantise_wq(1)
+        scale_x(2, 1)
+        turn_x(1, 0)
+        turn_x(1, 1)
+        quantise_wq(2)
+        scale_x(3, 0)
+        query(0, 0)
+        turn_ow(0, 0)
+        turn_ow(0, 1)
+        turn_x(2, 0)
+        quantise_wq(3)
+        scale_x(3, 1)
+        query(0, 1)
+        turn_x(2, 1)
+        turn_ow(1, 0)
+        turn_ow(1, 1)
         quantise_x(1)
-        for i in range(4):
-            quantise_ow(i)
-        for b in range(2, BLOCKS):
-            quantise_x(b)
-
-        tiles = [(j, c) for c in range(2) for j in range(J)]
-
-        def project_and_finish(b, some):
-            for j, c in some:
-                project(b, j, c)
-                finish(b, j, c, "V")
-
-        for i in range(4):
-            query(0, i)
-        last = BLOCKS - 1
-        for b in range(last):
-            for f in range(2):
-                turn_r(b, f)
-            for f in range(2):
-                gate(b, f)
-            for i in range(4):
-                query(b + 1, i)
-            for f in range(2):
-                quantise_y(b, f)
-            if b > 0:
-                project_and_finish(b - 1, tiles)
-        for f in range(2):
-            turn_r(last, f)
-        for f in range(2):
-            gate(last, f)
-            project_and_finish(last - 1, tiles[f : f + 1])
-        for f in range(2):
-            quantise_y(last, f)
-        project_and_finish(last - 1, tiles[2:])
-        project_and_finish(last, tiles)
+        quantise_ow(0)
+        query(0, 2)
+        turn_r(0, 0)
+        turn_x(3, 0)
+        turn_x(3, 1)
+        quantise_x(2)
+        gate(0, 0)
+        quantise_ow(1)
+        query(0, 3)
+        turn_ow(2, 0)
+        turn_ow(2, 1)
+        turn_r(0, 1)
+        quantise_x(3)
+        sort_rows(("r", 1, 0), r_raw[1][:, 0, :], "V")
+        sort_rows(("r", 1, 1), r_raw[1][:, 1, :], "V")
+        gate(0, 1)
+        query(1, 0)
+        query(1, 1)
+        query(1, 2)
+        query(1, 3)
+        quantise_ow(2)
+        quantise_block(0)
+        turn_r(1, 0)
+        turn_r(1, 1)
+        turn_ow(3, 0)
+        turn_ow(3, 1)
+        gate(1, 0)
+        gate(1, 1)
+        project(0, 0, 0)
+        project(0, 1, 0)
+        sort_rows(("r", 2, 0), r_raw[2][:, 0, :], "S")
+        sort_rows(("r", 2, 1), r_raw[2][:, 1, :], "S")
+        query(2, 0)
+        query(2, 1)
+        query(2, 2)
+        query(2, 3)
+        finish(0, 0, 0, "V")
+        finish(0, 1, 0, "V")
+        quantise_ow(3)
+        quantise_block(1)
+        sort_rows(("r", 3, 0), r_raw[3][:, 0, :], "S")
+        sort_rows(("r", 3, 1), r_raw[3][:, 1, :], "S")
+        project(0, 0, 1)
+        finish(0, 0, 1, "V")
+        project(0, 1, 1)
+        finish(0, 1, 1, "V")
+        project(1, 0, 0)
+        finish(1, 0, 0, "V")
+        project(1, 1, 0)
+        finish(1, 1, 0, "V")
+        turn_r(2, 0)
+        turn_r(2, 1)
+        gate(2, 0)
+        gate(2, 1)
+        query(3, 0)
+        query(3, 1)
+        query(3, 2)
+        query(3, 3)
+        quantise_block(2)
+        project(1, 0, 1)
+        finish(1, 0, 1, "V")
+        project(1, 1, 1)
+        finish(1, 1, 1, "V")
+        project(2, 0, 0)
+        finish(2, 0, 0, "V")
+        project(2, 1, 0)
+        finish(2, 1, 0, "V")
+        turn_r(3, 0)
+        turn_r(3, 1)
+        gate_tokens(3, 0, 0)
+        gate_tokens(3, 1, 0)
+        project(2, 0, 1)
+        finish(2, 0, 1, "V")
+        quantise_tokens(3, 0)
+        gate_tokens(3, 0, 1)
+        gate_tokens(3, 1, 1)
+        project(2, 1, 1)
+        finish(2, 1, 1, "V")
+        quantise_tokens(3, 1)
+        project(3, 0, 0)
+        finish(3, 0, 0, "V")
+        project(3, 0, 1)
+        finish(3, 0, 1, "V")
+        project(3, 1, 0)
+        finish(3, 1, 0, "V")
+        project(3, 1, 1)
+        finish(3, 1, 1, "V")

@@ -20,11 +20,11 @@ FLOPS = 2 * 2 * TOKENS * D * D
 BLOCKS = 4
 TB = TOKENS // BLOCKS
 J = TB // P
+PAIRS = 4
 HALF = 512
 WORDS = HALF // 2
-SORT_BUFS = 4
+SORTED_BUFS = 4
 KIN_BUFS = 9
-RESULT_BUFS = 16
 
 
 def tile_aft_full_pb_kernel(tc, x_bytes, x_scale, wq_w, wq_b, r_aft, out_w, out_b, out):
@@ -33,17 +33,17 @@ def tile_aft_full_pb_kernel(tc, x_bytes, x_scale, wq_w, wq_b, r_aft, out_w, out_
     r_hbm = r_aft[0, :, :].rearrange("(b p j) k -> b p j k", b=BLOCKS, p=P)
     out_hbm = out[0, :, :].rearrange("(b p j) n -> b p j n", b=BLOCKS, p=P)
     wq_hbm = wq_w.rearrange("(f m h s) k -> f h m s k", f=2, m=P, h=2)
-    ow_hbm = out_w.rearrange("(i s m) k -> i m s k", i=4, m=P)
+    ow_hbm = out_w.rearrange("(i s m) k -> i m s k", i=PAIRS, m=P)
 
     with ExitStack() as ctx:
         keep = ctx.enter_context(tc.tile_pool(name="keep", bufs=1))
-        flow = ctx.enter_context(tc.tile_pool(name="flow", bufs=4))
+        flow = ctx.enter_context(tc.tile_pool(name="flow", bufs=1))
         banks = ctx.enter_context(tc.psum_pool(name="banks", bufs=6))
         gate_banks = ctx.enter_context(tc.psum_pool(name="gate_banks", bufs=2))
         ctx.enter_context(tc.manual_schedule())
 
         x_mult = keep.tile([P, 2, 4], F32)
-        x_mult_rows = [keep.tile([P, HALF], F32, name="x_mult_rows%d" % g) for g in range(2)]
+        x_mult_rows = keep.tile([P, D], F32)
         query_bias = keep.tile([P, 2, 4], BF16)
         out_bias = keep.tile([P, D], BF16)
         identity = keep.tile([P, P], F32)
@@ -55,12 +55,12 @@ def tile_aft_full_pb_kernel(tc, x_bytes, x_scale, wq_w, wq_b, r_aft, out_w, out_
         x_raw = kept("x_raw", BLOCKS, [P, J, D], U8)
         r_raw = kept("r_raw", BLOCKS, [P, J, D], BF16)
         wq_first = kept("wq_first", 2, [P, D], BF16)
-        wq_raw = [None] + kept("wq_raw", 3, [P, 2, D], BF16)
-        ow_raw = kept("ow_raw", 4, [P, 2, D], BF16)
+        wq_rest = kept("wq_rest", PAIRS - 1, [P, 2, D], BF16)
+        ow_raw = kept("ow_raw", PAIRS, [P, 2, D], BF16)
         x_codes = kept("x_codes", BLOCKS, [P, 2, TB], U32)
         x_scales = kept("x_scales", BLOCKS, [P, 2, TB], U8)
-        wq_codes = kept("wq_codes", 4, [P, 2, 2, P], U32)
-        wq_scales = kept("wq_scales", 4, [P, 2, 2, P], U8)
+        wq_codes = kept("wq_codes", PAIRS, [P, 2, 2, P], U32)
+        wq_scales = kept("wq_scales", PAIRS, [P, 2, 2, P], U8)
         ow_codes = kept("ow_codes", 2, [P, 2, HALF], U32)
         ow_scales = kept("ow_scales", 2, [P, 2, HALF], U8)
         y_codes = kept("y_codes", BLOCKS, [P, 2, TB], U32)
@@ -68,107 +68,95 @@ def tile_aft_full_pb_kernel(tc, x_bytes, x_scale, wq_w, wq_b, r_aft, out_w, out_
         gate_sig = kept("gate_sig", 2 * BLOCKS, [P, 4, TB], F32)
         held = {}
 
+        def load_x(b):
+            nc.sync.dma_start(out=x_raw[b][:], in_=x_hbm[b])
+
+        def load_r(b):
+            nc.sync.dma_start(out=r_raw[b][:], in_=r_hbm[b])
+
+        def load_wq_first(s):
+            nc.sync.dma_start(out=wq_first[s][:], in_=wq_hbm[0][0][:, s, :])
+
+        def load_wq(i):
+            nc.sync.dma_start(out=wq_rest[i - 1][:], in_=wq_hbm[i // 2][i % 2])
+
+        def load_ow(i):
+            nc.sync.dma_start(out=ow_raw[i][:], in_=ow_hbm[i])
+
+        def flat(tile):
+            return tile[:].rearrange("p a c -> p (a c)")
+
         def quantise(codes, scales, values):
             nc.vector.quantize_mx(out=codes.bitcast(FP8X4), scales=scales, in_=values)
 
-        def strided(words, g, u):
-            return words[:, WORDS * g + u : WORDS * (g + 1) : 2]
-
-        def presorted(words, g, u):
-            return words[:, WORDS * g + P * u : WORDS * g + P * (u + 1)]
-
-        def sort_rows(key, row, engine):
-            ordered = flow.tile([P, HALF], F32, name="ordered", align_bytes=64, bufs=SORT_BUFS)
-            held["sorted", key] = ordered
-            dst = ordered[:].rearrange("p (g u m) -> p g u m", g=2, u=2)
-            src = row.bitcast(F32).rearrange("p (g m u) -> p g u m", g=2, u=2)
-            if engine == "S":
-                nc.scalar.copy(out=dst, in_=src)
-            else:
-                nc.vector.tensor_copy(out=dst, in_=src)
-
-        def picker(key, row):
-            if ("sorted", key) in held:
-                words = held["sorted", key][:]
-                return lambda g, u: presorted(words, g, u)
-            words = row.bitcast(F32)
-            return lambda g, u: strided(words, g, u)
-
-        def turn_rows(pick, kin_words):
-            rows = banks.tile([P, 2, P // 2, 2, 2], F32, name="bank")
-            for g in range(2):
-                for u in range(2):
-                    nc.tensor.transpose(rows[:, g, :, u, :], pick(g, u), identity[:])
-            nc.scalar.copy(out=kin_words.rearrange("p g (c i u) -> p g c u i", i=2, u=2), in_=rows[:])
-
-        def spread_scale(g):
-            spread = banks.tile([P, 4, P], F32, name="bank")
-            for t in range(4):
-                nc.tensor.transpose(spread[:, t, :], x_mult[:, g, t : t + 1].to_broadcast([P, P]), identity[:])
-            nc.scalar.copy(out=x_mult_rows[g][:].rearrange("p (m t) -> p m t", t=4), in_=spread[:].rearrange("p t m -> p m t"))
-
-        def scale_x(b, j):
-            wide = flow.tile([P, D], BF16, name="x_wide", align_bytes=64, bufs=8)
-            held["x_wide", b, j] = wide
-            for g in range(2):
-                half = slice(HALF * g, HALF * (g + 1))
-                nc.vector.tensor_tensor(
-                    out=wide[:, half], in0=x_raw[b][:, j, half].bitcast(FP8), in1=x_mult_rows[g][:], op=MULT
+        def sort_words(name, raw, i, copy):
+            for s in range(2):
+                ordered = flow.tile([P, HALF], F32, name="ordered", align_bytes=64, bufs=SORTED_BUFS)
+                held["sorted", name, i, s] = ordered
+                copy(
+                    out=ordered[:].rearrange("p (g u c e) -> p g c u e", g=2, u=2, e=2),
+                    in_=raw[i][:, s, :].bitcast(F32).rearrange("p (g c e u) -> p g c u e", g=2, u=2, e=2),
                 )
 
-        def widen(b, j, engine):
-            wide = flow.tile([P, D], BF16, name="x_wide", align_bytes=64, bufs=8)
-            held["x_wide", b, j] = wide
-            codes = x_raw[b][:, j, :].bitcast(FP8)
-            if engine == "V":
-                nc.vector.tensor_copy(out=wide[:], in_=codes)
-            elif engine == "S":
-                nc.scalar.copy(out=wide[:], in_=codes)
-            else:
-                nc.gpsimd.tensor_copy(out=wide[:], in_=codes)
-
-        def turn_wide(b, g):
-            turned = banks.tile([P, TB // 2, 2, 2], F32, name="bank")
-            held["turned", b, g] = turned
-            for j in range(J):
-                pick = picker(("x", b, j), held["x_wide", b, j][:])
-                for u in range(2):
-                    nc.tensor.transpose(turned[:, 64 * j : 64 * (j + 1), u, :], pick(g, u), identity[:])
-
-        def scale_turned(b, g):
-            kin = kin_tile(("x", b))
-            scale = x_mult[:, g, :].unsqueeze(1).unsqueeze(3).to_broadcast([P, TB // 2, 4, 2])
-            nc.vector.tensor_tensor(
-                out=kin[:, g, :].rearrange("p (c i u e) -> p c u e i", i=2, u=2, e=2),
-                in0=held["turned", b, g][:].bitcast(BF16).rearrange("p c u (i e) -> p c u e i", e=2),
-                in1=scale.rearrange("p c (u e) i -> p c u e i", u=2),
-                op=MULT,
-            )
+        def words_of(key, rows, g, u):
+            if ("sorted",) + key in held:
+                return held[("sorted",) + key][:, WORDS * g + P * u : WORDS * g + P * (u + 1)]
+            return rows.bitcast(F32)[:, WORDS * g + u : WORDS * (g + 1) : 2]
 
         def kin_tile(key):
             if key not in held:
                 held[key] = flow.tile([P, 2, 4 * TB], BF16, name="kin", align_bytes=64, bufs=KIN_BUFS)
             return held[key]
 
+        def turn_rows(key, rows, kin_words):
+            turned = banks.tile([P, 2, P // 2, 2, 2], F32, name="bank")
+            for g in range(2):
+                for u in range(2):
+                    nc.tensor.transpose(turned[:, g, :, u, :], words_of(key, rows, g, u), identity[:])
+            nc.scalar.copy(out=kin_words.rearrange("p g (c i u) -> p g c u i", i=2, u=2), in_=turned[:])
+
+        def spread_scale(g):
+            spread = gate_banks.tile([P, 4, P], F32, name="turned")
+            for t in range(4):
+                nc.tensor.transpose(spread[:, t, :], x_mult[:, g, t : t + 1].to_broadcast([P, P]), identity[:])
+            nc.scalar.copy(
+                out=x_mult_rows[:, HALF * g : HALF * (g + 1)].rearrange("p (m t) -> p m t", t=4),
+                in_=spread[:].rearrange("p t m -> p m t"),
+            )
+
+        def scale_x(b, j, width=D):
+            wide = flow.tile([P, D], BF16, name="x_wide", align_bytes=64, bufs=BLOCKS * J)
+            held["x_wide", b, j] = wide
+            for first in range(0, D, width):
+                part = slice(first, first + width)
+                nc.vector.tensor_tensor(
+                    out=wide[:, part], in0=x_raw[b][:, j, part].bitcast(FP8), in1=x_mult_rows[:, part], op=MULT
+                )
+
         def turn_x(b, j):
-            kin = kin_tile(("x", b))
-            turn_rows(picker(("x", b, j), held["x_wide", b, j][:]), kin[:].bitcast(F32)[:, :, WORDS * j : WORDS * (j + 1)])
+            kin_words = kin_tile(("x", b))[:].bitcast(F32)
+            turn_rows(("x", b, j), held["x_wide", b, j][:], kin_words[:, :, WORDS * j : WORDS * (j + 1)])
 
         def quantise_x(b):
-            quantise(x_codes[b][:].rearrange("p g c -> p (g c)"), x_scales[b][:].rearrange("p g c -> p (g c)"),
-                     held["x", b][:].rearrange("p g c -> p (g c)"))
+            quantise(flat(x_codes[b]), flat(x_scales[b]), flat(held["x", b]))
 
-        def turn_wq(i, s):
-            kin = kin_tile(("wq", i))
-            turn_rows(picker(("wq", i, s), wq_raw[i][:, s, :] if i else wq_first[s][:]), kin[:].bitcast(F32)[:, s, :].rearrange("p (g w) -> p g w", g=2))
+        def turn_wq(i):
+            for s in range(2):
+                kin_words = kin_tile(("wq", i))[:].bitcast(F32)
+                rows = wq_rest[i - 1][:, s, :] if i else wq_first[s][:]
+                turn_rows(("wq", i, s), rows, kin_words[:, s, :].rearrange("p (g w) -> p g w", g=2))
 
         def quantise_wq(i):
-            quantise(wq_codes[i][:].rearrange("p s g m -> p (s g m)"), wq_scales[i][:].rearrange("p s g m -> p (s g m)"),
-                     held["wq", i][:].rearrange("p s c -> p (s c)"))
+            quantise(
+                wq_codes[i][:].rearrange("p s g m -> p (s g m)"),
+                wq_scales[i][:].rearrange("p s g m -> p (s g m)"),
+                flat(held["wq", i]),
+            )
 
-        def turn_ow(i, s):
-            kin = kin_tile(("ow", i))
-            turn_rows(picker(("ow", i, s), ow_raw[i][:, s, :]), kin[:].bitcast(F32)[:, :, WORDS * s : WORDS * (s + 1)])
+        def turn_ow(i):
+            for s in range(2):
+                kin_words = kin_tile(("ow", i))[:].bitcast(F32)
+                turn_rows(("ow", i, s), ow_raw[i][:, s, :], kin_words[:, :, WORDS * s : WORDS * (s + 1)])
 
         def quantise_ow(i):
             columns = slice(TB * (i % 2), TB * (i % 2 + 1))
@@ -179,9 +167,9 @@ def tile_aft_full_pb_kernel(tc, x_bytes, x_scale, wq_w, wq_b, r_aft, out_w, out_
             turned = gate_banks.tile([P, TB // 2, 2, 2], F32, name="turned")
             held["r", b, f] = turned
             for j in range(J):
-                pick = picker(("r", b, j), r_raw[b][:, j, :])
+                pairs = slice(j * P // 2, (j + 1) * P // 2)
                 for u in range(2):
-                    nc.tensor.transpose(turned[:, 64 * j : 64 * (j + 1), u, :], pick(f, u), identity[:])
+                    nc.tensor.transpose(turned[:, pairs, u, :], words_of(("r", b, j), r_raw[b][:, j, :], f, u), identity[:])
 
         def query(b, i):
             f, h = i // 2, i % 2
@@ -203,46 +191,44 @@ def tile_aft_full_pb_kernel(tc, x_bytes, x_scale, wq_w, wq_b, r_aft, out_w, out_
                     out=gate_sig[2 * b + f][:, t, :], in_=q[:, s, :], func=SIGMOID, bias=query_bias[:, f, t : t + 1]
                 )
 
+        def query_block(b):
+            for i in range(PAIRS):
+                query(b, i)
+
         def gate(b, f):
-            kin = kin_tile(("y", b))
             nc.vector.tensor_tensor(
-                out=kin[:, f, :].rearrange("p (c i u e) -> p c u e i", i=2, u=2, e=2),
+                out=kin_tile(("y", b))[:, f, :].rearrange("p (c i u e) -> p c u e i", i=2, u=2, e=2),
                 in0=held["r", b, f][:].bitcast(BF16).rearrange("p c u (i e) -> p c u e i", e=2),
                 in1=gate_sig[2 * b + f][:].rearrange("p (u e) (c i) -> p c u e i", u=2, i=2),
                 op=MULT,
             )
 
         def gate_tokens(b, f, j):
-            kin = kin_tile(("y", b))
+            pairs = slice(j * P // 2, (j + 1) * P // 2)
             nc.vector.tensor_tensor(
-                out=kin[:, j, HALF * f : HALF * (f + 1)].rearrange("p (c i u e) -> p c u e i", i=2, u=2, e=2),
-                in0=held["r", b, f][:, 64 * j : 64 * (j + 1)].bitcast(BF16).rearrange("p c u (i e) -> p c u e i", e=2),
+                out=kin_tile(("y", b))[:, j, HALF * f : HALF * (f + 1)].rearrange("p (c i u e) -> p c u e i", i=2, u=2, e=2),
+                in0=held["r", b, f][:, pairs].bitcast(BF16).rearrange("p c u (i e) -> p c u e i", e=2),
                 in1=gate_sig[2 * b + f][:, :, P * j : P * (j + 1)].rearrange("p (u e) (c i) -> p c u e i", u=2, i=2),
                 op=MULT,
             )
 
         def quantise_tokens(b, j):
-            held["by tokens", b] = True
             quantise(y_codes[b][:, j, :], y_scales[b][:, j, :], held["y", b][:, j, :])
 
-        def quantise_block(b):
-            quantise(y_codes[b][:].rearrange("p f c -> p (f c)"), y_scales[b][:].rearrange("p f c -> p (f c)"),
-                     held["y", b][:].rearrange("p f c -> p (f c)"))
-
-        def quantise_y(b, f):
-            quantise(y_codes[b][:, f, :], y_scales[b][:, f, :], held["y", b][:, f, :])
-
         def y_part(tiles, b, j, g):
-            if ("by tokens", b) in held:
+            if b == BLOCKS - 1:
                 return tiles[b][:, j, g * P : (g + 1) * P]
             return tiles[b][:, g, j * P : (j + 1) * P]
 
-        def project(b, j, c):
-            rows = banks.tile([P, HALF], F32, name="bank")
-            held["out", b, j, c] = rows
+        def quantise_y(b):
+            quantise(flat(y_codes[b]), flat(y_scales[b]), flat(held["y", b]))
+
+        def project(n):
+            b, c, j = n // 4, n // 2 % 2, n % 2
+            held["sums", n] = banks.tile([P, HALF], F32, name="bank")
             for g in range(2):
                 nc.tensor.matmul_mx(
-                    out=rows[:],
+                    out=held["sums", n][:],
                     lhsT=y_part(y_codes, b, j, g).bitcast(FP8X4),
                     lhsT_scale=y_part(y_scales, b, j, g),
                     rhs=ow_codes[c][:, g, :].bitcast(FP8X4),
@@ -251,40 +237,36 @@ def tile_aft_full_pb_kernel(tc, x_bytes, x_scale, wq_w, wq_b, r_aft, out_w, out_
                     stop=(g == 1),
                 )
 
-        def finish(b, j, c, engine):
-            columns = slice(HALF * c, HALF * (c + 1))
-            result = flow.tile([P, HALF], F32, name="result", align_bytes=64, bufs=RESULT_BUFS)
-            held["result", b, j, c] = result
-            if engine == "V":
-                nc.vector.tensor_tensor(out=result[:], in0=held["out", b, j, c][:], in1=out_bias[:, columns], op=ADD)
-                store(b, j, c)
-            else:
-                nc.scalar.copy(out=result[:], in_=held["out", b, j, c][:])
-                nc.gpsimd.tensor_tensor(out=result[:], in0=result[:], in1=out_bias[:, columns], op=ADD)
+        def result_and_bias(n):
+            c = n // 2 % 2
+            held["result", n] = flow.tile([P, HALF], F32, name="result", align_bytes=64, bufs=4 * BLOCKS)
+            return held["result", n][:], out_bias[:, HALF * c : HALF * (c + 1)]
 
-        def store(b, j, c):
-            nc.sync.dma_start(out=out_hbm[b][:, j, HALF * c : HALF * (c + 1)], in_=held["result", b, j, c][:])
+        def store(n):
+            b, c, j = n // 4, n // 2 % 2, n % 2
+            nc.sync.dma_start(out=out_hbm[b][:, j, HALF * c : HALF * (c + 1)], in_=held["result", n][:])
 
-        def load_x(b):
-            nc.sync.dma_start(out=x_raw[b][:], in_=x_hbm[b])
+        def finish(n):
+            result, bias = result_and_bias(n)
+            nc.vector.tensor_tensor(out=result, in0=held["sums", n][:], in1=bias, op=ADD)
+            store(n)
 
-        def load_r(b):
-            nc.sync.dma_start(out=r_raw[b][:], in_=r_hbm[b])
+        def bias_beside_vector(n):
+            result, bias = result_and_bias(n)
+            nc.scalar.copy(out=result, in_=held["sums", n][:])
+            nc.gpsimd.tensor_tensor(out=result, in0=result, in1=bias, op=ADD)
 
-        def load_wq(i):
-            nc.sync.dma_start(out=wq_raw[i][:], in_=wq_hbm[i // 2][i % 2])
-
-        def load_wq_first(s):
-            nc.sync.dma_start(out=wq_first[s][:], in_=wq_hbm[0][0][:, s, :])
-
-        def load_ow(i):
-            nc.sync.dma_start(out=ow_raw[i][:], in_=ow_hbm[i])
+        def project_and_finish(*tiles):
+            for n in tiles:
+                project(n)
+                finish(n)
 
         nc.sync.dma_start(out=x_mult[:], in_=x_scale[0, :, :].rearrange("o (g p t) -> p (o g) t", p=P, t=4))
         nc.scalar.dma_start(out=query_bias[:], in_=wq_b.rearrange("(f p t) -> p f t", p=P, t=4))
         nc.gpsimd.memset(one_column[:], 0.0)
         make_identity(nc, identity[:])
         nc.scalar.activation(out=one_column[:], in_=one_column[:], func=SIGMOID)
+
         load_wq_first(0)
         load_x(0)
         load_wq_first(1)
@@ -292,10 +274,10 @@ def tile_aft_full_pb_kernel(tc, x_bytes, x_scale, wq_w, wq_b, r_aft, out_w, out_
         load_x(1)
         load_wq(2)
         load_wq(3)
-        load_ow(0)
         load_x(2)
-        load_ow(1)
+        load_ow(0)
         load_x(3)
+        load_ow(1)
         load_r(0)
         load_r(1)
         load_ow(2)
@@ -303,43 +285,41 @@ def tile_aft_full_pb_kernel(tc, x_bytes, x_scale, wq_w, wq_b, r_aft, out_w, out_
         nc.sync.dma_start(out=out_bias[:], in_=out_b.partition_broadcast(P))
         load_r(2)
         load_r(3)
+
         spread_scale(0)
         spread_scale(1)
-        scale_x(0, 0)
+        scale_x(0, 0, HALF)
         scale_x(0, 1)
-        turn_wq(0, 0)
-        turn_wq(0, 1)
+        turn_wq(0)
         turn_x(0, 0)
         scale_x(1, 0)
         scale_x(1, 1)
-        turn_wq(1, 0)
-        turn_wq(1, 1)
+        turn_wq(1)
         turn_x(0, 1)
         quantise_wq(0)
-        turn_wq(2, 0)
-        turn_wq(2, 1)
+        turn_wq(2)
         quantise_x(0)
         scale_x(2, 0)
-        turn_wq(3, 0)
-        turn_wq(3, 1)
+        turn_wq(3)
         quantise_wq(1)
         scale_x(2, 1)
         turn_x(1, 0)
         turn_x(1, 1)
         quantise_wq(2)
         scale_x(3, 0)
+
         query(0, 0)
-        turn_ow(0, 0)
-        turn_ow(0, 1)
+        turn_ow(0)
         turn_x(2, 0)
         quantise_wq(3)
         scale_x(3, 1)
+
         query(0, 1)
         turn_x(2, 1)
-        turn_ow(1, 0)
-        turn_ow(1, 1)
+        turn_ow(1)
         quantise_x(1)
         quantise_ow(0)
+
         query(0, 2)
         turn_r(0, 0)
         turn_x(3, 0)
@@ -347,82 +327,54 @@ def tile_aft_full_pb_kernel(tc, x_bytes, x_scale, wq_w, wq_b, r_aft, out_w, out_
         quantise_x(2)
         gate(0, 0)
         quantise_ow(1)
+
         query(0, 3)
-        turn_ow(2, 0)
-        turn_ow(2, 1)
+        turn_ow(2)
         turn_r(0, 1)
-        quantise_x(3)
-        sort_rows(("r", 1, 0), r_raw[1][:, 0, :], "V")
-        sort_rows(("r", 1, 1), r_raw[1][:, 1, :], "V")
+        sort_words("r", r_raw, 1, nc.vector.tensor_copy)
         gate(0, 1)
-        query(1, 0)
-        query(1, 1)
-        query(1, 2)
-        query(1, 3)
+
+        query_block(1)
         quantise_ow(2)
-        quantise_block(0)
+        quantise_y(0)
+
         turn_r(1, 0)
         turn_r(1, 1)
-        turn_ow(3, 0)
-        turn_ow(3, 1)
+        turn_ow(3)
         gate(1, 0)
         gate(1, 1)
-        project(0, 0, 0)
-        project(0, 1, 0)
-        sort_rows(("r", 2, 0), r_raw[2][:, 0, :], "S")
-        sort_rows(("r", 2, 1), r_raw[2][:, 1, :], "S")
-        query(2, 0)
-        query(2, 1)
-        query(2, 2)
-        query(2, 3)
-        finish(0, 0, 0, "V")
-        finish(0, 1, 0, "V")
+        project(0)
+        project(1)
+        sort_words("r", r_raw, 2, nc.scalar.copy)
+        query_block(2)
+        finish(0)
+        finish(1)
         quantise_ow(3)
-        quantise_block(1)
-        sort_rows(("r", 3, 0), r_raw[3][:, 0, :], "S")
-        sort_rows(("r", 3, 1), r_raw[3][:, 1, :], "S")
-        project(0, 0, 1)
-        finish(0, 0, 1, "V")
-        project(0, 1, 1)
-        finish(0, 1, 1, "V")
-        project(1, 0, 0)
-        finish(1, 0, 0, "V")
-        project(1, 1, 0)
-        finish(1, 1, 0, "V")
+        quantise_y(1)
+        quantise_x(3)
+        project(2)
+        bias_beside_vector(2)
+        sort_words("r", r_raw, 3, nc.scalar.copy)
+        project_and_finish(3, 4)
+        store(2)
+        project_and_finish(5)
+
         turn_r(2, 0)
         turn_r(2, 1)
         gate(2, 0)
         gate(2, 1)
-        query(3, 0)
-        query(3, 1)
-        query(3, 2)
-        query(3, 3)
-        quantise_block(2)
-        project(1, 0, 1)
-        finish(1, 0, 1, "V")
-        project(1, 1, 1)
-        finish(1, 1, 1, "V")
-        project(2, 0, 0)
-        finish(2, 0, 0, "V")
-        project(2, 1, 0)
-        finish(2, 1, 0, "V")
+        query_block(3)
+        quantise_y(2)
+        project(6)
+        bias_beside_vector(6)
+        project_and_finish(7, 8, 9)
+        store(6)
+
         turn_r(3, 0)
         turn_r(3, 1)
-        gate_tokens(3, 0, 0)
-        gate_tokens(3, 1, 0)
-        project(2, 0, 1)
-        finish(2, 0, 1, "V")
-        quantise_tokens(3, 0)
-        gate_tokens(3, 0, 1)
-        gate_tokens(3, 1, 1)
-        project(2, 1, 1)
-        finish(2, 1, 1, "V")
-        quantise_tokens(3, 1)
-        project(3, 0, 0)
-        finish(3, 0, 0, "V")
-        project(3, 0, 1)
-        finish(3, 0, 1, "V")
-        project(3, 1, 0)
-        finish(3, 1, 0, "V")
-        project(3, 1, 1)
-        finish(3, 1, 1, "V")
+        for j in range(J):
+            gate_tokens(3, 0, j)
+            gate_tokens(3, 1, j)
+            project_and_finish(10 + j)
+            quantise_tokens(3, j)
+        project_and_finish(12, 14, 13, 15)

@@ -23,7 +23,8 @@ J = TB // P
 PAIRS = 4
 HALF = 512
 WORDS = HALF // 2
-SORTED_BUFS = 4
+SORTED_BUFS = 7
+RESULT_BUFS = 13
 KIN_BUFS = 9
 
 
@@ -65,7 +66,8 @@ def tile_aft_full_pb_kernel(tc, x_bytes, x_scale, wq_w, wq_b, r_aft, out_w, out_
         ow_scales = kept("ow_scales", 2, [P, 2, HALF], U8)
         y_codes = kept("y_codes", BLOCKS, [P, 2, TB], U32)
         y_scales = kept("y_scales", BLOCKS, [P, 2, TB], U8)
-        gate_sig = kept("gate_sig", 2 * BLOCKS, [P, 4, TB], F32)
+        gate_sig = kept("gate_sig", 2 * (BLOCKS - 1), [P, 4, TB], F32)
+        last_sig = kept("last_sig", 2 * J, [P, 4, P], F32)
         held = {}
 
         def load_x(b):
@@ -83,20 +85,26 @@ def tile_aft_full_pb_kernel(tc, x_bytes, x_scale, wq_w, wq_b, r_aft, out_w, out_
         def load_ow(i):
             nc.sync.dma_start(out=ow_raw[i][:], in_=ow_hbm[i])
 
+        def load_out_bias():
+            nc.sync.dma_start(out=out_bias[:], in_=out_b.partition_broadcast(P))
+
+        def load_query_bias():
+            nc.sync.dma_start(out=query_bias[:], in_=wq_b.rearrange("(f p t) -> p f t", p=P, t=4))
+
         def flat(tile):
             return tile[:].rearrange("p a c -> p (a c)")
 
         def quantise(codes, scales, values):
             nc.vector.quantize_mx(out=codes.bitcast(FP8X4), scales=scales, in_=values)
 
-        def sort_words(name, raw, i, copy):
-            for s in range(2):
-                ordered = flow.tile([P, HALF], F32, name="ordered", align_bytes=64, bufs=SORTED_BUFS)
-                held["sorted", name, i, s] = ordered
-                copy(
-                    out=ordered[:].rearrange("p (g u c e) -> p g c u e", g=2, u=2, e=2),
-                    in_=raw[i][:, s, :].bitcast(F32).rearrange("p (g c e u) -> p g c u e", g=2, u=2, e=2),
-                )
+        def sort_words(name, i, s, copy):
+            ordered = flow.tile([P, HALF], F32, name="ordered", align_bytes=64, bufs=SORTED_BUFS)
+            held["sorted", name, i, s] = ordered
+            rows = r_raw[i][:, s, :] if name == "r" else rows_of(name, i, s)
+            copy(
+                out=ordered[:].rearrange("p (g u c e) -> p g c u e", g=2, u=2, e=2),
+                in_=rows.bitcast(F32).rearrange("p (g c e u) -> p g c u e", g=2, u=2, e=2),
+            )
 
         def words_of(key, rows, g, u):
             if ("sorted",) + key in held:
@@ -108,12 +116,27 @@ def tile_aft_full_pb_kernel(tc, x_bytes, x_scale, wq_w, wq_b, r_aft, out_w, out_
                 held[key] = flow.tile([P, 2, 4 * TB], BF16, name="kin", align_bytes=64, bufs=KIN_BUFS)
             return held[key]
 
-        def turn_rows(key, rows, kin_words):
+        def rows_of(name, i, s):
+            if name == "x":
+                return held["x_wide", i, s][:]
+            if name == "wq":
+                return wq_rest[i - 1][:, s, :] if i else wq_first[s][:]
+            return ow_raw[i][:, s, :]
+
+        def turn(name, i, s):
             turned = banks.tile([P, 2, P // 2, 2, 2], F32, name="bank")
+            held["turned", name, i, s] = turned
             for g in range(2):
                 for u in range(2):
-                    nc.tensor.transpose(turned[:, g, :, u, :], words_of(key, rows, g, u), identity[:])
-            nc.scalar.copy(out=kin_words.rearrange("p g (c i u) -> p g c u i", i=2, u=2), in_=turned[:])
+                    nc.tensor.transpose(turned[:, g, :, u, :], words_of((name, i, s), rows_of(name, i, s), g, u), identity[:])
+
+        def empty(name, i, s, copy=nc.scalar.copy):
+            kin_words = kin_tile((name, i))[:].bitcast(F32)
+            if name == "wq":
+                kin_words = kin_words[:, s, :].rearrange("p (g w) -> p g w", g=2)
+            else:
+                kin_words = kin_words[:, :, WORDS * s : WORDS * (s + 1)]
+            copy(out=kin_words.rearrange("p g (c i u) -> p g c u i", i=2, u=2), in_=held["turned", name, i, s][:])
 
         def spread_scale(g):
             spread = gate_banks.tile([P, 4, P], F32, name="turned")
@@ -133,18 +156,8 @@ def tile_aft_full_pb_kernel(tc, x_bytes, x_scale, wq_w, wq_b, r_aft, out_w, out_
                     out=wide[:, part], in0=x_raw[b][:, j, part].bitcast(FP8), in1=x_mult_rows[:, part], op=MULT
                 )
 
-        def turn_x(b, j):
-            kin_words = kin_tile(("x", b))[:].bitcast(F32)
-            turn_rows(("x", b, j), held["x_wide", b, j][:], kin_words[:, :, WORDS * j : WORDS * (j + 1)])
-
         def quantise_x(b):
             quantise(flat(x_codes[b]), flat(x_scales[b]), flat(held["x", b]))
-
-        def turn_wq(i):
-            for s in range(2):
-                kin_words = kin_tile(("wq", i))[:].bitcast(F32)
-                rows = wq_rest[i - 1][:, s, :] if i else wq_first[s][:]
-                turn_rows(("wq", i, s), rows, kin_words[:, s, :].rearrange("p (g w) -> p g w", g=2))
 
         def quantise_wq(i):
             quantise(
@@ -152,11 +165,6 @@ def tile_aft_full_pb_kernel(tc, x_bytes, x_scale, wq_w, wq_b, r_aft, out_w, out_
                 wq_scales[i][:].rearrange("p s g m -> p (s g m)"),
                 flat(held["wq", i]),
             )
-
-        def turn_ow(i):
-            for s in range(2):
-                kin_words = kin_tile(("ow", i))[:].bitcast(F32)
-                turn_rows(("ow", i, s), ow_raw[i][:, s, :], kin_words[:, :, WORDS * s : WORDS * (s + 1)])
 
         def quantise_ow(i):
             columns = slice(TB * (i % 2), TB * (i % 2 + 1))
@@ -172,8 +180,8 @@ def tile_aft_full_pb_kernel(tc, x_bytes, x_scale, wq_w, wq_b, r_aft, out_w, out_
                     nc.tensor.transpose(turned[:, pairs, u, :], words_of(("r", b, j), r_raw[b][:, j, :], f, u), identity[:])
 
         def query(b, i):
-            f, h = i // 2, i % 2
             q = banks.tile([P, 2, TB], F32, name="bank")
+            held["q", b, i] = q
             for s in range(2):
                 for g in range(2):
                     nc.tensor.matmul_mx(
@@ -185,15 +193,42 @@ def tile_aft_full_pb_kernel(tc, x_bytes, x_scale, wq_w, wq_b, r_aft, out_w, out_
                         start=(g == 0),
                         stop=(g == 1),
                     )
+
+        def sigmoid(b, i):
+            f, h = i // 2, i % 2
             for s in range(2):
                 t = 2 * h + s
                 nc.scalar.activation(
-                    out=gate_sig[2 * b + f][:, t, :], in_=q[:, s, :], func=SIGMOID, bias=query_bias[:, f, t : t + 1]
+                    out=gate_sig[2 * b + f][:, t, :], in_=held["q", b, i][:, s, :], func=SIGMOID, bias=query_bias[:, f, t : t + 1]
+                )
+
+        def query_tokens(j, i):
+            q = banks.tile([P, 2, P], F32, name="bank")
+            held["q", "last", j, i] = q
+            for s in range(2):
+                for g in range(2):
+                    nc.tensor.matmul_mx(
+                        out=q[:, s, :],
+                        lhsT=wq_codes[i][:, s, g, :].bitcast(FP8X4),
+                        lhsT_scale=wq_scales[i][:, s, g, :],
+                        rhs=x_codes[BLOCKS - 1][:, g, P * j : P * (j + 1)].bitcast(FP8X4),
+                        rhs_scale=x_scales[BLOCKS - 1][:, g, P * j : P * (j + 1)],
+                        start=(g == 0),
+                        stop=(g == 1),
+                    )
+
+        def sigmoid_tokens(j, i):
+            f, h = i // 2, i % 2
+            for s in range(2):
+                t = 2 * h + s
+                nc.scalar.activation(
+                    out=last_sig[2 * j + f][:, t, :], in_=held["q", "last", j, i][:, s, :], func=SIGMOID, bias=query_bias[:, f, t : t + 1]
                 )
 
         def query_block(b):
             for i in range(PAIRS):
                 query(b, i)
+                sigmoid(b, i)
 
         def gate(b, f):
             nc.vector.tensor_tensor(
@@ -208,7 +243,7 @@ def tile_aft_full_pb_kernel(tc, x_bytes, x_scale, wq_w, wq_b, r_aft, out_w, out_
             nc.vector.tensor_tensor(
                 out=kin_tile(("y", b))[:, j, HALF * f : HALF * (f + 1)].rearrange("p (c i u e) -> p c u e i", i=2, u=2, e=2),
                 in0=held["r", b, f][:, pairs].bitcast(BF16).rearrange("p c u (i e) -> p c u e i", e=2),
-                in1=gate_sig[2 * b + f][:, :, P * j : P * (j + 1)].rearrange("p (u e) (c i) -> p c u e i", u=2, i=2),
+                in1=last_sig[2 * j + f][:].rearrange("p (u e) (c i) -> p c u e i", u=2, i=2),
                 op=MULT,
             )
 
@@ -239,7 +274,7 @@ def tile_aft_full_pb_kernel(tc, x_bytes, x_scale, wq_w, wq_b, r_aft, out_w, out_
 
         def result_and_bias(n):
             c = n // 2 % 2
-            held["result", n] = flow.tile([P, HALF], F32, name="result", align_bytes=64, bufs=4 * BLOCKS)
+            held["result", n] = flow.tile([P, HALF], F32, name="result", align_bytes=64, bufs=RESULT_BUFS)
             return held["result", n][:], out_bias[:, HALF * c : HALF * (c + 1)]
 
         def store(n):
@@ -249,7 +284,6 @@ def tile_aft_full_pb_kernel(tc, x_bytes, x_scale, wq_w, wq_b, r_aft, out_w, out_
         def finish(n):
             result, bias = result_and_bias(n)
             nc.vector.tensor_tensor(out=result, in0=held["sums", n][:], in1=bias, op=ADD)
-            store(n)
 
         def bias_beside_vector(n):
             result, bias = result_and_bias(n)
@@ -260,9 +294,9 @@ def tile_aft_full_pb_kernel(tc, x_bytes, x_scale, wq_w, wq_b, r_aft, out_w, out_
             for n in tiles:
                 project(n)
                 finish(n)
+                store(n)
 
         nc.sync.dma_start(out=x_mult[:], in_=x_scale[0, :, :].rearrange("o (g p t) -> p (o g) t", p=P, t=4))
-        nc.scalar.dma_start(out=query_bias[:], in_=wq_b.rearrange("(f p t) -> p f t", p=P, t=4))
         nc.gpsimd.memset(one_column[:], 0.0)
         make_identity(nc, identity[:])
         nc.scalar.activation(out=one_column[:], in_=one_column[:], func=SIGMOID)
@@ -274,107 +308,206 @@ def tile_aft_full_pb_kernel(tc, x_bytes, x_scale, wq_w, wq_b, r_aft, out_w, out_
         load_x(1)
         load_wq(2)
         load_wq(3)
-        load_x(2)
-        load_ow(0)
-        load_x(3)
-        load_ow(1)
         load_r(0)
-        load_r(1)
+        load_ow(0)
+        load_query_bias()
+        load_x(2)
+        load_ow(1)
+        load_x(3)
         load_ow(2)
+        load_r(1)
         load_ow(3)
-        nc.sync.dma_start(out=out_bias[:], in_=out_b.partition_broadcast(P))
         load_r(2)
         load_r(3)
-
+        load_out_bias()
         spread_scale(0)
         spread_scale(1)
         scale_x(0, 0, HALF)
         scale_x(0, 1)
-        turn_wq(0)
-        turn_x(0, 0)
+        turn("wq", 0, 0)
+        empty("wq", 0, 0)
+        turn("wq", 0, 1)
+        empty("wq", 0, 1)
+        turn("x", 0, 0)
+        empty("x", 0, 0)
         scale_x(1, 0)
         scale_x(1, 1)
-        turn_wq(1)
-        turn_x(0, 1)
+        turn("wq", 1, 0)
+        empty("wq", 1, 0)
+        turn("wq", 1, 1)
+        empty("wq", 1, 1)
+        turn("x", 0, 1)
+        empty("x", 0, 1)
         quantise_wq(0)
-        turn_wq(2)
+        turn("wq", 2, 0)
+        empty("wq", 2, 0)
+        turn("wq", 2, 1)
+        empty("wq", 2, 1)
         quantise_x(0)
-        scale_x(2, 0)
-        turn_wq(3)
+        turn("wq", 3, 0)
+        empty("wq", 3, 0)
+        turn("wq", 3, 1)
+        empty("wq", 3, 1)
         quantise_wq(1)
-        scale_x(2, 1)
-        turn_x(1, 0)
-        turn_x(1, 1)
+        sort_words("r", 0, 0, nc.vector.tensor_copy)
+        sort_words("r", 0, 1, nc.vector.tensor_copy)
+        turn("x", 1, 0)
+        empty("x", 1, 0)
+        turn("x", 1, 1)
+        empty("x", 1, 1)
         quantise_wq(2)
-        scale_x(3, 0)
-
-        query(0, 0)
-        turn_ow(0)
-        turn_x(2, 0)
+        sort_words("ow", 0, 0, nc.scalar.copy)
+        sort_words("ow", 0, 1, nc.vector.tensor_copy)
         quantise_wq(3)
-        scale_x(3, 1)
-
-        query(0, 1)
-        turn_x(2, 1)
-        turn_ow(1)
-        quantise_x(1)
-        quantise_ow(0)
-
-        query(0, 2)
+        query(0, 0)
+        sigmoid(0, 0)
         turn_r(0, 0)
-        turn_x(3, 0)
-        turn_x(3, 1)
-        quantise_x(2)
+        turn_r(0, 1)
+        turn("ow", 0, 0)
+        empty("ow", 0, 0)
+        turn("ow", 0, 1)
+        empty("ow", 0, 1)
+        turn("ow", 1, 0)
+        empty("ow", 1, 0)
+        turn("ow", 1, 1)
+        empty("ow", 1, 1)
+        quantise_x(1)
+        scale_x(2, 0)
+        scale_x(2, 1)
+        scale_x(3, 0)
+        query(0, 1)
+        sigmoid(0, 1)
+        query(0, 2)
+        sigmoid(0, 2)
+        query(0, 3)
+        sigmoid(0, 3)
+        turn("x", 2, 0)
+        empty("x", 2, 0)
+        turn("x", 2, 1)
+        empty("x", 2, 1)
+        turn("ow", 2, 0)
+        empty("ow", 2, 0)
+        turn("ow", 2, 1)
+        empty("ow", 2, 1)
+        quantise_ow(0)
+        scale_x(3, 1)
         gate(0, 0)
         quantise_ow(1)
-
-        query(0, 3)
-        turn_ow(2)
-        turn_r(0, 1)
-        sort_words("r", r_raw, 1, nc.vector.tensor_copy)
         gate(0, 1)
-
-        query_block(1)
-        quantise_ow(2)
+        sort_words("r", 1, 0, nc.vector.tensor_copy)
+        sort_words("r", 1, 1, nc.vector.tensor_copy)
+        query(1, 0)
+        sigmoid(1, 0)
+        query(1, 1)
+        sigmoid(1, 1)
+        query(1, 2)
+        sigmoid(1, 2)
+        query(1, 3)
+        sigmoid(1, 3)
         quantise_y(0)
-
+        quantise_x(2)
+        quantise_ow(2)
         turn_r(1, 0)
         turn_r(1, 1)
-        turn_ow(3)
+        turn("ow", 3, 0)
+        empty("ow", 3, 0)
+        turn("ow", 3, 1)
+        empty("ow", 3, 1)
         gate(1, 0)
         gate(1, 1)
+        sort_words("r", 2, 0, nc.scalar.copy)
+        sort_words("r", 2, 1, nc.scalar.copy)
         project(0)
         project(1)
-        sort_words("r", r_raw, 2, nc.scalar.copy)
-        query_block(2)
+        query(2, 0)
+        sigmoid(2, 0)
+        query(2, 1)
+        sigmoid(2, 1)
+        query(2, 2)
+        sigmoid(2, 2)
+        query(2, 3)
+        sigmoid(2, 3)
         finish(0)
-        finish(1)
-        quantise_ow(3)
+        store(0)
         quantise_y(1)
-        quantise_x(3)
+        quantise_ow(3)
+        finish(1)
+        store(1)
         project(2)
-        bias_beside_vector(2)
-        sort_words("r", r_raw, 3, nc.scalar.copy)
-        project_and_finish(3, 4)
+        project(3)
+        bias_beside_vector(3)
+        finish(2)
         store(2)
-        project_and_finish(5)
-
         turn_r(2, 0)
         turn_r(2, 1)
+        turn("x", 3, 0)
+        empty("x", 3, 0)
+        turn("x", 3, 1)
+        empty("x", 3, 1)
         gate(2, 0)
         gate(2, 1)
-        query_block(3)
-        quantise_y(2)
+        store(3)
+        sort_words("r", 3, 0, nc.scalar.copy)
+        sort_words("r", 3, 1, nc.scalar.copy)
+        project(4)
+        project(5)
         project(6)
         bias_beside_vector(6)
-        project_and_finish(7, 8, 9)
-        store(6)
-
+        project(7)
+        quantise_x(3)
+        finish(4)
+        store(4)
+        quantise_y(2)
+        finish(5)
+        store(5)
+        finish(7)
+        store(7)
+        query_tokens(0, 0)
+        sigmoid_tokens(0, 0)
+        query_tokens(0, 1)
+        sigmoid_tokens(0, 1)
+        query_tokens(0, 2)
+        sigmoid_tokens(0, 2)
+        query_tokens(0, 3)
+        sigmoid_tokens(0, 3)
         turn_r(3, 0)
         turn_r(3, 1)
-        for j in range(J):
-            gate_tokens(3, 0, j)
-            gate_tokens(3, 1, j)
-            project_and_finish(10 + j)
-            quantise_tokens(3, j)
-        project_and_finish(12, 14, 13, 15)
+        store(6)
+        project(8)
+        query_tokens(1, 0)
+        sigmoid_tokens(1, 0)
+        query_tokens(1, 1)
+        sigmoid_tokens(1, 1)
+        project(9)
+        query_tokens(1, 2)
+        sigmoid_tokens(1, 2)
+        query_tokens(1, 3)
+        sigmoid_tokens(1, 3)
+        gate_tokens(3, 0, 0)
+        gate_tokens(3, 1, 0)
+        finish(8)
+        store(8)
+        quantise_tokens(3, 0)
+        finish(9)
+        store(9)
+        gate_tokens(3, 0, 1)
+        project(10)
+        project(11)
+        project(12)
+        project(14)
+        gate_tokens(3, 1, 1)
+        finish(10)
+        store(10)
+        quantise_tokens(3, 1)
+        finish(11)
+        store(11)
+        finish(12)
+        store(12)
+        project(13)
+        finish(14)
+        store(14)
+        finish(13)
+        store(13)
+        project(15)
+        finish(15)
+        store(15)

@@ -23,9 +23,10 @@ J = TB // P
 PAIRS = 4
 HALF = 512
 WORDS = HALF // 2
-SORTED_BUFS = 7
+SORTED_BUFS = 4
 RESULT_BUFS = 13
-KIN_BUFS = 9
+LATE_Y = (("y", 2), ("y", 3))
+KIN_BUFS = 8
 
 
 def tile_aft_full_pb_kernel(tc, x_bytes, x_scale, wq_w, wq_b, r_aft, out_w, out_b, out):
@@ -113,7 +114,10 @@ def tile_aft_full_pb_kernel(tc, x_bytes, x_scale, wq_w, wq_b, r_aft, out_w, out_
 
         def kin_tile(key):
             if key not in held:
-                held[key] = flow.tile([P, 2, 4 * TB], BF16, name="kin", align_bytes=64, bufs=KIN_BUFS)
+                if key in LATE_Y:
+                    held[key] = flow.tile([P, 2, 4 * TB], BF16, name="y_in%d" % key[1], align_bytes=64)
+                else:
+                    held[key] = flow.tile([P, 2, 4 * TB], BF16, name="kin", align_bytes=64, bufs=KIN_BUFS)
             return held[key]
 
         def rows_of(name, i, s):
@@ -225,6 +229,23 @@ def tile_aft_full_pb_kernel(tc, x_bytes, x_scale, wq_w, wq_b, r_aft, out_w, out_
                     out=last_sig[2 * j + f][:, t, :], in_=held["q", "last", j, i][:, s, :], func=SIGMOID, bias=query_bias[:, f, t : t + 1]
                 )
 
+        def query_half(j, f):
+            q = banks.tile([P, 4, P], F32, name="bank")
+            for t in range(4):
+                i, s = 2 * f + t // 2, t % 2
+                for g in range(2):
+                    nc.tensor.matmul_mx(
+                        out=q[:, t, :],
+                        lhsT=wq_codes[i][:, s, g, :].bitcast(FP8X4),
+                        lhsT_scale=wq_scales[i][:, s, g, :],
+                        rhs=x_codes[BLOCKS - 1][:, g, P * j : P * (j + 1)].bitcast(FP8X4),
+                        rhs_scale=x_scales[BLOCKS - 1][:, g, P * j : P * (j + 1)],
+                        start=(g == 0),
+                        stop=(g == 1),
+                    )
+            for t in range(4):
+                nc.scalar.activation(out=last_sig[2 * j + f][:, t, :], in_=q[:, t, :], func=SIGMOID, bias=query_bias[:, f, t : t + 1])
+
         def query_block(b):
             for i in range(PAIRS):
                 query(b, i)
@@ -290,6 +311,14 @@ def tile_aft_full_pb_kernel(tc, x_bytes, x_scale, wq_w, wq_b, r_aft, out_w, out_
             nc.scalar.copy(out=result, in_=held["sums", n][:])
             nc.gpsimd.tensor_tensor(out=result, in0=result, in1=bias, op=ADD)
 
+        def bias_behind_quantise(n, b, place):
+            result, bias = result_and_bias(n)
+            nc.scalar.copy(out=result, in_=held["sums", n][:])
+            if ("spare", b) not in held:
+                held["spare", b] = flow.tile([P, 2, HALF], F32, name="y_in%d" % b, align_bytes=64)
+            held["result", n] = held["spare", b][:, place]
+            nc.gpsimd.tensor_tensor(out=held["result", n], in0=result, in1=bias, op=ADD)
+
         def project_and_finish(*tiles):
             for n in tiles:
                 project(n)
@@ -307,17 +336,17 @@ def tile_aft_full_pb_kernel(tc, x_bytes, x_scale, wq_w, wq_b, r_aft, out_w, out_
         load_wq(1)
         load_x(1)
         load_wq(2)
-        load_wq(3)
-        load_r(0)
-        load_ow(0)
         load_query_bias()
+        load_wq(3)
         load_x(2)
-        load_ow(1)
+        load_r(0)
         load_x(3)
-        load_ow(2)
+        load_ow(0)
+        load_ow(1)
         load_r(1)
-        load_ow(3)
+        load_ow(2)
         load_r(2)
+        load_ow(3)
         load_r(3)
         load_out_bias()
         spread_scale(0)
@@ -349,53 +378,41 @@ def tile_aft_full_pb_kernel(tc, x_bytes, x_scale, wq_w, wq_b, r_aft, out_w, out_
         turn("wq", 3, 1)
         empty("wq", 3, 1)
         quantise_wq(1)
-        sort_words("r", 0, 0, nc.vector.tensor_copy)
-        sort_words("r", 0, 1, nc.vector.tensor_copy)
+        sort_words("r", 0, 0, nc.scalar.copy)
+        query(0, 0)
+        sigmoid(0, 0)
         turn("x", 1, 0)
         empty("x", 1, 0)
         turn("x", 1, 1)
         empty("x", 1, 1)
         quantise_wq(2)
-        sort_words("ow", 0, 0, nc.scalar.copy)
-        sort_words("ow", 0, 1, nc.vector.tensor_copy)
-        quantise_wq(3)
-        query(0, 0)
-        sigmoid(0, 0)
-        turn_r(0, 0)
-        turn_r(0, 1)
-        turn("ow", 0, 0)
-        empty("ow", 0, 0)
-        turn("ow", 0, 1)
-        empty("ow", 0, 1)
-        turn("ow", 1, 0)
-        empty("ow", 1, 0)
-        turn("ow", 1, 1)
-        empty("ow", 1, 1)
-        quantise_x(1)
         scale_x(2, 0)
+        quantise_wq(3)
         scale_x(2, 1)
-        scale_x(3, 0)
+        sort_words("r", 0, 1, nc.scalar.copy)
         query(0, 1)
         sigmoid(0, 1)
         query(0, 2)
         sigmoid(0, 2)
         query(0, 3)
         sigmoid(0, 3)
+        quantise_x(1)
+        scale_x(3, 0)
         turn("x", 2, 0)
         empty("x", 2, 0)
+        turn_r(0, 0)
         turn("x", 2, 1)
         empty("x", 2, 1)
-        turn("ow", 2, 0)
-        empty("ow", 2, 0)
-        turn("ow", 2, 1)
-        empty("ow", 2, 1)
-        quantise_ow(0)
-        scale_x(3, 1)
+        turn("ow", 0, 0)
+        empty("ow", 0, 0)
+        turn_r(0, 1)
+        turn("ow", 0, 1)
+        empty("ow", 0, 1)
         gate(0, 0)
-        quantise_ow(1)
+        scale_x(3, 1)
         gate(0, 1)
-        sort_words("r", 1, 0, nc.vector.tensor_copy)
-        sort_words("r", 1, 1, nc.vector.tensor_copy)
+        sort_words("r", 1, 0, nc.scalar.copy)
+        sort_words("r", 1, 1, nc.scalar.copy)
         query(1, 0)
         sigmoid(1, 0)
         query(1, 1)
@@ -404,21 +421,26 @@ def tile_aft_full_pb_kernel(tc, x_bytes, x_scale, wq_w, wq_b, r_aft, out_w, out_
         sigmoid(1, 2)
         query(1, 3)
         sigmoid(1, 3)
-        quantise_y(0)
         quantise_x(2)
-        quantise_ow(2)
+        quantise_ow(0)
+        quantise_y(0)
+        turn("ow", 1, 0)
+        empty("ow", 1, 0)
         turn_r(1, 0)
+        turn("ow", 1, 1)
+        empty("ow", 1, 1)
+        turn("ow", 2, 0)
+        empty("ow", 2, 0)
         turn_r(1, 1)
-        turn("ow", 3, 0)
-        empty("ow", 3, 0)
-        turn("ow", 3, 1)
-        empty("ow", 3, 1)
+        turn("ow", 2, 1)
+        empty("ow", 2, 1)
         gate(1, 0)
         gate(1, 1)
         sort_words("r", 2, 0, nc.scalar.copy)
         sort_words("r", 2, 1, nc.scalar.copy)
-        project(0)
-        project(1)
+        quantise_ow(1)
+        quantise_y(1)
+        quantise_ow(2)
         query(2, 0)
         sigmoid(2, 0)
         query(2, 1)
@@ -427,74 +449,73 @@ def tile_aft_full_pb_kernel(tc, x_bytes, x_scale, wq_w, wq_b, r_aft, out_w, out_
         sigmoid(2, 2)
         query(2, 3)
         sigmoid(2, 3)
+        project(0)
+        project(1)
+        project(4)
         finish(0)
         store(0)
-        quantise_y(1)
-        quantise_ow(3)
         finish(1)
         store(1)
-        project(2)
-        project(3)
-        bias_beside_vector(3)
-        finish(2)
-        store(2)
+        finish(4)
+        store(4)
+        turn("ow", 3, 0)
+        empty("ow", 3, 0)
         turn_r(2, 0)
-        turn_r(2, 1)
+        turn("ow", 3, 1)
+        empty("ow", 3, 1)
         turn("x", 3, 0)
         empty("x", 3, 0)
+        turn_r(2, 1)
         turn("x", 3, 1)
         empty("x", 3, 1)
         gate(2, 0)
-        gate(2, 1)
-        store(3)
+        quantise_ow(3)
         sort_words("r", 3, 0, nc.scalar.copy)
         sort_words("r", 3, 1, nc.scalar.copy)
-        project(4)
-        project(5)
-        project(6)
-        bias_beside_vector(6)
-        project(7)
+        gate(2, 1)
         quantise_x(3)
-        finish(4)
-        store(4)
         quantise_y(2)
-        finish(5)
-        store(5)
+        project(5)
+        bias_behind_quantise(5, 2, 0)
+        project(2)
+        bias_behind_quantise(2, 2, 1)
+        project(3)
+        project(6)
+        project(7)
+        finish(3)
+        store(3)
+        finish(6)
+        store(6)
         finish(7)
         store(7)
-        query_tokens(0, 0)
-        sigmoid_tokens(0, 0)
-        query_tokens(0, 1)
-        sigmoid_tokens(0, 1)
-        query_tokens(0, 2)
-        sigmoid_tokens(0, 2)
-        query_tokens(0, 3)
-        sigmoid_tokens(0, 3)
+        store(5)
+        query_half(0, 0)
+        query_half(0, 1)
         turn_r(3, 0)
         turn_r(3, 1)
-        store(6)
         project(8)
         query_tokens(1, 0)
         sigmoid_tokens(1, 0)
         query_tokens(1, 1)
         sigmoid_tokens(1, 1)
-        project(9)
         query_tokens(1, 2)
         sigmoid_tokens(1, 2)
         query_tokens(1, 3)
         sigmoid_tokens(1, 3)
+        project(9)
         gate_tokens(3, 0, 0)
         gate_tokens(3, 1, 0)
+        store(2)
         finish(8)
         store(8)
         quantise_tokens(3, 0)
-        finish(9)
-        store(9)
         gate_tokens(3, 0, 1)
         project(10)
         project(11)
         project(12)
         project(14)
+        finish(9)
+        store(9)
         gate_tokens(3, 1, 1)
         finish(10)
         store(10)

@@ -25,8 +25,8 @@ HALF = 512
 WORDS = HALF // 2
 SORTED_BUFS = 4
 RESULT_BUFS = 13
-LATE_Y = (("y", 2), ("y", 3))
-KIN_BUFS = 8
+HANDED_ON = (("x", 1), ("y", 0), ("y", 1), ("y", 2))
+KIN_BUFS = 6
 
 
 def tile_aft_full_pb_kernel(tc, x_bytes, x_scale, wq_w, wq_b, r_aft, out_w, out_b, out):
@@ -107,6 +107,15 @@ def tile_aft_full_pb_kernel(tc, x_bytes, x_scale, wq_w, wq_b, r_aft, out_w, out_
                 in_=rows.bitcast(F32).rearrange("p (g c e u) -> p g c u e", g=2, u=2, e=2),
             )
 
+        def sort_behind_quantise(name, b, key):
+            ordered = flow.tile([P, J, HALF], F32, name="%s_in%d" % key, align_bytes=64)
+            for j in range(J):
+                held["sorted", name, b, j] = ordered[:, j]
+            nc.gpsimd.tensor_copy(
+                out=ordered[:].bitcast(U32).rearrange("p j (g u c) -> p (j g) u c", g=2, u=2),
+                in_=(r_raw if name == "r" else ow_raw)[b][:].bitcast(U32).rearrange("p j (g c u) -> p (j g) u c", g=2, u=2),
+            )
+
         def words_of(key, rows, g, u):
             if ("sorted",) + key in held:
                 return held[("sorted",) + key][:, WORDS * g + P * u : WORDS * g + P * (u + 1)]
@@ -114,8 +123,8 @@ def tile_aft_full_pb_kernel(tc, x_bytes, x_scale, wq_w, wq_b, r_aft, out_w, out_
 
         def kin_tile(key):
             if key not in held:
-                if key in LATE_Y:
-                    held[key] = flow.tile([P, 2, 4 * TB], BF16, name="y_in%d" % key[1], align_bytes=64)
+                if key in HANDED_ON:
+                    held[key] = flow.tile([P, 2, 4 * TB], BF16, name="%s_in%d" % key, align_bytes=64)
                 else:
                     held[key] = flow.tile([P, 2, 4 * TB], BF16, name="kin", align_bytes=64, bufs=KIN_BUFS)
             return held[key]
@@ -127,9 +136,13 @@ def tile_aft_full_pb_kernel(tc, x_bytes, x_scale, wq_w, wq_b, r_aft, out_w, out_
                 return wq_rest[i - 1][:, s, :] if i else wq_first[s][:]
             return ow_raw[i][:, s, :]
 
-        def turn(name, i, s):
+        def turn(name, i, s, warm=0):
             turned = banks.tile([P, 2, P // 2, 2, 2], F32, name="bank")
             held["turned", name, i, s] = turned
+            if warm:
+                rows = rows_of(name, i, s)
+                idle = turned[:].rearrange("p g c u i -> p (g c u i)")
+                nc.tensor.matmul(out=idle[:, :warm], lhsT=rows[:, :P], rhs=rows[:, :warm], start=True, stop=True)
             for g in range(2):
                 for u in range(2):
                     nc.tensor.transpose(turned[:, g, :, u, :], words_of((name, i, s), rows_of(name, i, s), g, u), identity[:])
@@ -342,8 +355,8 @@ def tile_aft_full_pb_kernel(tc, x_bytes, x_scale, wq_w, wq_b, r_aft, out_w, out_
         load_r(0)
         load_x(3)
         load_ow(0)
-        load_ow(1)
         load_r(1)
+        load_ow(1)
         load_ow(2)
         load_r(2)
         load_ow(3)
@@ -394,10 +407,12 @@ def tile_aft_full_pb_kernel(tc, x_bytes, x_scale, wq_w, wq_b, r_aft, out_w, out_
         sigmoid(0, 1)
         query(0, 2)
         sigmoid(0, 2)
+        sort_words("ow", 0, 1, nc.scalar.copy)
         query(0, 3)
         sigmoid(0, 3)
-        quantise_x(1)
         scale_x(3, 0)
+        quantise_x(1)
+        sort_behind_quantise("r", 1, ("x", 1))
         turn("x", 2, 0)
         empty("x", 2, 0)
         turn_r(0, 0)
@@ -409,10 +424,8 @@ def tile_aft_full_pb_kernel(tc, x_bytes, x_scale, wq_w, wq_b, r_aft, out_w, out_
         turn("ow", 0, 1)
         empty("ow", 0, 1)
         gate(0, 0)
-        scale_x(3, 1)
         gate(0, 1)
-        sort_words("r", 1, 0, nc.scalar.copy)
-        sort_words("r", 1, 1, nc.scalar.copy)
+        sort_words("ow", 2, 0, nc.scalar.copy)
         query(1, 0)
         sigmoid(1, 0)
         query(1, 1)
@@ -421,9 +434,11 @@ def tile_aft_full_pb_kernel(tc, x_bytes, x_scale, wq_w, wq_b, r_aft, out_w, out_
         sigmoid(1, 2)
         query(1, 3)
         sigmoid(1, 3)
+        scale_x(3, 1)
         quantise_x(2)
         quantise_ow(0)
         quantise_y(0)
+        sort_behind_quantise("r", 2, ("y", 0))
         turn("ow", 1, 0)
         empty("ow", 1, 0)
         turn_r(1, 0)
@@ -436,11 +451,10 @@ def tile_aft_full_pb_kernel(tc, x_bytes, x_scale, wq_w, wq_b, r_aft, out_w, out_
         empty("ow", 2, 1)
         gate(1, 0)
         gate(1, 1)
-        sort_words("r", 2, 0, nc.scalar.copy)
-        sort_words("r", 2, 1, nc.scalar.copy)
+        sort_words("ow", 3, 0, nc.scalar.copy)
         quantise_ow(1)
-        quantise_y(1)
         quantise_ow(2)
+        quantise_y(1)
         query(2, 0)
         sigmoid(2, 0)
         query(2, 1)

@@ -23,10 +23,12 @@ J = TB // P
 PAIRS = 4
 HALF = 512
 WORDS = HALF // 2
-SORTED_BUFS = 4
-RESULT_BUFS = 13
-HANDED_ON = (("x", 1), ("y", 0), ("y", 1), ("y", 2))
-KIN_BUFS = 6
+SORTED_BUFS = 6
+RESULT_BUFS = 12
+SORTED_IN_RUN = 1
+KIN_BUFS = 7
+HANDED_ON = (("x", 1), ("y", 0), ("y", 2))
+LAST = BLOCKS - 1
 
 
 def tile_aft_full_pb_kernel(tc, x_bytes, x_scale, wq_w, wq_b, r_aft, out_w, out_b, out):
@@ -56,8 +58,8 @@ def tile_aft_full_pb_kernel(tc, x_bytes, x_scale, wq_w, wq_b, r_aft, out_w, out_
 
         x_raw = kept("x_raw", BLOCKS, [P, J, D], U8)
         r_raw = kept("r_raw", BLOCKS, [P, J, D], BF16)
-        wq_first = kept("wq_first", 2, [P, D], BF16)
-        wq_rest = kept("wq_rest", PAIRS - 1, [P, 2, D], BF16)
+        wq_first = kept("wq_first", 4, [P, D], BF16)
+        wq_rest = kept("wq_rest", PAIRS - 2, [P, 2, D], BF16)
         ow_raw = kept("ow_raw", PAIRS, [P, 2, D], BF16)
         x_codes = kept("x_codes", BLOCKS, [P, 2, TB], U32)
         x_scales = kept("x_scales", BLOCKS, [P, 2, TB], U8)
@@ -67,7 +69,7 @@ def tile_aft_full_pb_kernel(tc, x_bytes, x_scale, wq_w, wq_b, r_aft, out_w, out_
         ow_scales = kept("ow_scales", 2, [P, 2, HALF], U8)
         y_codes = kept("y_codes", BLOCKS, [P, 2, TB], U32)
         y_scales = kept("y_scales", BLOCKS, [P, 2, TB], U8)
-        gate_sig = kept("gate_sig", 2 * (BLOCKS - 1), [P, 4, TB], F32)
+        gate_sig = kept("gate_sig", 2 * LAST, [P, 4, TB], F32)
         last_sig = kept("last_sig", 2 * J, [P, 4, P], F32)
         held = {}
 
@@ -77,11 +79,11 @@ def tile_aft_full_pb_kernel(tc, x_bytes, x_scale, wq_w, wq_b, r_aft, out_w, out_
         def load_r(b):
             nc.sync.dma_start(out=r_raw[b][:], in_=r_hbm[b])
 
-        def load_wq_first(s):
-            nc.sync.dma_start(out=wq_first[s][:], in_=wq_hbm[0][0][:, s, :])
+        def load_wq_first(i, s):
+            nc.sync.dma_start(out=wq_first[2 * i + s][:], in_=wq_hbm[0][i][:, s, :])
 
         def load_wq(i):
-            nc.sync.dma_start(out=wq_rest[i - 1][:], in_=wq_hbm[i // 2][i % 2])
+            nc.sync.dma_start(out=wq_rest[i - 2][:], in_=wq_hbm[i // 2][i % 2])
 
         def load_ow(i):
             nc.sync.dma_start(out=ow_raw[i][:], in_=ow_hbm[i])
@@ -98,28 +100,37 @@ def tile_aft_full_pb_kernel(tc, x_bytes, x_scale, wq_w, wq_b, r_aft, out_w, out_
         def quantise(codes, scales, values):
             nc.vector.quantize_mx(out=codes.bitcast(FP8X4), scales=scales, in_=values)
 
-        def sort_words(name, i, s, copy):
+        def rows_of(name, i, s):
+            if name == "x":
+                return held["x_wide", i, s][:]
+            if name == "wq":
+                return wq_rest[i - 2][:, s, :] if i >= 2 else wq_first[2 * i + s][:]
+            return (r_raw if name == "r" else ow_raw)[i][:, s, :]
+
+        def sort_rows(name, i, s):
             ordered = flow.tile([P, HALF], F32, name="ordered", align_bytes=64, bufs=SORTED_BUFS)
             held["sorted", name, i, s] = ordered
-            rows = r_raw[i][:, s, :] if name == "r" else rows_of(name, i, s)
-            copy(
+            nc.scalar.copy(
                 out=ordered[:].rearrange("p (g u c e) -> p g c u e", g=2, u=2, e=2),
-                in_=rows.bitcast(F32).rearrange("p (g c e u) -> p g c u e", g=2, u=2, e=2),
+                in_=rows_of(name, i, s).bitcast(F32).rearrange("p (g c e u) -> p g c u e", g=2, u=2, e=2),
             )
 
-        def sort_behind_quantise(name, b, key):
-            ordered = flow.tile([P, J, HALF], F32, name="%s_in%d" % key, align_bytes=64)
+        def handed_on(key, shape):
+            return flow.tile(shape, F32, name="%s_in%d" % key, align_bytes=64)
+
+        def sort_r_behind(b, key):
+            ordered = handed_on(key, [P, J, HALF])
             for j in range(J):
-                held["sorted", name, b, j] = ordered[:, j]
+                held["sorted", "r", b, j] = ordered[:, j]
             nc.gpsimd.tensor_copy(
                 out=ordered[:].bitcast(U32).rearrange("p j (g u c) -> p (j g) u c", g=2, u=2),
-                in_=(r_raw if name == "r" else ow_raw)[b][:].bitcast(U32).rearrange("p j (g c u) -> p (j g) u c", g=2, u=2),
+                in_=r_raw[b][:].bitcast(U32).rearrange("p j (g c u) -> p (j g) u c", g=2, u=2),
             )
 
-        def words_of(key, rows, g, u):
-            if ("sorted",) + key in held:
-                return held[("sorted",) + key][:, WORDS * g + P * u : WORDS * g + P * (u + 1)]
-            return rows.bitcast(F32)[:, WORDS * g + u : WORDS * (g + 1) : 2]
+        def words_of(name, i, s, g, u):
+            if ("sorted", name, i, s) in held:
+                return held["sorted", name, i, s][:, WORDS * g + P * u : WORDS * g + P * (u + 1)]
+            return rows_of(name, i, s).bitcast(F32)[:, WORDS * g + u : WORDS * (g + 1) : 2]
 
         def kin_tile(key):
             if key not in held:
@@ -129,31 +140,24 @@ def tile_aft_full_pb_kernel(tc, x_bytes, x_scale, wq_w, wq_b, r_aft, out_w, out_
                     held[key] = flow.tile([P, 2, 4 * TB], BF16, name="kin", align_bytes=64, bufs=KIN_BUFS)
             return held[key]
 
-        def rows_of(name, i, s):
-            if name == "x":
-                return held["x_wide", i, s][:]
-            if name == "wq":
-                return wq_rest[i - 1][:, s, :] if i else wq_first[s][:]
-            return ow_raw[i][:, s, :]
-
-        def turn(name, i, s, warm=0):
+        def turn(name, i, s):
             turned = banks.tile([P, 2, P // 2, 2, 2], F32, name="bank")
             held["turned", name, i, s] = turned
-            if warm:
-                rows = rows_of(name, i, s)
-                idle = turned[:].rearrange("p g c u i -> p (g c u i)")
-                nc.tensor.matmul(out=idle[:, :warm], lhsT=rows[:, :P], rhs=rows[:, :warm], start=True, stop=True)
             for g in range(2):
                 for u in range(2):
-                    nc.tensor.transpose(turned[:, g, :, u, :], words_of((name, i, s), rows_of(name, i, s), g, u), identity[:])
+                    nc.tensor.transpose(turned[:, g, :, u, :], words_of(name, i, s, g, u), identity[:])
 
-        def empty(name, i, s, copy=nc.scalar.copy):
+        def empty(name, i, s, copy):
             kin_words = kin_tile((name, i))[:].bitcast(F32)
             if name == "wq":
                 kin_words = kin_words[:, s, :].rearrange("p (g w) -> p g w", g=2)
             else:
                 kin_words = kin_words[:, :, WORDS * s : WORDS * (s + 1)]
             copy(out=kin_words.rearrange("p g (c i u) -> p g c u i", i=2, u=2), in_=held["turned", name, i, s][:])
+
+        def turn_and_empty(name, i, s):
+            turn(name, i, s)
+            empty(name, i, s, nc.scalar.copy)
 
         def spread_scale(g):
             spread = gate_banks.tile([P, 4, P], F32, name="turned")
@@ -194,75 +198,40 @@ def tile_aft_full_pb_kernel(tc, x_bytes, x_scale, wq_w, wq_b, r_aft, out_w, out_
             for j in range(J):
                 pairs = slice(j * P // 2, (j + 1) * P // 2)
                 for u in range(2):
-                    nc.tensor.transpose(turned[:, pairs, u, :], words_of(("r", b, j), r_raw[b][:, j, :], f, u), identity[:])
+                    nc.tensor.transpose(turned[:, pairs, u, :], words_of("r", b, j, f, u), identity[:])
 
-        def query(b, i):
-            q = banks.tile([P, 2, TB], F32, name="bank")
-            held["q", b, i] = q
-            for s in range(2):
-                for g in range(2):
-                    nc.tensor.matmul_mx(
-                        out=q[:, s, :],
-                        lhsT=wq_codes[i][:, s, g, :].bitcast(FP8X4),
-                        lhsT_scale=wq_scales[i][:, s, g, :],
-                        rhs=x_codes[b][:, g, :].bitcast(FP8X4),
-                        rhs_scale=x_scales[b][:, g, :],
-                        start=(g == 0),
-                        stop=(g == 1),
-                    )
-
-        def sigmoid(b, i):
-            f, h = i // 2, i % 2
-            for s in range(2):
-                t = 2 * h + s
-                nc.scalar.activation(
-                    out=gate_sig[2 * b + f][:, t, :], in_=held["q", b, i][:, s, :], func=SIGMOID, bias=query_bias[:, f, t : t + 1]
-                )
-
-        def query_tokens(j, i):
-            q = banks.tile([P, 2, P], F32, name="bank")
-            held["q", "last", j, i] = q
-            for s in range(2):
-                for g in range(2):
-                    nc.tensor.matmul_mx(
-                        out=q[:, s, :],
-                        lhsT=wq_codes[i][:, s, g, :].bitcast(FP8X4),
-                        lhsT_scale=wq_scales[i][:, s, g, :],
-                        rhs=x_codes[BLOCKS - 1][:, g, P * j : P * (j + 1)].bitcast(FP8X4),
-                        rhs_scale=x_scales[BLOCKS - 1][:, g, P * j : P * (j + 1)],
-                        start=(g == 0),
-                        stop=(g == 1),
-                    )
-
-        def sigmoid_tokens(j, i):
-            f, h = i // 2, i % 2
-            for s in range(2):
-                t = 2 * h + s
-                nc.scalar.activation(
-                    out=last_sig[2 * j + f][:, t, :], in_=held["q", "last", j, i][:, s, :], func=SIGMOID, bias=query_bias[:, f, t : t + 1]
-                )
-
-        def query_half(j, f):
-            q = banks.tile([P, 4, P], F32, name="bank")
-            for t in range(4):
+        def query(b, tokens, tiles, sig):
+            q = banks.tile([P, len(tiles), tokens.stop - tokens.start], F32, name="bank")
+            for place, (f, t) in enumerate(tiles):
                 i, s = 2 * f + t // 2, t % 2
                 for g in range(2):
                     nc.tensor.matmul_mx(
-                        out=q[:, t, :],
+                        out=q[:, place, :],
                         lhsT=wq_codes[i][:, s, g, :].bitcast(FP8X4),
                         lhsT_scale=wq_scales[i][:, s, g, :],
-                        rhs=x_codes[BLOCKS - 1][:, g, P * j : P * (j + 1)].bitcast(FP8X4),
-                        rhs_scale=x_scales[BLOCKS - 1][:, g, P * j : P * (j + 1)],
+                        rhs=x_codes[b][:, g, tokens].bitcast(FP8X4),
+                        rhs_scale=x_scales[b][:, g, tokens],
                         start=(g == 0),
                         stop=(g == 1),
                     )
-            for t in range(4):
-                nc.scalar.activation(out=last_sig[2 * j + f][:, t, :], in_=q[:, t, :], func=SIGMOID, bias=query_bias[:, f, t : t + 1])
+            for place, (f, t) in enumerate(tiles):
+                nc.scalar.activation(out=sig[:, t, :], in_=q[:, place, :], func=SIGMOID, bias=query_bias[:, f, t : t + 1])
+
+        def pair_tiles(i):
+            return [(i // 2, 2 * (i % 2) + s) for s in range(2)]
+
+        def query_pair(b, i):
+            query(b, slice(0, TB), pair_tiles(i), gate_sig[2 * b + i // 2])
 
         def query_block(b):
             for i in range(PAIRS):
-                query(b, i)
-                sigmoid(b, i)
+                query_pair(b, i)
+
+        def query_last_half(j, f):
+            query(LAST, slice(P * j, P * (j + 1)), [(f, t) for t in range(4)], last_sig[2 * j + f])
+
+        def query_last_pair(j, i):
+            query(LAST, slice(P * j, P * (j + 1)), pair_tiles(i), last_sig[2 * j + i // 2])
 
         def gate(b, f):
             nc.vector.tensor_tensor(
@@ -272,89 +241,81 @@ def tile_aft_full_pb_kernel(tc, x_bytes, x_scale, wq_w, wq_b, r_aft, out_w, out_
                 op=MULT,
             )
 
-        def gate_tokens(b, f, j):
+        def gate_last(f, j):
             pairs = slice(j * P // 2, (j + 1) * P // 2)
             nc.vector.tensor_tensor(
-                out=kin_tile(("y", b))[:, j, HALF * f : HALF * (f + 1)].rearrange("p (c i u e) -> p c u e i", i=2, u=2, e=2),
-                in0=held["r", b, f][:, pairs].bitcast(BF16).rearrange("p c u (i e) -> p c u e i", e=2),
+                out=kin_tile(("y", LAST))[:, j, HALF * f : HALF * (f + 1)].rearrange("p (c i u e) -> p c u e i", i=2, u=2, e=2),
+                in0=held["r", LAST, f][:, pairs].bitcast(BF16).rearrange("p c u (i e) -> p c u e i", e=2),
                 in1=last_sig[2 * j + f][:].rearrange("p (u e) (c i) -> p c u e i", u=2, i=2),
                 op=MULT,
             )
 
-        def quantise_tokens(b, j):
-            quantise(y_codes[b][:, j, :], y_scales[b][:, j, :], held["y", b][:, j, :])
+        def quantise_last(j):
+            quantise(y_codes[LAST][:, j, :], y_scales[LAST][:, j, :], held["y", LAST][:, j, :])
 
         def y_part(tiles, b, j, g):
-            if b == BLOCKS - 1:
+            if b == LAST:
                 return tiles[b][:, j, g * P : (g + 1) * P]
             return tiles[b][:, g, j * P : (j + 1) * P]
 
         def quantise_y(b):
             quantise(flat(y_codes[b]), flat(y_scales[b]), flat(held["y", b]))
 
-        def project(n):
-            b, c, j = n // 4, n // 2 % 2, n % 2
-            held["sums", n] = banks.tile([P, HALF], F32, name="bank")
-            for g in range(2):
-                nc.tensor.matmul_mx(
-                    out=held["sums", n][:],
-                    lhsT=y_part(y_codes, b, j, g).bitcast(FP8X4),
-                    lhsT_scale=y_part(y_scales, b, j, g),
-                    rhs=ow_codes[c][:, g, :].bitcast(FP8X4),
-                    rhs_scale=ow_scales[c][:, g, :],
-                    start=(g == 0),
-                    stop=(g == 1),
-                )
+        def project(*tiles):
+            for n in tiles:
+                b, c, j = n // 4, n // 2 % 2, n % 2
+                held["sums", n] = banks.tile([P, HALF], F32, name="bank")
+                for g in range(2):
+                    nc.tensor.matmul_mx(
+                        out=held["sums", n][:],
+                        lhsT=y_part(y_codes, b, j, g).bitcast(FP8X4),
+                        lhsT_scale=y_part(y_scales, b, j, g),
+                        rhs=ow_codes[c][:, g, :].bitcast(FP8X4),
+                        rhs_scale=ow_scales[c][:, g, :],
+                        start=(g == 0),
+                        stop=(g == 1),
+                    )
 
         def result_and_bias(n):
             c = n // 2 % 2
-            held["result", n] = flow.tile([P, HALF], F32, name="result", align_bytes=64, bufs=RESULT_BUFS)
-            return held["result", n][:], out_bias[:, HALF * c : HALF * (c + 1)]
+            result = flow.tile([P, HALF], F32, name="result", align_bytes=64, bufs=RESULT_BUFS)
+            return result[:], out_bias[:, HALF * c : HALF * (c + 1)]
 
-        def store(n):
+        def store(n, result):
             b, c, j = n // 4, n // 2 % 2, n % 2
-            nc.sync.dma_start(out=out_hbm[b][:, j, HALF * c : HALF * (c + 1)], in_=held["result", n][:])
+            nc.sync.dma_start(out=out_hbm[b][:, j, HALF * c : HALF * (c + 1)], in_=result)
 
-        def finish(n):
-            result, bias = result_and_bias(n)
-            nc.vector.tensor_tensor(out=result, in0=held["sums", n][:], in1=bias, op=ADD)
-
-        def bias_beside_vector(n):
-            result, bias = result_and_bias(n)
-            nc.scalar.copy(out=result, in_=held["sums", n][:])
-            nc.gpsimd.tensor_tensor(out=result, in0=result, in1=bias, op=ADD)
-
-        def bias_behind_quantise(n, b, place):
-            result, bias = result_and_bias(n)
-            nc.scalar.copy(out=result, in_=held["sums", n][:])
-            if ("spare", b) not in held:
-                held["spare", b] = flow.tile([P, 2, HALF], F32, name="y_in%d" % b, align_bytes=64)
-            held["result", n] = held["spare", b][:, place]
-            nc.gpsimd.tensor_tensor(out=held["result", n], in0=result, in1=bias, op=ADD)
-
-        def project_and_finish(*tiles):
+        def finish(*tiles):
             for n in tiles:
-                project(n)
-                finish(n)
-                store(n)
+                result, bias = result_and_bias(n)
+                nc.vector.tensor_tensor(out=result, in0=held["sums", n][:], in1=bias, op=ADD)
+                store(n, result)
+
+        def bias_on_gpsimd(n, result):
+            sums, bias = result_and_bias(n)
+            nc.scalar.copy(out=sums, in_=held["sums", n][:])
+            nc.gpsimd.tensor_tensor(out=result, in0=sums, in1=bias, op=ADD)
 
         nc.sync.dma_start(out=x_mult[:], in_=x_scale[0, :, :].rearrange("o (g p t) -> p (o g) t", p=P, t=4))
         nc.gpsimd.memset(one_column[:], 0.0)
         make_identity(nc, identity[:])
         nc.scalar.activation(out=one_column[:], in_=one_column[:], func=SIGMOID)
 
-        load_wq_first(0)
+        rounds = ((("x", 2), ("ow", 0)), (("ow", 1), ("ow", 2)), (("ow", 3), ("x", 3)))
+
+        load_wq_first(0, 0)
         load_x(0)
-        load_wq_first(1)
-        load_wq(1)
+        load_wq_first(0, 1)
+        load_wq_first(1, 0)
+        load_wq_first(1, 1)
         load_x(1)
         load_wq(2)
-        load_query_bias()
         load_wq(3)
         load_x(2)
         load_r(0)
-        load_x(3)
+        load_query_bias()
         load_ow(0)
+        load_x(3)
         load_r(1)
         load_ow(1)
         load_ow(2)
@@ -362,187 +323,121 @@ def tile_aft_full_pb_kernel(tc, x_bytes, x_scale, wq_w, wq_b, r_aft, out_w, out_
         load_ow(3)
         load_r(3)
         load_out_bias()
+
         spread_scale(0)
         spread_scale(1)
         scale_x(0, 0, HALF)
         scale_x(0, 1)
-        turn("wq", 0, 0)
-        empty("wq", 0, 0)
-        turn("wq", 0, 1)
-        empty("wq", 0, 1)
-        turn("x", 0, 0)
-        empty("x", 0, 0)
+        turn_and_empty("wq", 0, 0)
+        turn_and_empty("wq", 0, 1)
+        turn_and_empty("wq", 1, 0)
+        turn_and_empty("x", 0, 0)
         scale_x(1, 0)
-        scale_x(1, 1)
-        turn("wq", 1, 0)
-        empty("wq", 1, 0)
-        turn("wq", 1, 1)
-        empty("wq", 1, 1)
-        turn("x", 0, 1)
-        empty("x", 0, 1)
+        turn_and_empty("wq", 1, 1)
+        turn_and_empty("x", 0, 1)
         quantise_wq(0)
-        turn("wq", 2, 0)
-        empty("wq", 2, 0)
-        turn("wq", 2, 1)
-        empty("wq", 2, 1)
+        scale_x(1, 1)
         quantise_x(0)
-        turn("wq", 3, 0)
-        empty("wq", 3, 0)
-        turn("wq", 3, 1)
-        empty("wq", 3, 1)
+        for i in range(2, PAIRS):
+            turn_and_empty("wq", i, 0)
+            turn_and_empty("wq", i, 1)
+        turn_and_empty("x", 1, 0)
         quantise_wq(1)
-        sort_words("r", 0, 0, nc.scalar.copy)
-        query(0, 0)
-        sigmoid(0, 0)
-        turn("x", 1, 0)
-        empty("x", 1, 0)
-        turn("x", 1, 1)
-        empty("x", 1, 1)
+
+        sort_rows("r", 0, 0)
+        query_pair(0, 0)
         quantise_wq(2)
         scale_x(2, 0)
         quantise_wq(3)
         scale_x(2, 1)
-        sort_words("r", 0, 1, nc.scalar.copy)
-        query(0, 1)
-        sigmoid(0, 1)
-        query(0, 2)
-        sigmoid(0, 2)
-        sort_words("ow", 0, 1, nc.scalar.copy)
-        query(0, 3)
-        sigmoid(0, 3)
+        turn_and_empty("x", 1, 1)
+        sort_rows("r", 0, 1)
+
+        def sort_for_round(b):
+            name, i = rounds[b][1]
+            for s in range(2 - SORTED_IN_RUN, 2):
+                sort_rows(name, i, s)
+
+        def run(b, keep_first):
+            (first, i), (second, k) = rounds[b]
+            turn(first, i, 0)
+            if not keep_first:
+                empty(first, i, 0, nc.scalar.copy)
+            turn_r(b, 0)
+            turn_and_empty(first, i, 1)
+            turn_and_empty(second, k, 0)
+            turn_r(b, 1)
+            turn_and_empty(second, k, 1)
+
+        def run_beside_gpsimd(b):
+            run(b, True)
+            empty(*rounds[b][0], 0, nc.vector.tensor_copy)
+            gate(b, 0)
+            gate(b, 1)
+
+        sort_for_round(0)
+        for i in range(1, PAIRS):
+            query_pair(0, i)
         scale_x(3, 0)
         quantise_x(1)
-        sort_behind_quantise("r", 1, ("x", 1))
-        turn("x", 2, 0)
-        empty("x", 2, 0)
-        turn_r(0, 0)
-        turn("x", 2, 1)
-        empty("x", 2, 1)
-        turn("ow", 0, 0)
-        empty("ow", 0, 0)
-        turn_r(0, 1)
-        turn("ow", 0, 1)
-        empty("ow", 0, 1)
-        gate(0, 0)
-        gate(0, 1)
-        sort_words("ow", 2, 0, nc.scalar.copy)
-        query(1, 0)
-        sigmoid(1, 0)
-        query(1, 1)
-        sigmoid(1, 1)
-        query(1, 2)
-        sigmoid(1, 2)
-        query(1, 3)
-        sigmoid(1, 3)
+        sort_r_behind(1, ("x", 1))
         scale_x(3, 1)
-        quantise_x(2)
+        run_beside_gpsimd(0)
+
+        sort_for_round(1)
+        query_block(1)
         quantise_ow(0)
         quantise_y(0)
-        sort_behind_quantise("r", 2, ("y", 0))
-        turn("ow", 1, 0)
-        empty("ow", 1, 0)
-        turn_r(1, 0)
-        turn("ow", 1, 1)
-        empty("ow", 1, 1)
-        turn("ow", 2, 0)
-        empty("ow", 2, 0)
-        turn_r(1, 1)
-        turn("ow", 2, 1)
-        empty("ow", 2, 1)
-        gate(1, 0)
-        gate(1, 1)
-        sort_words("ow", 3, 0, nc.scalar.copy)
+        sort_r_behind(2, ("y", 0))
+        quantise_x(2)
+        run_beside_gpsimd(1)
+
+        sort_for_round(2)
+        query_block(2)
         quantise_ow(1)
-        quantise_ow(2)
         quantise_y(1)
-        query(2, 0)
-        sigmoid(2, 0)
-        query(2, 1)
-        sigmoid(2, 1)
-        query(2, 2)
-        sigmoid(2, 2)
-        query(2, 3)
-        sigmoid(2, 3)
-        project(0)
-        project(1)
-        project(4)
-        finish(0)
-        store(0)
-        finish(1)
-        store(1)
-        finish(4)
-        store(4)
-        turn("ow", 3, 0)
-        empty("ow", 3, 0)
-        turn_r(2, 0)
-        turn("ow", 3, 1)
-        empty("ow", 3, 1)
-        turn("x", 3, 0)
-        empty("x", 3, 0)
-        turn_r(2, 1)
-        turn("x", 3, 1)
-        empty("x", 3, 1)
+        quantise_ow(2)
+        project(0, 1)
+        finish(0, 1)
+        run(2, False)
         gate(2, 0)
         quantise_ow(3)
-        sort_words("r", 3, 0, nc.scalar.copy)
-        sort_words("r", 3, 1, nc.scalar.copy)
         gate(2, 1)
-        quantise_x(3)
+        sort_rows("r", LAST, 0)
+        sort_rows("r", LAST, 1)
+
+        quantise_x(LAST)
         quantise_y(2)
+        beside = handed_on(("y", 2), [P, 2, HALF])
+        project(4)
+        bias_on_gpsimd(4, beside[:, 0])
         project(5)
-        bias_behind_quantise(5, 2, 0)
-        project(2)
-        bias_behind_quantise(2, 2, 1)
-        project(3)
-        project(6)
-        project(7)
-        finish(3)
-        store(3)
-        finish(6)
-        store(6)
-        finish(7)
-        store(7)
-        store(5)
-        query_half(0, 0)
-        query_half(0, 1)
-        turn_r(3, 0)
-        turn_r(3, 1)
+        bias_on_gpsimd(5, beside[:, 1])
+        project(2, 3, 6, 7)
+        finish(2, 3, 6, 7)
+        store(4, beside[:, 0])
+
+        query_last_half(0, 0)
+        query_last_half(0, 1)
+        turn_r(LAST, 0)
+        turn_r(LAST, 1)
         project(8)
-        query_tokens(1, 0)
-        sigmoid_tokens(1, 0)
-        query_tokens(1, 1)
-        sigmoid_tokens(1, 1)
-        query_tokens(1, 2)
-        sigmoid_tokens(1, 2)
-        query_tokens(1, 3)
-        sigmoid_tokens(1, 3)
+        for i in range(PAIRS):
+            query_last_pair(1, i)
         project(9)
-        gate_tokens(3, 0, 0)
-        gate_tokens(3, 1, 0)
-        store(2)
+        gate_last(0, 0)
+        gate_last(1, 0)
+        store(5, beside[:, 1])
         finish(8)
-        store(8)
-        quantise_tokens(3, 0)
-        gate_tokens(3, 0, 1)
-        project(10)
-        project(11)
-        project(12)
-        project(14)
+        quantise_last(0)
+        gate_last(0, 1)
+        project(10, 11, 12, 14)
         finish(9)
-        store(9)
-        gate_tokens(3, 1, 1)
+        gate_last(1, 1)
         finish(10)
-        store(10)
-        quantise_tokens(3, 1)
-        finish(11)
-        store(11)
-        finish(12)
-        store(12)
+        quantise_last(1)
+        finish(11, 12)
         project(13)
-        finish(14)
-        store(14)
-        finish(13)
-        store(13)
+        finish(14, 13)
         project(15)
         finish(15)
-        store(15)

@@ -25,7 +25,7 @@ HALF = 512
 WORDS = HALF // 2
 SORTED_BUFS = 6
 RESULT_BUFS = 12
-SORTED_IN_RUN = 1
+SORTED_IN_RUN = 2
 KIN_BUFS = 7
 HANDED_ON = (("x", 1), ("y", 0), ("y", 2))
 LAST = BLOCKS - 1

@@ -24,10 +24,10 @@ PAIRS = 4
 HALF = 512
 WORDS = HALF // 2
 SORTED_BUFS = 6
-RESULT_BUFS = 12
+RESULT_BUFS = 10
 SORTED_IN_RUN = 2
-KIN_BUFS = 7
-HANDED_ON = (("x", 1), ("y", 0), ("y", 2))
+KIN_BUFS = 4
+HANDED_ON = (("x", 0), ("x", 1), ("wq", 3), ("ow", 1), ("x", 3), ("y", 2))
 LAST = BLOCKS - 1
 
 
@@ -42,16 +42,17 @@ def tile_aft_full_pb_kernel(tc, x_bytes, x_scale, wq_w, wq_b, r_aft, out_w, out_
     with ExitStack() as ctx:
         keep = ctx.enter_context(tc.tile_pool(name="keep", bufs=1))
         flow = ctx.enter_context(tc.tile_pool(name="flow", bufs=1))
-        banks = ctx.enter_context(tc.psum_pool(name="banks", bufs=6))
-        gate_banks = ctx.enter_context(tc.psum_pool(name="gate_banks", bufs=2))
+        banks = ctx.enter_context(tc.psum_pool(name="banks", bufs=5))
+        gate_banks = ctx.enter_context(tc.psum_pool(name="gate_banks", bufs=3))
         ctx.enter_context(tc.manual_schedule())
 
         x_mult = keep.tile([P, 2, 4], F32)
-        x_mult_rows = keep.tile([P, D], F32)
         query_bias = keep.tile([P, 2, 4], BF16)
-        out_bias = keep.tile([P, D], BF16)
+        out_bias = [keep.tile([P, HALF], BF16, name="out_bias%d" % c) for c in range(2)]
         identity = keep.tile([P, P], F32)
         one_column = keep.tile([P, 1], F32)
+        ones = keep.tile([P, 1], F32)
+        x_wide = {b: keep.tile([P, J, D], BF16, name="x_wide%d" % b, align_bytes=64) for b in range(2)}
 
         def kept(name, count, shape, dtype):
             return [keep.tile(shape, dtype, name="%s%d" % (name, i), align_bytes=64) for i in range(count)]
@@ -88,8 +89,8 @@ def tile_aft_full_pb_kernel(tc, x_bytes, x_scale, wq_w, wq_b, r_aft, out_w, out_
         def load_ow(i):
             nc.sync.dma_start(out=ow_raw[i][:], in_=ow_hbm[i])
 
-        def load_out_bias():
-            nc.sync.dma_start(out=out_bias[:], in_=out_b.partition_broadcast(P))
+        def load_out_bias(c):
+            nc.sync.dma_start(out=out_bias[c][:], in_=out_b[HALF * c : HALF * (c + 1)].partition_broadcast(P))
 
         def load_query_bias():
             nc.sync.dma_start(out=query_bias[:], in_=wq_b.rearrange("(f p t) -> p f t", p=P, t=4))
@@ -102,34 +103,50 @@ def tile_aft_full_pb_kernel(tc, x_bytes, x_scale, wq_w, wq_b, r_aft, out_w, out_
 
         def rows_of(name, i, s):
             if name == "x":
-                return held["x_wide", i, s][:]
+                return x_wide[i][:, s, :]
             if name == "wq":
                 return wq_rest[i - 2][:, s, :] if i >= 2 else wq_first[2 * i + s][:]
             return (r_raw if name == "r" else ow_raw)[i][:, s, :]
 
         def sort_rows(name, i, s):
             ordered = flow.tile([P, HALF], F32, name="ordered", align_bytes=64, bufs=SORTED_BUFS)
-            held["sorted", name, i, s] = ordered
+            for g in range(2):
+                held["sorted", name, i, s, g] = ordered[:, WORDS * g : WORDS * (g + 1)]
             nc.scalar.copy(
                 out=ordered[:].rearrange("p (g u c e) -> p g c u e", g=2, u=2, e=2),
                 in_=rows_of(name, i, s).bitcast(F32).rearrange("p (g c e u) -> p g c u e", g=2, u=2, e=2),
             )
 
+        def sort_half(b, f):
+            ordered = flow.tile([P, J, WORDS], F32, name="ordered", align_bytes=64, bufs=SORTED_BUFS)
+            for j in range(J):
+                held["sorted", "r", b, j, f] = ordered[:, j]
+            nc.scalar.copy(
+                out=ordered[:].rearrange("p j (u c e) -> p j c u e", u=2, e=2),
+                in_=r_raw[b][:].bitcast(F32)[:, :, WORDS * f : WORDS * (f + 1)].rearrange("p j (c e u) -> p j c u e", u=2, e=2),
+            )
+
         def handed_on(key, shape):
             return flow.tile(shape, F32, name="%s_in%d" % key, align_bytes=64)
 
-        def sort_r_behind(b, key):
-            ordered = handed_on(key, [P, J, HALF])
-            for j in range(J):
-                held["sorted", "r", b, j] = ordered[:, j]
-            nc.gpsimd.tensor_copy(
-                out=ordered[:].bitcast(U32).rearrange("p j (g u c) -> p (j g) u c", g=2, u=2),
-                in_=r_raw[b][:].bitcast(U32).rearrange("p j (g c u) -> p (j g) u c", g=2, u=2),
-            )
+        def sort_behind(key, *banks_of_rows, spare=0):
+            ordered = handed_on(key, [P, len(banks_of_rows) + spare, 2, WORDS])
+            for place, (name, i, s) in enumerate(banks_of_rows):
+                if name == "r":
+                    source = r_raw[i][:].bitcast(U32)[:, :, WORDS * s : WORDS * (s + 1)]
+                else:
+                    source = rows_of(name, i, s).bitcast(U32).rearrange("p (g w) -> p g w", g=2)
+                for part in range(2):
+                    held[("sorted", name, i, part, s) if name == "r" else ("sorted", name, i, s, part)] = ordered[:, place, part]
+                nc.gpsimd.tensor_copy(
+                    out=ordered[:, place].bitcast(U32).rearrange("p a (u c) -> p a u c", u=2),
+                    in_=source.rearrange("p a (c u) -> p a u c", u=2),
+                )
+            return ordered
 
         def words_of(name, i, s, g, u):
-            if ("sorted", name, i, s) in held:
-                return held["sorted", name, i, s][:, WORDS * g + P * u : WORDS * g + P * (u + 1)]
+            if ("sorted", name, i, s, g) in held:
+                return held["sorted", name, i, s, g][:, P * u : P * (u + 1)]
             return rows_of(name, i, s).bitcast(F32)[:, WORDS * g + u : WORDS * (g + 1) : 2]
 
         def kin_tile(key):
@@ -140,6 +157,14 @@ def tile_aft_full_pb_kernel(tc, x_bytes, x_scale, wq_w, wq_b, r_aft, out_w, out_
                     held[key] = flow.tile([P, 2, 4 * TB], BF16, name="kin", align_bytes=64, bufs=KIN_BUFS)
             return held[key]
 
+        def last_tile(j):
+            if ("last", j) not in held:
+                held["last", j] = flow.tile([P, D], BF16, name="last_in%d" % j, align_bytes=64)
+            return held["last", j]
+
+        def handed_on_codes(j):
+            return handed_on(("last", j), [P, HALF])[:]
+
         def turn(name, i, s):
             turned = banks.tile([P, 2, P // 2, 2, 2], F32, name="bank")
             held["turned", name, i, s] = turned
@@ -147,35 +172,50 @@ def tile_aft_full_pb_kernel(tc, x_bytes, x_scale, wq_w, wq_b, r_aft, out_w, out_
                 for u in range(2):
                     nc.tensor.transpose(turned[:, g, :, u, :], words_of(name, i, s, g, u), identity[:])
 
-        def empty(name, i, s, copy):
+        def empty(name, i, s):
             kin_words = kin_tile((name, i))[:].bitcast(F32)
             if name == "wq":
                 kin_words = kin_words[:, s, :].rearrange("p (g w) -> p g w", g=2)
             else:
                 kin_words = kin_words[:, :, WORDS * s : WORDS * (s + 1)]
-            copy(out=kin_words.rearrange("p g (c i u) -> p g c u i", i=2, u=2), in_=held["turned", name, i, s][:])
+            nc.scalar.copy(out=kin_words.rearrange("p g (c i u) -> p g c u i", i=2, u=2), in_=held["turned", name, i, s][:])
 
         def turn_and_empty(name, i, s):
             turn(name, i, s)
-            empty(name, i, s, nc.scalar.copy)
+            empty(name, i, s)
 
-        def spread_scale(g):
-            spread = gate_banks.tile([P, 4, P], F32, name="turned")
-            for t in range(4):
-                nc.tensor.transpose(spread[:, t, :], x_mult[:, g, t : t + 1].to_broadcast([P, P]), identity[:])
-            nc.scalar.copy(
-                out=x_mult_rows[:, HALF * g : HALF * (g + 1)].rearrange("p (m t) -> p m t", t=4),
-                in_=spread[:].rearrange("p t m -> p m t"),
+        def widen_sorted(b, j, g):
+            held["sorted", "x", b, j, g] = x_wide[b][:, j, HALF * g : HALF * (g + 1)].bitcast(F32)
+            nc.vector.tensor_scalar(
+                out=x_wide[b][:, j, HALF * g : HALF * (g + 1)].rearrange("p (u c e) -> p c u e", u=2, e=2),
+                in0=x_raw[b][:, j, HALF * g : HALF * (g + 1)].bitcast(FP8).rearrange("p (c u e) -> p c u e", u=2, e=2),
+                scalar1=ones[:],
+                scalar2=None,
+                op0=MULT,
             )
 
-        def scale_x(b, j, width=D):
-            wide = flow.tile([P, D], BF16, name="x_wide", align_bytes=64, bufs=BLOCKS * J)
-            held["x_wide", b, j] = wide
-            for first in range(0, D, width):
-                part = slice(first, first + width)
-                nc.vector.tensor_tensor(
-                    out=wide[:, part], in0=x_raw[b][:, j, part].bitcast(FP8), in1=x_mult_rows[:, part], op=MULT
-                )
+        def widen(b, key=None):
+            if key:
+                x_wide[b] = flow.tile([P, J, D], BF16, name="%s_in%d" % key, align_bytes=64)
+            if b == LAST:
+                x_wide[b] = keep.tile([P, J, D], BF16, name="x_wide3", align_bytes=64)
+            nc.gpsimd.tensor_copy(out=flat(x_wide[b]), in_=flat(x_raw[b]).bitcast(FP8))
+
+        def turn_half(name, b, g, pool=gate_banks, tag="turned"):
+            turned = pool.tile([P, TB // 2, 2, 2], F32, name=tag)
+            held[name + "_turned", b, g] = turned
+            for j in range(J):
+                pairs = slice(j * P // 2, (j + 1) * P // 2)
+                for u in range(2):
+                    nc.tensor.transpose(turned[:, pairs, u, :], words_of(name, b, j, g, u), identity[:])
+
+        def scale_x(b, g):
+            nc.vector.tensor_tensor(
+                out=kin_tile(("x", b))[:, g, :].rearrange("p (c i u e) -> p c u e i", i=2, u=2, e=2),
+                in0=held["x_turned", b, g][:].bitcast(BF16).rearrange("p c u (i e) -> p c u e i", e=2),
+                in1=x_mult[:, g, :].rearrange("p (c u e i) -> p c u e i", c=1, u=2, i=1).to_broadcast([P, TB // 2, 2, 2, 2]),
+                op=MULT,
+            )
 
         def quantise_x(b):
             quantise(flat(x_codes[b]), flat(x_scales[b]), flat(held["x", b]))
@@ -192,14 +232,6 @@ def tile_aft_full_pb_kernel(tc, x_bytes, x_scale, wq_w, wq_b, r_aft, out_w, out_
             for g in range(2):
                 quantise(ow_codes[i // 2][:, g, columns], ow_scales[i // 2][:, g, columns], held["ow", i][:, g, :])
 
-        def turn_r(b, f):
-            turned = gate_banks.tile([P, TB // 2, 2, 2], F32, name="turned")
-            held["r", b, f] = turned
-            for j in range(J):
-                pairs = slice(j * P // 2, (j + 1) * P // 2)
-                for u in range(2):
-                    nc.tensor.transpose(turned[:, pairs, u, :], words_of("r", b, j, f, u), identity[:])
-
         def query(b, tokens, tiles, sig):
             q = banks.tile([P, len(tiles), tokens.stop - tokens.start], F32, name="bank")
             for place, (f, t) in enumerate(tiles):
@@ -214,6 +246,9 @@ def tile_aft_full_pb_kernel(tc, x_bytes, x_scale, wq_w, wq_b, r_aft, out_w, out_
                         start=(g == 0),
                         stop=(g == 1),
                     )
+            return q, tiles, sig
+
+        def sigmoids(q, tiles, sig):
             for place, (f, t) in enumerate(tiles):
                 nc.scalar.activation(out=sig[:, t, :], in_=q[:, place, :], func=SIGMOID, bias=query_bias[:, f, t : t + 1])
 
@@ -221,22 +256,22 @@ def tile_aft_full_pb_kernel(tc, x_bytes, x_scale, wq_w, wq_b, r_aft, out_w, out_
             return [(i // 2, 2 * (i % 2) + s) for s in range(2)]
 
         def query_pair(b, i):
-            query(b, slice(0, TB), pair_tiles(i), gate_sig[2 * b + i // 2])
+            sigmoids(*query(b, slice(0, TB), pair_tiles(i), gate_sig[2 * b + i // 2]))
 
         def query_block(b):
             for i in range(PAIRS):
                 query_pair(b, i)
 
         def query_last_half(j, f):
-            query(LAST, slice(P * j, P * (j + 1)), [(f, t) for t in range(4)], last_sig[2 * j + f])
+            sigmoids(*query(LAST, slice(P * j, P * (j + 1)), [(f, t) for t in range(4)], last_sig[2 * j + f]))
 
         def query_last_pair(j, i):
-            query(LAST, slice(P * j, P * (j + 1)), pair_tiles(i), last_sig[2 * j + i // 2])
+            sigmoids(*query(LAST, slice(P * j, P * (j + 1)), pair_tiles(i), last_sig[2 * j + i // 2]))
 
         def gate(b, f):
             nc.vector.tensor_tensor(
                 out=kin_tile(("y", b))[:, f, :].rearrange("p (c i u e) -> p c u e i", i=2, u=2, e=2),
-                in0=held["r", b, f][:].bitcast(BF16).rearrange("p c u (i e) -> p c u e i", e=2),
+                in0=held["r_turned", b, f][:].bitcast(BF16).rearrange("p c u (i e) -> p c u e i", e=2),
                 in1=gate_sig[2 * b + f][:].rearrange("p (u e) (c i) -> p c u e i", u=2, i=2),
                 op=MULT,
             )
@@ -244,14 +279,14 @@ def tile_aft_full_pb_kernel(tc, x_bytes, x_scale, wq_w, wq_b, r_aft, out_w, out_
         def gate_last(f, j):
             pairs = slice(j * P // 2, (j + 1) * P // 2)
             nc.vector.tensor_tensor(
-                out=kin_tile(("y", LAST))[:, j, HALF * f : HALF * (f + 1)].rearrange("p (c i u e) -> p c u e i", i=2, u=2, e=2),
-                in0=held["r", LAST, f][:, pairs].bitcast(BF16).rearrange("p c u (i e) -> p c u e i", e=2),
+                out=last_tile(j)[:, HALF * f : HALF * (f + 1)].rearrange("p (c i u e) -> p c u e i", i=2, u=2, e=2),
+                in0=held["r_turned", LAST, f][:, pairs].bitcast(BF16).rearrange("p c u (i e) -> p c u e i", e=2),
                 in1=last_sig[2 * j + f][:].rearrange("p (u e) (c i) -> p c u e i", u=2, i=2),
                 op=MULT,
             )
 
         def quantise_last(j):
-            quantise(y_codes[LAST][:, j, :], y_scales[LAST][:, j, :], held["y", LAST][:, j, :])
+            quantise(y_codes[LAST][:, j, :], y_scales[LAST][:, j, :], last_tile(j)[:])
 
         def y_part(tiles, b, j, g):
             if b == LAST:
@@ -279,7 +314,7 @@ def tile_aft_full_pb_kernel(tc, x_bytes, x_scale, wq_w, wq_b, r_aft, out_w, out_
         def result_and_bias(n):
             c = n // 2 % 2
             result = flow.tile([P, HALF], F32, name="result", align_bytes=64, bufs=RESULT_BUFS)
-            return result[:], out_bias[:, HALF * c : HALF * (c + 1)]
+            return result[:], out_bias[c][:]
 
         def store(n, result):
             b, c, j = n // 4, n // 2 % 2, n % 2
@@ -291,153 +326,178 @@ def tile_aft_full_pb_kernel(tc, x_bytes, x_scale, wq_w, wq_b, r_aft, out_w, out_
                 nc.vector.tensor_tensor(out=result, in0=held["sums", n][:], in1=bias, op=ADD)
                 store(n, result)
 
+        def empty_sums(n):
+            held["emptied", n] = result_and_bias(n)
+            nc.scalar.copy(out=held["emptied", n][0], in_=held["sums", n][:])
+
         def bias_on_gpsimd(n, result):
-            sums, bias = result_and_bias(n)
-            nc.scalar.copy(out=sums, in_=held["sums", n][:])
+            sums, bias = held["emptied", n]
             nc.gpsimd.tensor_tensor(out=result, in0=sums, in1=bias, op=ADD)
 
-        nc.sync.dma_start(out=x_mult[:], in_=x_scale[0, :, :].rearrange("o (g p t) -> p (o g) t", p=P, t=4))
+        nc.gpsimd.memset(ones[:], 1.0)
         nc.gpsimd.memset(one_column[:], 0.0)
         make_identity(nc, identity[:])
         nc.scalar.activation(out=one_column[:], in_=one_column[:], func=SIGMOID)
 
-        rounds = ((("x", 2), ("ow", 0)), (("ow", 1), ("ow", 2)), (("ow", 3), ("x", 3)))
-
-        load_wq_first(0, 0)
         load_x(0)
+        load_wq_first(0, 0)
+        nc.sync.dma_start(out=x_mult[:], in_=x_scale[0, :, :].rearrange("o (g p t) -> p (o g) t", p=P, t=4))
+        load_x(1)
         load_wq_first(0, 1)
         load_wq_first(1, 0)
         load_wq_first(1, 1)
-        load_x(1)
         load_wq(2)
-        load_wq(3)
         load_x(2)
-        load_r(0)
+        load_wq(3)
         load_query_bias()
-        load_ow(0)
+        load_r(0)
         load_x(3)
+        load_ow(0)
         load_r(1)
         load_ow(1)
         load_ow(2)
-        load_r(2)
         load_ow(3)
+        load_out_bias(0)
+        load_r(2)
+        load_out_bias(1)
         load_r(3)
-        load_out_bias()
 
-        spread_scale(0)
-        spread_scale(1)
-        scale_x(0, 0, HALF)
-        scale_x(0, 1)
+        widen_sorted(0, 0, 0)
+        widen_sorted(0, 1, 0)
+        turn_half("x", 0, 0)
+        widen_sorted(0, 0, 1)
+        widen_sorted(0, 1, 1)
+        widen(1)
         turn_and_empty("wq", 0, 0)
+        turn_half("x", 0, 1)
+        scale_x(0, 0)
         turn_and_empty("wq", 0, 1)
+        scale_x(0, 1)
         turn_and_empty("wq", 1, 0)
-        turn_and_empty("x", 0, 0)
-        scale_x(1, 0)
         turn_and_empty("wq", 1, 1)
-        turn_and_empty("x", 0, 1)
         quantise_wq(0)
-        scale_x(1, 1)
         quantise_x(0)
-        for i in range(2, PAIRS):
-            turn_and_empty("wq", i, 0)
-            turn_and_empty("wq", i, 1)
-        turn_and_empty("x", 1, 0)
         quantise_wq(1)
-
-        sort_rows("r", 0, 0)
-        query_pair(0, 0)
+        widen(2, ("x", 0))
+        turn("wq", 2, 0)
+        turn_half("x", 1, 0)
+        turn_half("x", 1, 1)
+        turn("wq", 2, 1)
+        empty("wq", 2, 0)
+        sort_rows("wq", 3, 0)
+        empty("wq", 2, 1)
+        sort_rows("wq", 3, 1)
+        scale_x(1, 0)
+        scale_x(1, 1)
         quantise_wq(2)
-        scale_x(2, 0)
-        quantise_wq(3)
-        scale_x(2, 1)
-        turn_and_empty("x", 1, 1)
-        sort_rows("r", 0, 1)
-
-        def sort_for_round(b):
-            name, i = rounds[b][1]
-            for s in range(2 - SORTED_IN_RUN, 2):
-                sort_rows(name, i, s)
-
-        def run(b, keep_first):
-            (first, i), (second, k) = rounds[b]
-            turn(first, i, 0)
-            if not keep_first:
-                empty(first, i, 0, nc.scalar.copy)
-            turn_r(b, 0)
-            turn_and_empty(first, i, 1)
-            turn_and_empty(second, k, 0)
-            turn_r(b, 1)
-            turn_and_empty(second, k, 1)
-
-        def run_beside_gpsimd(b):
-            run(b, True)
-            empty(*rounds[b][0], 0, nc.vector.tensor_copy)
-            gate(b, 0)
-            gate(b, 1)
-
-        sort_for_round(0)
-        for i in range(1, PAIRS):
-            query_pair(0, i)
-        scale_x(3, 0)
         quantise_x(1)
-        sort_r_behind(1, ("x", 1))
-        scale_x(3, 1)
-        run_beside_gpsimd(0)
-
-        sort_for_round(1)
-        query_block(1)
+        sort_behind(("x", 1), ("ow", 0, 0), ("ow", 0, 1), ("r", 1, 0))
+        sort_rows("r", 0, 0)
+        sort_rows("r", 0, 1)
+        query_pair(0, 0)
+        waiting = query(0, slice(0, TB), pair_tiles(1), gate_sig[0])
+        turn_half("x", 2, 0)
+        turn_and_empty("wq", 3, 0)
+        turn_and_empty("wq", 3, 1)
+        turn_half("x", 2, 1)
+        turn_half("r", 0, 0)
+        sigmoids(*waiting)
+        scale_x(2, 0)
+        scale_x(2, 1)
+        quantise_wq(3)
+        quantise_x(2)
+        sort_behind(("wq", 3), ("ow", 1, 0), ("ow", 1, 1))
+        widen(3)
+        query_pair(0, 2)
+        query_pair(1, 0)
+        query_pair(1, 1)
+        query_pair(0, 3)
+        gate(0, 0)
+        sort_half(1, 1)
+        turn_half("r", 1, 0)
+        turn_half("r", 0, 1)
+        turn_and_empty("ow", 0, 0)
+        turn_and_empty("ow", 0, 1)
+        turn_and_empty("ow", 1, 0)
+        turn_and_empty("ow", 1, 1)
+        gate(1, 0)
+        turn_half("r", 1, 1)
+        gate(0, 1)
         quantise_ow(0)
         quantise_y(0)
-        sort_r_behind(2, ("y", 0))
-        quantise_x(2)
-        run_beside_gpsimd(1)
-
-        sort_for_round(2)
-        query_block(2)
         quantise_ow(1)
-        quantise_y(1)
-        quantise_ow(2)
+        sort_behind(("ow", 1), ("ow", 2, 0), ("ow", 2, 1), ("r", 2, 0))
+        query_pair(1, 2)
+        query_pair(1, 3)
+        query_pair(2, 0)
+        query_pair(2, 1)
+        gate(1, 1)
+        turn_half("x", 3, 0)
+        turn_half("x", 3, 1)
+        scale_x(3, 0)
+        scale_x(3, 1)
+        sort_rows("ow", 3, 0)
         project(0, 1)
-        finish(0, 1)
-        run(2, False)
+        empty_sums(0)
+        sort_rows("ow", 3, 1)
+        first = flow.tile([P, HALF], F32, name="first", align_bytes=64)
+        bias_on_gpsimd(0, first[:])
+        store(0, first[:])
+        query_pair(2, 2)
+        query_pair(2, 3)
+        finish(1)
+        quantise_y(1)
+        quantise_x(3)
+
+        turn_half("r", 2, 0)
+        turn_and_empty("ow", 2, 0)
+        turn_and_empty("ow", 2, 1)
+        turn_and_empty("ow", 3, 0)
+        turn_and_empty("ow", 3, 1)
+        turn_half("r", 2, 1)
+        sort_behind(("x", 3), ("r", 3, 0), ("r", 3, 1))
         gate(2, 0)
-        quantise_ow(3)
         gate(2, 1)
-        sort_rows("r", LAST, 0)
-        sort_rows("r", LAST, 1)
-
-        quantise_x(LAST)
+        project(4, 5)
+        empty_sums(4)
+        empty_sums(5)
+        quantise_ow(2)
+        quantise_ow(3)
         quantise_y(2)
-        beside = handed_on(("y", 2), [P, 2, HALF])
-        project(4)
-        bias_on_gpsimd(4, beside[:, 0])
-        project(5)
-        bias_on_gpsimd(5, beside[:, 1])
-        project(2, 3, 6, 7)
-        finish(2, 3, 6, 7)
-        store(4, beside[:, 0])
-
+        second = handed_on(("y", 2), [P, 2, HALF])
+        bias_on_gpsimd(4, second[:, 0])
+        bias_on_gpsimd(5, second[:, 1])
         query_last_half(0, 0)
         query_last_half(0, 1)
-        turn_r(LAST, 0)
-        turn_r(LAST, 1)
-        project(8)
-        for i in range(PAIRS):
-            query_last_pair(1, i)
-        project(9)
+        turn_half("r", 3, 0)
+        turn_half("r", 3, 1)
+        project(2, 3, 6, 7, 8)
         gate_last(0, 0)
         gate_last(1, 0)
-        store(5, beside[:, 1])
-        finish(8)
+        store(4, second[:, 0])
+        finish(2)
+        store(5, second[:, 1])
+        finish(3)
+        empty_sums(6)
+        empty_sums(8)
         quantise_last(0)
+        fourth = handed_on(("last", 0), [P, 2, HALF])
+        bias_on_gpsimd(6, fourth[:, 0])
+        bias_on_gpsimd(8, fourth[:, 1])
+        finish(7)
+        for i in range(PAIRS):
+            query_last_pair(1, i)
+        project(9, 10, 11, 12, 14)
         gate_last(0, 1)
-        project(10, 11, 12, 14)
-        finish(9)
+        store(6, fourth[:, 0])
         gate_last(1, 1)
-        finish(10)
+        finish(9)
+        empty_sums(10)
         quantise_last(1)
+        store(8, fourth[:, 1])
+        fifth = handed_on_codes(1)
+        bias_on_gpsimd(10, fifth)
         finish(11, 12)
-        project(13)
-        finish(14, 13)
-        project(15)
-        finish(15)
+        project(13, 15)
+        store(10, fifth)
+        finish(14, 13, 15)

@@ -70,8 +70,8 @@ def tile_aft_full_pb_kernel(tc, x_bytes, x_scale, wq_w, wq_b, r_aft, out_w, out_
         ow_scales = kept("ow_scales", 2, [P, 2, HALF], U8)
         y_codes = kept("y_codes", BLOCKS, [P, 2, TB], U32)
         y_scales = kept("y_scales", BLOCKS, [P, 2, TB], U8)
-        gate_sig = kept("gate_sig", 2 * LAST, [P, 4, TB], F32)
-        last_sig = kept("last_sig", 2 * J, [P, 4, P], F32)
+        gate_sig = kept("gate_sig", 2 * LAST, [P, TB // 4, 4, 4], F32)
+        last_sig = kept("last_sig", 2 * J, [P, P // 4, 4, 4], F32)
         held = {}
 
         def load_x(b):
@@ -202,10 +202,11 @@ def tile_aft_full_pb_kernel(tc, x_bytes, x_scale, wq_w, wq_b, r_aft, out_w, out_
             nc.gpsimd.tensor_copy(out=flat(x_wide[b]), in_=flat(x_raw[b]).bitcast(FP8))
 
         def turn_half(name, b, g, pool=gate_banks, tag="turned"):
-            turned = pool.tile([P, TB // 2, 2, 2], F32, name=tag)
+            run = 4 if name == "r" else 2
+            turned = pool.tile([P, TB // run, 2, run], F32, name=tag)
             held[name + "_turned", b, g] = turned
             for j in range(J):
-                pairs = slice(j * P // 2, (j + 1) * P // 2)
+                pairs = slice(j * P // run, (j + 1) * P // run)
                 for u in range(2):
                     nc.tensor.transpose(turned[:, pairs, u, :], words_of(name, b, j, g, u), identity[:])
 
@@ -250,7 +251,12 @@ def tile_aft_full_pb_kernel(tc, x_bytes, x_scale, wq_w, wq_b, r_aft, out_w, out_
 
         def sigmoids(q, tiles, sig):
             for place, (f, t) in enumerate(tiles):
-                nc.scalar.activation(out=sig[:, t, :], in_=q[:, place, :], func=SIGMOID, bias=query_bias[:, f, t : t + 1])
+                nc.scalar.activation(
+                    out=sig[:, :, t, :],
+                    in_=q[:, place, :].rearrange("p (c i) -> p c i", i=4),
+                    func=SIGMOID,
+                    bias=query_bias[:, f, t : t + 1],
+                )
 
         def pair_tiles(i):
             return [(i // 2, 2 * (i % 2) + s) for s in range(2)]
@@ -270,18 +276,18 @@ def tile_aft_full_pb_kernel(tc, x_bytes, x_scale, wq_w, wq_b, r_aft, out_w, out_
 
         def gate(b, f):
             nc.vector.tensor_tensor(
-                out=kin_tile(("y", b))[:, f, :].rearrange("p (c i u e) -> p c u e i", i=2, u=2, e=2),
+                out=kin_tile(("y", b))[:, f, :].rearrange("p (c i u e) -> p c u e i", i=4, u=2, e=2),
                 in0=held["r_turned", b, f][:].bitcast(BF16).rearrange("p c u (i e) -> p c u e i", e=2),
-                in1=gate_sig[2 * b + f][:].rearrange("p (u e) (c i) -> p c u e i", u=2, i=2),
+                in1=gate_sig[2 * b + f][:].rearrange("p c (u e) i -> p c u e i", u=2),
                 op=MULT,
             )
 
         def gate_last(f, j):
-            pairs = slice(j * P // 2, (j + 1) * P // 2)
+            pairs = slice(j * P // 4, (j + 1) * P // 4)
             nc.vector.tensor_tensor(
-                out=last_tile(j)[:, HALF * f : HALF * (f + 1)].rearrange("p (c i u e) -> p c u e i", i=2, u=2, e=2),
+                out=last_tile(j)[:, HALF * f : HALF * (f + 1)].rearrange("p (c i u e) -> p c u e i", i=4, u=2, e=2),
                 in0=held["r_turned", LAST, f][:, pairs].bitcast(BF16).rearrange("p c u (i e) -> p c u e i", e=2),
-                in1=last_sig[2 * j + f][:].rearrange("p (u e) (c i) -> p c u e i", u=2, i=2),
+                in1=last_sig[2 * j + f][:].rearrange("p c (u e) i -> p c u e i", u=2),
                 op=MULT,
             )
 

@@ -27,7 +27,7 @@ SORTED_BUFS = 6
 RESULT_BUFS = 10
 SORTED_IN_RUN = 2
 KIN_BUFS = 4
-HANDED_ON = (("x", 0), ("x", 1), ("wq", 3), ("ow", 1), ("x", 3), ("y", 2))
+HANDED_ON = (("wq", 0), ("wq", 2), ("wq", 3), ("ow", 1), ("y", 1), ("x", 3), ("y", 2))
 LAST = BLOCKS - 1
 
 
@@ -52,12 +52,13 @@ def tile_aft_full_pb_kernel(tc, x_bytes, x_scale, wq_w, wq_b, r_aft, out_w, out_
         identity = keep.tile([P, P], F32)
         one_column = keep.tile([P, 1], F32)
         ones = keep.tile([P, 1], F32)
-        x_wide = {b: keep.tile([P, J, D], BF16, name="x_wide%d" % b, align_bytes=64) for b in range(2)}
+        x_wide = {b: keep.tile([P, J, D], BF16, name="x_wide%d" % b, align_bytes=64) for b in range(1)}
 
         def kept(name, count, shape, dtype):
             return [keep.tile(shape, dtype, name="%s%d" % (name, i), align_bytes=64) for i in range(count)]
 
-        x_raw = kept("x_raw", BLOCKS, [P, J, D], U8)
+        x_raw = [None] + kept("x_raw", LAST, [P, J, D], U8)
+        x_first = kept("x_first", J, [P, D], U8)
         r_raw = kept("r_raw", BLOCKS, [P, J, D], BF16)
         wq_first = kept("wq_first", 4, [P, D], BF16)
         wq_rest = kept("wq_rest", PAIRS - 2, [P, 2, D], BF16)
@@ -76,6 +77,9 @@ def tile_aft_full_pb_kernel(tc, x_bytes, x_scale, wq_w, wq_b, r_aft, out_w, out_
 
         def load_x(b):
             nc.sync.dma_start(out=x_raw[b][:], in_=x_hbm[b])
+
+        def load_x_first(j):
+            nc.sync.dma_start(out=x_first[j][:], in_=x_hbm[0][:, j, :])
 
         def load_r(b):
             nc.sync.dma_start(out=r_raw[b][:], in_=r_hbm[b])
@@ -103,7 +107,7 @@ def tile_aft_full_pb_kernel(tc, x_bytes, x_scale, wq_w, wq_b, r_aft, out_w, out_
 
         def rows_of(name, i, s):
             if name == "x":
-                return x_wide[i][:, s, :]
+                return x_wide[i, s, "tile"][:] if (i, s, "tile") in x_wide else x_wide[i][:, s, :]
             if name == "wq":
                 return wq_rest[i - 2][:, s, :] if i >= 2 else wq_first[2 * i + s][:]
             return (r_raw if name == "r" else ow_raw)[i][:, s, :]
@@ -144,9 +148,25 @@ def tile_aft_full_pb_kernel(tc, x_bytes, x_scale, wq_w, wq_b, r_aft, out_w, out_
                 )
             return ordered
 
+        def sort_pair(ordered, name, i):
+            for s in range(2):
+                for g in range(2):
+                    held["sorted", name, i, s, g] = ordered[:, s, WORDS * g : WORDS * (g + 1)]
+            nc.gpsimd.tensor_copy(
+                out=ordered[:].bitcast(U32).rearrange("p s (g u c) -> p (s g) u c", g=2, u=2),
+                in_=(r_raw if name == "r" else ow_raw)[i][:].bitcast(U32).rearrange("p s (g c u) -> p (s g) u c", g=2, u=2),
+            )
+
+        def widen_tile(b, j, copy, key=None):
+            name = "%s_in%d" % key if key else "x_wide%d_%d" % (b, j)
+            x_wide[b, j, "tile"] = flow.tile([P, D], BF16, name=name, align_bytes=64)
+            copy(out=x_wide[b, j, "tile"][:], in_=x_raw[b][:, j, :].bitcast(FP8))
+
         def words_of(name, i, s, g, u):
             if ("sorted", name, i, s, g) in held:
                 return held["sorted", name, i, s, g][:, P * u : P * (u + 1)]
+            if name == "x" and (i, g) in x_wide:
+                return x_wide[i, g][:, s, :].bitcast(F32)[:, u::2]
             return rows_of(name, i, s).bitcast(F32)[:, WORDS * g + u : WORDS * (g + 1) : 2]
 
         def kin_tile(key):
@@ -188,7 +208,7 @@ def tile_aft_full_pb_kernel(tc, x_bytes, x_scale, wq_w, wq_b, r_aft, out_w, out_
             held["sorted", "x", b, j, g] = x_wide[b][:, j, HALF * g : HALF * (g + 1)].bitcast(F32)
             nc.vector.tensor_scalar(
                 out=x_wide[b][:, j, HALF * g : HALF * (g + 1)].rearrange("p (u c e) -> p c u e", u=2, e=2),
-                in0=x_raw[b][:, j, HALF * g : HALF * (g + 1)].bitcast(FP8).rearrange("p (c u e) -> p c u e", u=2, e=2),
+                in0=x_first[j][:, HALF * g : HALF * (g + 1)].bitcast(FP8).rearrange("p (c u e) -> p c u e", u=2, e=2),
                 scalar1=ones[:],
                 scalar2=None,
                 op0=MULT,
@@ -200,6 +220,11 @@ def tile_aft_full_pb_kernel(tc, x_bytes, x_scale, wq_w, wq_b, r_aft, out_w, out_
             if b == LAST:
                 x_wide[b] = keep.tile([P, J, D], BF16, name="x_wide3", align_bytes=64)
             nc.gpsimd.tensor_copy(out=flat(x_wide[b]), in_=flat(x_raw[b]).bitcast(FP8))
+
+        def widen_half(b, g, copy):
+            for j in range(J):
+                part = slice(HALF * g, HALF * (g + 1))
+                copy(out=x_wide[b, g][:, j, :], in_=x_raw[b][:, j, part].bitcast(FP8))
 
         def turn_half(name, b, g, pool=gate_banks, tag="turned"):
             run = 4 if name == "r" else 2
@@ -217,6 +242,20 @@ def tile_aft_full_pb_kernel(tc, x_bytes, x_scale, wq_w, wq_b, r_aft, out_w, out_
                 in1=x_mult[:, g, :].rearrange("p (c u e i) -> p c u e i", c=1, u=2, i=1).to_broadcast([P, TB // 2, 2, 2, 2]),
                 op=MULT,
             )
+
+        def first_tokens(j):
+            for g in range(2):
+                widen_sorted(0, j, g)
+            turn("x", 0, j)
+
+        def scale_first(j):
+            for g in range(2):
+                nc.vector.tensor_tensor(
+                    out=kin_tile(("x", 0))[:, g, HALF * j : HALF * (j + 1)].rearrange("p (c i u e) -> p c u e i", i=2, u=2, e=2),
+                    in0=held["turned", "x", 0, j][:, g].bitcast(BF16).rearrange("p c u (i e) -> p c u e i", e=2),
+                    in1=x_mult[:, g, :].rearrange("p (c u e i) -> p c u e i", c=1, u=2, i=1).to_broadcast([P, P // 2, 2, 2, 2]),
+                    op=MULT,
+                )
 
         def quantise_x(b):
             quantise(flat(x_codes[b]), flat(x_scales[b]), flat(held["x", b]))
@@ -326,6 +365,14 @@ def tile_aft_full_pb_kernel(tc, x_bytes, x_scale, wq_w, wq_b, r_aft, out_w, out_
             b, c, j = n // 4, n // 2 % 2, n % 2
             nc.sync.dma_start(out=out_hbm[b][:, j, HALF * c : HALF * (c + 1)], in_=result)
 
+        def finish_by_halves(n):
+            b, c, j = n // 4, n // 2 % 2, n % 2
+            for h in range(2):
+                part = slice(TB * h, TB * (h + 1))
+                result = flow.tile([P, TB], F32, name="result", align_bytes=64, bufs=RESULT_BUFS)
+                nc.vector.tensor_tensor(out=result[:], in0=held["sums", n][:, part], in1=out_bias[c][:, part], op=ADD)
+                nc.sync.dma_start(out=out_hbm[b][:, j, HALF * c + TB * h : HALF * c + TB * (h + 1)], in_=result[:])
+
         def finish(*tiles):
             for n in tiles:
                 result, bias = result_and_bias(n)
@@ -345,9 +392,10 @@ def tile_aft_full_pb_kernel(tc, x_bytes, x_scale, wq_w, wq_b, r_aft, out_w, out_
         make_identity(nc, identity[:])
         nc.scalar.activation(out=one_column[:], in_=one_column[:], func=SIGMOID)
 
-        load_x(0)
-        load_wq_first(0, 0)
+        load_x_first(0)
+        load_x_first(1)
         nc.sync.dma_start(out=x_mult[:], in_=x_scale[0, :, :].rearrange("o (g p t) -> p (o g) t", p=P, t=4))
+        load_wq_first(0, 0)
         load_x(1)
         load_wq_first(0, 1)
         load_wq_first(1, 0)
@@ -368,26 +416,24 @@ def tile_aft_full_pb_kernel(tc, x_bytes, x_scale, wq_w, wq_b, r_aft, out_w, out_
         load_out_bias(1)
         load_r(3)
 
-        widen_sorted(0, 0, 0)
-        widen_sorted(0, 1, 0)
-        turn_half("x", 0, 0)
-        widen_sorted(0, 0, 1)
-        widen_sorted(0, 1, 1)
-        widen(1)
+        first_tokens(0)
+        first_tokens(1)
+        widen_tile(1, 0, nc.scalar.copy)
+        widen_tile(1, 1, nc.gpsimd.tensor_copy)
+        scale_first(0)
         turn_and_empty("wq", 0, 0)
-        turn_half("x", 0, 1)
-        scale_x(0, 0)
+        scale_first(1)
         turn_and_empty("wq", 0, 1)
-        scale_x(0, 1)
         turn_and_empty("wq", 1, 0)
         turn_and_empty("wq", 1, 1)
-        quantise_wq(0)
         quantise_x(0)
+        quantise_wq(0)
         quantise_wq(1)
-        widen(2, ("x", 0))
-        turn("wq", 2, 0)
+        widen_tile(2, 0, nc.scalar.copy)
+        widen_tile(2, 1, nc.gpsimd.tensor_copy, ("wq", 0))
         turn_half("x", 1, 0)
         turn_half("x", 1, 1)
+        turn("wq", 2, 0)
         turn("wq", 2, 1)
         empty("wq", 2, 0)
         sort_rows("wq", 3, 0)
@@ -395,9 +441,9 @@ def tile_aft_full_pb_kernel(tc, x_bytes, x_scale, wq_w, wq_b, r_aft, out_w, out_
         sort_rows("wq", 3, 1)
         scale_x(1, 0)
         scale_x(1, 1)
-        quantise_wq(2)
         quantise_x(1)
-        sort_behind(("x", 1), ("ow", 0, 0), ("ow", 0, 1), ("r", 1, 0))
+        quantise_wq(2)
+        sort_pair(handed_on(("wq", 2), [P, 2, HALF]), "ow", 0)
         sort_rows("r", 0, 0)
         sort_rows("r", 0, 1)
         query_pair(0, 0)
@@ -412,14 +458,13 @@ def tile_aft_full_pb_kernel(tc, x_bytes, x_scale, wq_w, wq_b, r_aft, out_w, out_
         scale_x(2, 1)
         quantise_wq(3)
         quantise_x(2)
-        sort_behind(("wq", 3), ("ow", 1, 0), ("ow", 1, 1))
+        sort_pair(handed_on(("wq", 3), [P, 2, HALF]), "ow", 1)
         widen(3)
         query_pair(0, 2)
         query_pair(1, 0)
         query_pair(1, 1)
         query_pair(0, 3)
         gate(0, 0)
-        sort_half(1, 1)
         turn_half("r", 1, 0)
         turn_half("r", 0, 1)
         turn_and_empty("ow", 0, 0)
@@ -432,78 +477,81 @@ def tile_aft_full_pb_kernel(tc, x_bytes, x_scale, wq_w, wq_b, r_aft, out_w, out_
         quantise_ow(0)
         quantise_y(0)
         quantise_ow(1)
-        sort_behind(("ow", 1), ("ow", 2, 0), ("ow", 2, 1), ("r", 2, 0))
+
+        sort_pair(handed_on(("ow", 1), [P, 2, HALF]), "ow", 2)
         query_pair(1, 2)
         query_pair(1, 3)
         query_pair(2, 0)
         query_pair(2, 1)
         gate(1, 1)
-        turn_half("x", 3, 0)
-        turn_half("x", 3, 1)
-        scale_x(3, 0)
-        scale_x(3, 1)
         sort_rows("ow", 3, 0)
         project(0, 1)
-        empty_sums(0)
+        empty_sums(1)
         sort_rows("ow", 3, 1)
-        first = flow.tile([P, HALF], F32, name="first", align_bytes=64)
-        bias_on_gpsimd(0, first[:])
-        store(0, first[:])
-        query_pair(2, 2)
-        query_pair(2, 3)
-        finish(1)
+        finish(0)
         quantise_y(1)
-        quantise_x(3)
-
-        turn_half("r", 2, 0)
+        first = handed_on(("y", 1), [P, HALF])
+        bias_on_gpsimd(1, first[:])
+        turn_half("x", 3, 0)
+        turn_half("x", 3, 1)
         turn_and_empty("ow", 2, 0)
         turn_and_empty("ow", 2, 1)
         turn_and_empty("ow", 3, 0)
         turn_and_empty("ow", 3, 1)
-        turn_half("r", 2, 1)
-        sort_behind(("x", 3), ("r", 3, 0), ("r", 3, 1))
-        gate(2, 0)
-        gate(2, 1)
-        project(4, 5)
-        empty_sums(4)
-        empty_sums(5)
+        scale_x(3, 0)
+        scale_x(3, 1)
+        store(1, first[:])
         quantise_ow(2)
+        quantise_x(3)
         quantise_ow(3)
+        project(4, 5)
+        sort_half(2, 0)
+        sort_half(2, 1)
+        sort_pair(handed_on(("x", 3), [P, 2, HALF]), "r", 3)
+        query_pair(2, 2)
+        query_pair(2, 3)
+        empty_sums(4)
+        second = flow.tile([P, HALF], F32, name="second", align_bytes=64)
+        bias_on_gpsimd(4, second[:])
+        turn_half("r", 2, 0)
+        turn_half("r", 2, 1)
+        finish(5)
+        project(2, 3)
+        empty_sums(2)
+        gate(2, 0)
+        store(4, second[:])
+        gate(2, 1)
+        finish(3)
         quantise_y(2)
-        second = handed_on(("y", 2), [P, 2, HALF])
-        bias_on_gpsimd(4, second[:, 0])
-        bias_on_gpsimd(5, second[:, 1])
+        third = handed_on(("y", 2), [P, HALF])
+        bias_on_gpsimd(2, third[:])
         query_last_half(0, 0)
         query_last_half(0, 1)
         turn_half("r", 3, 0)
         turn_half("r", 3, 1)
-        project(2, 3, 6, 7, 8)
+        project(6, 7, 8, 9)
+        empty_sums(6)
         gate_last(0, 0)
         gate_last(1, 0)
-        store(4, second[:, 0])
-        finish(2)
-        store(5, second[:, 1])
-        finish(3)
-        empty_sums(6)
+        finish(7)
         empty_sums(8)
         quantise_last(0)
+        store(2, third[:])
         fourth = handed_on(("last", 0), [P, 2, HALF])
         bias_on_gpsimd(6, fourth[:, 0])
         bias_on_gpsimd(8, fourth[:, 1])
-        finish(7)
+        finish(9)
         for i in range(PAIRS):
             query_last_pair(1, i)
-        project(9, 10, 11, 12, 14)
+        project(10, 11, 12, 14)
         gate_last(0, 1)
         store(6, fourth[:, 0])
+        finish(10)
         gate_last(1, 1)
-        finish(9)
-        empty_sums(10)
-        quantise_last(1)
         store(8, fourth[:, 1])
-        fifth = handed_on_codes(1)
-        bias_on_gpsimd(10, fifth)
-        finish(11, 12)
+        finish(11)
+        quantise_last(1)
+        finish(12, 14)
         project(13, 15)
-        store(10, fifth)
-        finish(14, 13, 15)
+        finish(13)
+        finish_by_halves(15)

@@ -27,7 +27,7 @@ SORTED_BUFS = 6
 RESULT_BUFS = 10
 SORTED_IN_RUN = 2
 KIN_BUFS = 4
-HANDED_ON = (("wq", 0), ("wq", 2), ("wq", 3), ("ow", 1), ("y", 1), ("x", 3), ("y", 2))
+HANDED_ON = (("wq", 0), ("wq", 2), ("wq", 3), ("y", 0), ("y", 1), ("ow", 3), ("y", 2))
 LAST = BLOCKS - 1
 
 
@@ -51,7 +51,6 @@ def tile_aft_full_pb_kernel(tc, x_bytes, x_scale, wq_w, wq_b, r_aft, out_w, out_
         out_bias = [keep.tile([P, HALF], BF16, name="out_bias%d" % c) for c in range(2)]
         identity = keep.tile([P, P], F32)
         one_column = keep.tile([P, 1], F32)
-        ones = keep.tile([P, 1], F32)
         x_wide = {b: keep.tile([P, J, D], BF16, name="x_wide%d" % b, align_bytes=64) for b in range(1)}
 
         def kept(name, count, shape, dtype):
@@ -192,27 +191,17 @@ def tile_aft_full_pb_kernel(tc, x_bytes, x_scale, wq_w, wq_b, r_aft, out_w, out_
                 for u in range(2):
                     nc.tensor.transpose(turned[:, g, :, u, :], words_of(name, i, s, g, u), identity[:])
 
-        def empty(name, i, s):
+        def empty(name, i, s, copy=nc.scalar.copy):
             kin_words = kin_tile((name, i))[:].bitcast(F32)
             if name == "wq":
                 kin_words = kin_words[:, s, :].rearrange("p (g w) -> p g w", g=2)
             else:
                 kin_words = kin_words[:, :, WORDS * s : WORDS * (s + 1)]
-            nc.scalar.copy(out=kin_words.rearrange("p g (c i u) -> p g c u i", i=2, u=2), in_=held["turned", name, i, s][:])
+            copy(out=kin_words.rearrange("p g (c i u) -> p g c u i", i=2, u=2), in_=held["turned", name, i, s][:])
 
         def turn_and_empty(name, i, s):
             turn(name, i, s)
             empty(name, i, s)
-
-        def widen_sorted(b, j, g):
-            held["sorted", "x", b, j, g] = x_wide[b][:, j, HALF * g : HALF * (g + 1)].bitcast(F32)
-            nc.vector.tensor_scalar(
-                out=x_wide[b][:, j, HALF * g : HALF * (g + 1)].rearrange("p (u c e) -> p c u e", u=2, e=2),
-                in0=x_first[j][:, HALF * g : HALF * (g + 1)].bitcast(FP8).rearrange("p (c u e) -> p c u e", u=2, e=2),
-                scalar1=ones[:],
-                scalar2=None,
-                op0=MULT,
-            )
 
         def widen(b, key=None):
             if key:
@@ -243,10 +232,10 @@ def tile_aft_full_pb_kernel(tc, x_bytes, x_scale, wq_w, wq_b, r_aft, out_w, out_
                 op=MULT,
             )
 
-        def first_tokens(j):
-            for g in range(2):
-                widen_sorted(0, j, g)
-            turn("x", 0, j)
+        def widen_first(j, copy, width):
+            for first in range(0, D, width):
+                part = slice(first, first + width)
+                copy(out=x_wide[0][:, j, part], in_=x_first[j][:, part].bitcast(FP8))
 
         def scale_first(j):
             for g in range(2):
@@ -387,7 +376,6 @@ def tile_aft_full_pb_kernel(tc, x_bytes, x_scale, wq_w, wq_b, r_aft, out_w, out_
             sums, bias = held["emptied", n]
             nc.gpsimd.tensor_tensor(out=result, in0=sums, in1=bias, op=ADD)
 
-        nc.gpsimd.memset(ones[:], 1.0)
         nc.gpsimd.memset(one_column[:], 0.0)
         make_identity(nc, identity[:])
         nc.scalar.activation(out=one_column[:], in_=one_column[:], func=SIGMOID)
@@ -404,8 +392,8 @@ def tile_aft_full_pb_kernel(tc, x_bytes, x_scale, wq_w, wq_b, r_aft, out_w, out_
         load_x(2)
         load_wq(3)
         load_query_bias()
-        load_r(0)
         load_x(3)
+        load_r(0)
         load_ow(0)
         load_r(1)
         load_ow(1)
@@ -416,12 +404,14 @@ def tile_aft_full_pb_kernel(tc, x_bytes, x_scale, wq_w, wq_b, r_aft, out_w, out_
         load_out_bias(1)
         load_r(3)
 
-        first_tokens(0)
-        first_tokens(1)
+        widen_first(0, nc.vector.tensor_copy, HALF)
+        widen_first(1, nc.scalar.copy, D)
         widen_tile(1, 0, nc.scalar.copy)
         widen_tile(1, 1, nc.gpsimd.tensor_copy)
+        turn("x", 0, 0)
         scale_first(0)
         turn_and_empty("wq", 0, 0)
+        turn("x", 0, 1)
         scale_first(1)
         turn_and_empty("wq", 0, 1)
         turn_and_empty("wq", 1, 0)
@@ -465,33 +455,34 @@ def tile_aft_full_pb_kernel(tc, x_bytes, x_scale, wq_w, wq_b, r_aft, out_w, out_
         query_pair(1, 1)
         query_pair(0, 3)
         gate(0, 0)
+        sort_half(1, 1)
         turn_half("r", 1, 0)
         turn_half("r", 0, 1)
         turn_and_empty("ow", 0, 0)
         turn_and_empty("ow", 0, 1)
         turn_and_empty("ow", 1, 0)
-        turn_and_empty("ow", 1, 1)
+        turn("ow", 1, 1)
         gate(1, 0)
         turn_half("r", 1, 1)
         gate(0, 1)
+        empty("ow", 1, 1, nc.vector.tensor_copy)
         quantise_ow(0)
         quantise_y(0)
         quantise_ow(1)
 
-        sort_pair(handed_on(("ow", 1), [P, 2, HALF]), "ow", 2)
+        sort_pair(handed_on(("y", 0), [P, 2, HALF]), "ow", 2)
         query_pair(1, 2)
         query_pair(1, 3)
         query_pair(2, 0)
         query_pair(2, 1)
         gate(1, 1)
         sort_rows("ow", 3, 0)
+        query_pair(2, 2)
         project(0, 1)
-        empty_sums(1)
         sort_rows("ow", 3, 1)
-        finish(0)
+        finish(0, 1)
         quantise_y(1)
-        first = handed_on(("y", 1), [P, HALF])
-        bias_on_gpsimd(1, first[:])
+        sort_pair(handed_on(("y", 1), [P, 2, HALF]), "r", 2)
         turn_half("x", 3, 0)
         turn_half("x", 3, 1)
         turn_and_empty("ow", 2, 0)
@@ -500,27 +491,26 @@ def tile_aft_full_pb_kernel(tc, x_bytes, x_scale, wq_w, wq_b, r_aft, out_w, out_
         turn_and_empty("ow", 3, 1)
         scale_x(3, 0)
         scale_x(3, 1)
-        store(1, first[:])
         quantise_ow(2)
-        quantise_x(3)
         quantise_ow(3)
+        quantise_x(3)
         project(4, 5)
-        sort_half(2, 0)
-        sort_half(2, 1)
-        sort_pair(handed_on(("x", 3), [P, 2, HALF]), "r", 3)
-        query_pair(2, 2)
-        query_pair(2, 3)
         empty_sums(4)
-        second = flow.tile([P, HALF], F32, name="second", align_bytes=64)
-        bias_on_gpsimd(4, second[:])
+        query_pair(2, 3)
+        empty_sums(5)
+        second = handed_on(("ow", 3), [P, 2, HALF])
+        bias_on_gpsimd(4, second[:, 0])
+        bias_on_gpsimd(5, second[:, 1])
+        sort_rows("r", 3, 0)
         turn_half("r", 2, 0)
         turn_half("r", 2, 1)
-        finish(5)
         project(2, 3)
         empty_sums(2)
+        sort_rows("r", 3, 1)
         gate(2, 0)
-        store(4, second[:])
+        store(4, second[:, 0])
         gate(2, 1)
+        store(5, second[:, 1])
         finish(3)
         quantise_y(2)
         third = handed_on(("y", 2), [P, HALF])
@@ -534,21 +524,18 @@ def tile_aft_full_pb_kernel(tc, x_bytes, x_scale, wq_w, wq_b, r_aft, out_w, out_
         gate_last(0, 0)
         gate_last(1, 0)
         finish(7)
-        empty_sums(8)
         quantise_last(0)
         store(2, third[:])
-        fourth = handed_on(("last", 0), [P, 2, HALF])
-        bias_on_gpsimd(6, fourth[:, 0])
-        bias_on_gpsimd(8, fourth[:, 1])
-        finish(9)
+        fourth = handed_on(("last", 0), [P, HALF])
+        bias_on_gpsimd(6, fourth[:])
+        finish(8, 9)
         for i in range(PAIRS):
             query_last_pair(1, i)
         project(10, 11, 12, 14)
         gate_last(0, 1)
-        store(6, fourth[:, 0])
+        store(6, fourth[:])
         finish(10)
         gate_last(1, 1)
-        store(8, fourth[:, 1])
         finish(11)
         quantise_last(1)
         finish(12, 14)

@@ -215,36 +215,47 @@ def tile_aft_full_pb_kernel(tc, x_bytes, x_scale, wq_w, wq_b, r_aft, out_w, out_
                 part = slice(HALF * g, HALF * (g + 1))
                 copy(out=x_wide[b, g][:, j, :], in_=x_raw[b][:, j, part].bitcast(FP8))
 
-        def turn_half(name, b, g, pool=gate_banks, tag="turned"):
-            run = 4 if name == "r" else 2
-            turned = pool.tile([P, TB // run, 2, run], F32, name=tag)
+        def turn_half(name, b, g):
+            if name == "x":
+                turned = gate_banks.tile([P, 2, TB], F32, name="turned")
+            else:
+                turned = gate_banks.tile([P, TB // 4, 2, 4], F32, name="turned")
             held[name + "_turned", b, g] = turned
             for j in range(J):
-                pairs = slice(j * P // run, (j + 1) * P // run)
                 for u in range(2):
-                    nc.tensor.transpose(turned[:, pairs, u, :], words_of(name, b, j, g, u), identity[:])
+                    if name == "x":
+                        place = turned[:, u, j * P : (j + 1) * P]
+                    else:
+                        place = turned[:, j * P // 4 : (j + 1) * P // 4, u, :]
+                    nc.tensor.transpose(place, words_of(name, b, j, g, u), identity[:])
 
-        def scale_x(b, g):
+        def scale(result, turned, g):
+            tokens = turned.shape[2]
             nc.vector.tensor_tensor(
-                out=kin_tile(("x", b))[:, g, :].rearrange("p (c i u e) -> p c u e i", i=2, u=2, e=2),
-                in0=held["x_turned", b, g][:].bitcast(BF16).rearrange("p c u (i e) -> p c u e i", e=2),
-                in1=x_mult[:, g, :].rearrange("p (c u e i) -> p c u e i", c=1, u=2, i=1).to_broadcast([P, TB // 2, 2, 2, 2]),
+                out=result.rearrange("p (n u e) -> p n u e", u=2, e=2),
+                in0=turned.bitcast(BF16).rearrange("p u (n e) -> p n u e", e=2),
+                in1=x_mult[:, g, :].rearrange("p (n u e) -> p n u e", n=1, u=2).to_broadcast([P, tokens, 2, 2]),
                 op=MULT,
             )
+
+        def scale_x(b, g):
+            scale(kin_tile(("x", b))[:, g, :], held["x_turned", b, g][:], g)
 
         def widen_first(j, copy, width):
             for first in range(0, D, width):
                 part = slice(first, first + width)
                 copy(out=x_wide[0][:, j, part], in_=x_first[j][:, part].bitcast(FP8))
 
+        def turn_first(j):
+            turned = banks.tile([P, 2, 2, P], F32, name="bank")
+            held["first", j] = turned
+            for g in range(2):
+                for u in range(2):
+                    nc.tensor.transpose(turned[:, g, u, :], words_of("x", 0, j, g, u), identity[:])
+
         def scale_first(j):
             for g in range(2):
-                nc.vector.tensor_tensor(
-                    out=kin_tile(("x", 0))[:, g, HALF * j : HALF * (j + 1)].rearrange("p (c i u e) -> p c u e i", i=2, u=2, e=2),
-                    in0=held["turned", "x", 0, j][:, g].bitcast(BF16).rearrange("p c u (i e) -> p c u e i", e=2),
-                    in1=x_mult[:, g, :].rearrange("p (c u e i) -> p c u e i", c=1, u=2, i=1).to_broadcast([P, P // 2, 2, 2, 2]),
-                    op=MULT,
-                )
+                scale(kin_tile(("x", 0))[:, g, HALF * j : HALF * (j + 1)], held["first", j][:, g], g)
 
         def quantise_x(b):
             quantise(flat(x_codes[b]), flat(x_scales[b]), flat(held["x", b]))
@@ -408,10 +419,10 @@ def tile_aft_full_pb_kernel(tc, x_bytes, x_scale, wq_w, wq_b, r_aft, out_w, out_
         widen_first(1, nc.scalar.copy, D)
         widen_tile(1, 0, nc.scalar.copy)
         widen_tile(1, 1, nc.gpsimd.tensor_copy)
-        turn("x", 0, 0)
+        turn_first(0)
         scale_first(0)
         turn_and_empty("wq", 0, 0)
-        turn("x", 0, 1)
+        turn_first(1)
         scale_first(1)
         turn_and_empty("wq", 0, 1)
         turn_and_empty("wq", 1, 0)
@@ -461,11 +472,10 @@ def tile_aft_full_pb_kernel(tc, x_bytes, x_scale, wq_w, wq_b, r_aft, out_w, out_
         turn_and_empty("ow", 0, 0)
         turn_and_empty("ow", 0, 1)
         turn_and_empty("ow", 1, 0)
-        turn("ow", 1, 1)
+        turn_and_empty("ow", 1, 1)
         gate(1, 0)
         turn_half("r", 1, 1)
         gate(0, 1)
-        empty("ow", 1, 1, nc.vector.tensor_copy)
         quantise_ow(0)
         quantise_y(0)
         quantise_ow(1)
@@ -480,9 +490,11 @@ def tile_aft_full_pb_kernel(tc, x_bytes, x_scale, wq_w, wq_b, r_aft, out_w, out_
         query_pair(2, 2)
         project(0, 1)
         sort_rows("ow", 3, 1)
-        finish(0, 1)
+        empty_sums(1)
+        finish(0)
         quantise_y(1)
-        sort_pair(handed_on(("y", 1), [P, 2, HALF]), "r", 2)
+        first = handed_on(("y", 1), [P, HALF])
+        bias_on_gpsimd(1, first[:])
         turn_half("x", 3, 0)
         turn_half("x", 3, 1)
         turn_and_empty("ow", 2, 0)
@@ -491,6 +503,7 @@ def tile_aft_full_pb_kernel(tc, x_bytes, x_scale, wq_w, wq_b, r_aft, out_w, out_
         turn_and_empty("ow", 3, 1)
         scale_x(3, 0)
         scale_x(3, 1)
+        store(1, first[:])
         quantise_ow(2)
         quantise_ow(3)
         quantise_x(3)
@@ -524,18 +537,21 @@ def tile_aft_full_pb_kernel(tc, x_bytes, x_scale, wq_w, wq_b, r_aft, out_w, out_
         gate_last(0, 0)
         gate_last(1, 0)
         finish(7)
+        empty_sums(8)
         quantise_last(0)
         store(2, third[:])
-        fourth = handed_on(("last", 0), [P, HALF])
-        bias_on_gpsimd(6, fourth[:])
-        finish(8, 9)
+        fourth = handed_on(("last", 0), [P, 2, HALF])
+        bias_on_gpsimd(6, fourth[:, 0])
+        bias_on_gpsimd(8, fourth[:, 1])
+        finish(9)
         for i in range(PAIRS):
             query_last_pair(1, i)
         project(10, 11, 12, 14)
         gate_last(0, 1)
-        store(6, fourth[:])
+        store(6, fourth[:, 0])
         finish(10)
         gate_last(1, 1)
+        store(8, fourth[:, 1])
         finish(11)
         quantise_last(1)
         finish(12, 14)

@@ -23,12 +23,13 @@ J = TB // P
 PAIRS = 4
 HALF = 512
 WORDS = HALF // 2
-SORTED_BUFS = 6
-RESULT_BUFS = 10
-SORTED_IN_RUN = 2
+VECTOR_BANKS = 3
+FLOW_BANKS = 5
+RESULT_BUFS = 9
+SORTED_BUFS = 4
 KIN_BUFS = 4
-HANDED_ON = (("wq", 0), ("wq", 2), ("wq", 3), ("y", 0), ("y", 1), ("ow", 3), ("y", 2))
 LAST = BLOCKS - 1
+OWN = (("wq", 0), ("wq", 3), ("x", 2), ("y", 0), ("y", 1), ("ow", 1), ("y", 2), ("ow", 0), ("last", 0), ("last", 1))
 
 
 def tile_aft_full_pb_kernel(tc, x_bytes, x_scale, wq_w, wq_b, r_aft, out_w, out_b, out):
@@ -42,8 +43,7 @@ def tile_aft_full_pb_kernel(tc, x_bytes, x_scale, wq_w, wq_b, r_aft, out_w, out_
     with ExitStack() as ctx:
         keep = ctx.enter_context(tc.tile_pool(name="keep", bufs=1))
         flow = ctx.enter_context(tc.tile_pool(name="flow", bufs=1))
-        banks = ctx.enter_context(tc.psum_pool(name="banks", bufs=5))
-        gate_banks = ctx.enter_context(tc.psum_pool(name="gate_banks", bufs=3))
+        psum = ctx.enter_context(tc.psum_pool(name="psum", bufs=1))
         ctx.enter_context(tc.manual_schedule())
 
         x_mult = keep.tile([P, 2, 4], F32)
@@ -51,16 +51,15 @@ def tile_aft_full_pb_kernel(tc, x_bytes, x_scale, wq_w, wq_b, r_aft, out_w, out_
         out_bias = [keep.tile([P, HALF], BF16, name="out_bias%d" % c) for c in range(2)]
         identity = keep.tile([P, P], F32)
         one_column = keep.tile([P, 1], F32)
-        x_wide = {b: keep.tile([P, J, D], BF16, name="x_wide%d" % b, align_bytes=64) for b in range(1)}
 
         def kept(name, count, shape, dtype):
             return [keep.tile(shape, dtype, name="%s%d" % (name, i), align_bytes=64) for i in range(count)]
 
-        x_raw = [None] + kept("x_raw", LAST, [P, J, D], U8)
         x_first = kept("x_first", J, [P, D], U8)
+        x_raw = [None] + kept("x_raw", LAST, [P, J, D], U8)
         r_raw = kept("r_raw", BLOCKS, [P, J, D], BF16)
         wq_first = kept("wq_first", 4, [P, D], BF16)
-        wq_rest = kept("wq_rest", PAIRS - 2, [P, 2, D], BF16)
+        wq_raw = [None, None] + kept("wq_raw", PAIRS - 2, [P, 2, D], BF16)
         ow_raw = kept("ow_raw", PAIRS, [P, 2, D], BF16)
         x_codes = kept("x_codes", BLOCKS, [P, 2, TB], U32)
         x_scales = kept("x_scales", BLOCKS, [P, 2, TB], U8)
@@ -70,46 +69,62 @@ def tile_aft_full_pb_kernel(tc, x_bytes, x_scale, wq_w, wq_b, r_aft, out_w, out_
         ow_scales = kept("ow_scales", 2, [P, 2, HALF], U8)
         y_codes = kept("y_codes", BLOCKS, [P, 2, TB], U32)
         y_scales = kept("y_scales", BLOCKS, [P, 2, TB], U8)
-        gate_sig = kept("gate_sig", 2 * LAST, [P, TB // 4, 4, 4], F32)
-        last_sig = kept("last_sig", 2 * J, [P, P // 4, 4, 4], F32)
+        sig = kept("sig", 2 * BLOCKS, [P, TB // 4, 4, 4], F32)
         held = {}
+        taken = {"vector": [], "flow": []}
 
-        def load_x(b):
-            nc.sync.dma_start(out=x_raw[b][:], in_=x_hbm[b])
+        def bank(kind, shape, dtype):
+            count = VECTOR_BANKS if kind == "vector" else FLOW_BANKS
+            taken[kind].append(shape)
+            return psum.tile(shape, dtype, name="%s%d" % (kind, len(taken[kind]) % count))
 
-        def load_x_first(j):
-            nc.sync.dma_start(out=x_first[j][:], in_=x_hbm[0][:, j, :])
-
-        def load_r(b):
-            nc.sync.dma_start(out=r_raw[b][:], in_=r_hbm[b])
-
-        def load_wq_first(i, s):
-            nc.sync.dma_start(out=wq_first[2 * i + s][:], in_=wq_hbm[0][i][:, s, :])
-
-        def load_wq(i):
-            nc.sync.dma_start(out=wq_rest[i - 2][:], in_=wq_hbm[i // 2][i % 2])
-
-        def load_ow(i):
-            nc.sync.dma_start(out=ow_raw[i][:], in_=ow_hbm[i])
-
-        def load_out_bias(c):
-            nc.sync.dma_start(out=out_bias[c][:], in_=out_b[HALF * c : HALF * (c + 1)].partition_broadcast(P))
-
-        def load_query_bias():
-            nc.sync.dma_start(out=query_bias[:], in_=wq_b.rearrange("(f p t) -> p f t", p=P, t=4))
+        def load(tile, source):
+            nc.sync.dma_start(out=tile[:], in_=source)
 
         def flat(tile):
             return tile[:].rearrange("p a c -> p (a c)")
 
-        def quantise(codes, scales, values):
-            nc.vector.quantize_mx(out=codes.bitcast(FP8X4), scales=scales, in_=values)
+        def own_tile(key, shape, dtype):
+            return flow.tile(shape, dtype, name="%s_in%d" % key, align_bytes=64)
+
+        def kin(key):
+            if key not in held:
+                shape = {"ow": [P, 2, 4 * HALF], "last": [P, D]}.get(key[0], [P, 2, 4 * TB])
+                if key in OWN:
+                    held[key] = own_tile(key, shape, BF16)
+                else:
+                    held[key] = flow.tile(shape, BF16, name="kin", align_bytes=64, bufs=KIN_BUFS)
+            return held[key]
 
         def rows_of(name, i, s):
             if name == "x":
-                return x_wide[i, s, "tile"][:] if (i, s, "tile") in x_wide else x_wide[i][:, s, :]
+                return held["wide", i, s]
             if name == "wq":
-                return wq_rest[i - 2][:, s, :] if i >= 2 else wq_first[2 * i + s][:]
+                return wq_raw[i][:, s, :] if i >= 2 else wq_first[2 * i + s][:]
             return (r_raw if name == "r" else ow_raw)[i][:, s, :]
+
+        def widen_tile(b, j, copy, width=D, key=None):
+            wide = own_tile(key, [P, D], BF16) if key else flow.tile([P, D], BF16, name="wide%d_%d" % (b, j), align_bytes=64)
+            held["wide", b, j] = wide[:]
+            source = x_raw[b][:, j, :] if b else x_first[j][:]
+            for first in range(0, D, width):
+                copy(out=wide[:, first : first + width], in_=source[:, first : first + width].bitcast(FP8))
+
+        def widen_block(b, key=None):
+            wide = own_tile(key or ("wide", b), [P, J, D], BF16)
+            for j in range(J):
+                held["wide", b, j] = wide[:, j, :]
+            nc.gpsimd.tensor_copy(out=flat(wide), in_=flat(x_raw[b]).bitcast(FP8))
+
+        def sort_pair(name, i, key):
+            ordered = own_tile(key, [P, 2, HALF], F32)
+            for s in range(2):
+                for g in range(2):
+                    held["sorted", name, i, s, g] = ordered[:, s, WORDS * g : WORDS * (g + 1)]
+            nc.gpsimd.tensor_copy(
+                out=ordered[:].bitcast(U32).rearrange("p s (g u c) -> p (s g) u c", g=2, u=2),
+                in_={"r": r_raw, "ow": ow_raw, "wq": wq_raw}[name][i][:].bitcast(U32).rearrange("p s (g c u) -> p (s g) u c", g=2, u=2),
+            )
 
         def sort_rows(name, i, s):
             ordered = flow.tile([P, HALF], F32, name="ordered", align_bytes=64, bufs=SORTED_BUFS)
@@ -118,6 +133,15 @@ def tile_aft_full_pb_kernel(tc, x_bytes, x_scale, wq_w, wq_b, r_aft, out_w, out_
             nc.scalar.copy(
                 out=ordered[:].rearrange("p (g u c e) -> p g c u e", g=2, u=2, e=2),
                 in_=rows_of(name, i, s).bitcast(F32).rearrange("p (g c e u) -> p g c u e", g=2, u=2, e=2),
+            )
+
+        def sort_tile(name, i, s, copy):
+            ordered = flow.tile([P, HALF], F32, name="ordered", align_bytes=64, bufs=SORTED_BUFS)
+            for g in range(2):
+                held["sorted", name, i, s, g] = ordered[:, WORDS * g : WORDS * (g + 1)]
+            copy(
+                out=ordered[:].bitcast(U32).rearrange("p (g u c) -> p g u c", g=2, u=2),
+                in_=rows_of(name, i, s).bitcast(U32).rearrange("p (g c u) -> p g u c", g=2, u=2),
             )
 
         def sort_half(b, f):
@@ -129,105 +153,40 @@ def tile_aft_full_pb_kernel(tc, x_bytes, x_scale, wq_w, wq_b, r_aft, out_w, out_
                 in_=r_raw[b][:].bitcast(F32)[:, :, WORDS * f : WORDS * (f + 1)].rearrange("p j (c e u) -> p j c u e", u=2, e=2),
             )
 
-        def handed_on(key, shape):
-            return flow.tile(shape, F32, name="%s_in%d" % key, align_bytes=64)
-
-        def sort_behind(key, *banks_of_rows, spare=0):
-            ordered = handed_on(key, [P, len(banks_of_rows) + spare, 2, WORDS])
-            for place, (name, i, s) in enumerate(banks_of_rows):
-                if name == "r":
-                    source = r_raw[i][:].bitcast(U32)[:, :, WORDS * s : WORDS * (s + 1)]
-                else:
-                    source = rows_of(name, i, s).bitcast(U32).rearrange("p (g w) -> p g w", g=2)
-                for part in range(2):
-                    held[("sorted", name, i, part, s) if name == "r" else ("sorted", name, i, s, part)] = ordered[:, place, part]
-                nc.gpsimd.tensor_copy(
-                    out=ordered[:, place].bitcast(U32).rearrange("p a (u c) -> p a u c", u=2),
-                    in_=source.rearrange("p a (c u) -> p a u c", u=2),
-                )
-            return ordered
-
-        def sort_pair(ordered, name, i):
-            for s in range(2):
-                for g in range(2):
-                    held["sorted", name, i, s, g] = ordered[:, s, WORDS * g : WORDS * (g + 1)]
-            nc.gpsimd.tensor_copy(
-                out=ordered[:].bitcast(U32).rearrange("p s (g u c) -> p (s g) u c", g=2, u=2),
-                in_=(r_raw if name == "r" else ow_raw)[i][:].bitcast(U32).rearrange("p s (g c u) -> p (s g) u c", g=2, u=2),
-            )
-
-        def widen_tile(b, j, copy, key=None):
-            name = "%s_in%d" % key if key else "x_wide%d_%d" % (b, j)
-            x_wide[b, j, "tile"] = flow.tile([P, D], BF16, name=name, align_bytes=64)
-            copy(out=x_wide[b, j, "tile"][:], in_=x_raw[b][:, j, :].bitcast(FP8))
-
         def words_of(name, i, s, g, u):
             if ("sorted", name, i, s, g) in held:
                 return held["sorted", name, i, s, g][:, P * u : P * (u + 1)]
-            if name == "x" and (i, g) in x_wide:
-                return x_wide[i, g][:, s, :].bitcast(F32)[:, u::2]
             return rows_of(name, i, s).bitcast(F32)[:, WORDS * g + u : WORDS * (g + 1) : 2]
 
-        def kin_tile(key):
-            if key not in held:
-                if key in HANDED_ON:
-                    held[key] = flow.tile([P, 2, 4 * TB], BF16, name="%s_in%d" % key, align_bytes=64)
-                else:
-                    held[key] = flow.tile([P, 2, 4 * TB], BF16, name="kin", align_bytes=64, bufs=KIN_BUFS)
-            return held[key]
-
-        def last_tile(j):
-            if ("last", j) not in held:
-                held["last", j] = flow.tile([P, D], BF16, name="last_in%d" % j, align_bytes=64)
-            return held["last", j]
-
-        def handed_on_codes(j):
-            return handed_on(("last", j), [P, HALF])[:]
-
-        def turn(name, i, s):
-            turned = banks.tile([P, 2, P // 2, 2, 2], F32, name="bank")
-            held["turned", name, i, s] = turned
+        def turn_only(name, i, s):
+            turned = bank("flow", [P, 2, P // 2, 2, 2], F32)
             for g in range(2):
                 for u in range(2):
                     nc.tensor.transpose(turned[:, g, :, u, :], words_of(name, i, s, g, u), identity[:])
+            held["turned", name, i, s] = turned
 
-        def empty(name, i, s, copy=nc.scalar.copy):
-            kin_words = kin_tile((name, i))[:].bitcast(F32)
+        def empty_weight(name, i, s):
+            turned = held["turned", name, i, s]
             if name == "wq":
-                kin_words = kin_words[:, s, :].rearrange("p (g w) -> p g w", g=2)
+                words = kin((name, i))[:, s, :].bitcast(F32).rearrange("p (g w) -> p g w", g=2)
             else:
-                kin_words = kin_words[:, :, WORDS * s : WORDS * (s + 1)]
-            copy(out=kin_words.rearrange("p g (c i u) -> p g c u i", i=2, u=2), in_=held["turned", name, i, s][:])
+                place = 2 * (i % 2) + s
+                words = kin((name, i // 2))[:].bitcast(F32)[:, :, WORDS * place : WORDS * (place + 1)]
+            nc.scalar.copy(out=words.rearrange("p g (c i u) -> p g c u i", i=2, u=2), in_=turned[:])
 
-        def turn_and_empty(name, i, s):
-            turn(name, i, s)
-            empty(name, i, s)
+        def turn_weight(name, i, s):
+            turn_only(name, i, s)
+            empty_weight(name, i, s)
 
-        def widen(b, key=None):
-            if key:
-                x_wide[b] = flow.tile([P, J, D], BF16, name="%s_in%d" % key, align_bytes=64)
-            if b == LAST:
-                x_wide[b] = keep.tile([P, J, D], BF16, name="x_wide3", align_bytes=64)
-            nc.gpsimd.tensor_copy(out=flat(x_wide[b]), in_=flat(x_raw[b]).bitcast(FP8))
-
-        def widen_half(b, g, copy):
-            for j in range(J):
-                part = slice(HALF * g, HALF * (g + 1))
-                copy(out=x_wide[b, g][:, j, :], in_=x_raw[b][:, j, part].bitcast(FP8))
-
-        def turn_half(name, b, g):
-            if name == "x":
-                turned = gate_banks.tile([P, 2, TB], F32, name="turned")
-            else:
-                turned = gate_banks.tile([P, TB // 4, 2, 4], F32, name="turned")
-            held[name + "_turned", b, g] = turned
-            for j in range(J):
+        def turn_x(b, g):
+            turned = bank("vector", [P, 2, TB], F32)
+            held["x_turned", b, g] = turned
+            for part in range(2):
                 for u in range(2):
-                    if name == "x":
-                        place = turned[:, u, j * P : (j + 1) * P]
+                    if b:
+                        nc.tensor.transpose(turned[:, u, part * P : (part + 1) * P], words_of("x", b, part, g, u), identity[:])
                     else:
-                        place = turned[:, j * P // 4 : (j + 1) * P // 4, u, :]
-                    nc.tensor.transpose(place, words_of(name, b, j, g, u), identity[:])
+                        nc.tensor.transpose(turned[:, part, u * P : (u + 1) * P], words_of("x", 0, g, part, u), identity[:])
 
         def scale(result, turned, g):
             tokens = turned.shape[2]
@@ -239,41 +198,52 @@ def tile_aft_full_pb_kernel(tc, x_bytes, x_scale, wq_w, wq_b, r_aft, out_w, out_
             )
 
         def scale_x(b, g):
-            scale(kin_tile(("x", b))[:, g, :], held["x_turned", b, g][:], g)
+            turned = held["x_turned", b, g]
+            if b:
+                scale(kin(("x", b))[:, g, :], turned[:], g)
+            else:
+                for part in range(2):
+                    scale(kin(("x", 0))[:, part, HALF * g : HALF * (g + 1)], turned[:, part, :].rearrange("p (u n) -> p u n", u=2), part)
 
-        def widen_first(j, copy, width):
-            for first in range(0, D, width):
-                part = slice(first, first + width)
-                copy(out=x_wide[0][:, j, part], in_=x_first[j][:, part].bitcast(FP8))
-
-        def turn_first(j):
-            turned = banks.tile([P, 2, 2, P], F32, name="bank")
-            held["first", j] = turned
-            for g in range(2):
+        def turn_r(b, f):
+            turned = bank("vector", [P, TB // 4, 2, 4], F32)
+            held["r_turned", b, f] = turned[:].bitcast(BF16).rearrange("p c u (i e) -> p c u e i", e=2)
+            for j in range(J):
                 for u in range(2):
-                    nc.tensor.transpose(turned[:, g, u, :], words_of("x", 0, j, g, u), identity[:])
+                    nc.tensor.transpose(turned[:, j * P // 4 : (j + 1) * P // 4, u, :], words_of("r", b, j, f, u), identity[:])
 
-        def scale_first(j):
-            for g in range(2):
-                scale(kin_tile(("x", 0))[:, g, HALF * j : HALF * (j + 1)], held["first", j][:, g], g)
+        def quantise(codes, scales, values):
+            nc.vector.quantize_mx(out=codes.bitcast(FP8X4), scales=scales, in_=values)
 
         def quantise_x(b):
             quantise(flat(x_codes[b]), flat(x_scales[b]), flat(held["x", b]))
 
         def quantise_wq(i):
-            quantise(
-                wq_codes[i][:].rearrange("p s g m -> p (s g m)"),
-                wq_scales[i][:].rearrange("p s g m -> p (s g m)"),
-                flat(held["wq", i]),
-            )
+            quantise(wq_codes[i][:].rearrange("p s g m -> p (s g m)"), wq_scales[i][:].rearrange("p s g m -> p (s g m)"), flat(held["wq", i]))
 
-        def quantise_ow(i):
-            columns = slice(TB * (i % 2), TB * (i % 2 + 1))
+        def quantise_ow(c, g):
+            quantise(ow_codes[c][:, g, :], ow_scales[c][:, g, :], held["ow", c][:, g, :])
+
+        def quantise_ow_pair(i):
             for g in range(2):
-                quantise(ow_codes[i // 2][:, g, columns], ow_scales[i // 2][:, g, columns], held["ow", i][:, g, :])
+                columns = slice(TB * (i % 2), TB * (i % 2 + 1))
+                values = slice(4 * columns.start, 4 * columns.stop)
+                quantise(ow_codes[i // 2][:, g, columns], ow_scales[i // 2][:, g, columns], held["ow", i // 2][:, g, values])
 
-        def query(b, tokens, tiles, sig):
-            q = banks.tile([P, len(tiles), tokens.stop - tokens.start], F32, name="bank")
+        def quantise_y(b):
+            quantise(flat(y_codes[b]), flat(y_scales[b]), flat(held["y", b]))
+
+        def quantise_y_tile(b, j):
+            quantise(y_codes[b][:, j, :], y_scales[b][:, j, :], held["last", j][:])
+
+        def y_part(tiles, b, j, g):
+            if ("by_tiles", b) in held:
+                return tiles[b][:, j, g * P : (g + 1) * P]
+            return tiles[b][:, g, j * P : (j + 1) * P]
+
+        def query_only(b, tiles, tokens):
+            q = bank("flow", [P, len(tiles), tokens.stop - tokens.start], F32)
+            held["query", b, tiles[0], tokens.start] = q
             for place, (f, t) in enumerate(tiles):
                 i, s = 2 * f + t // 2, t % 2
                 for g in range(2):
@@ -286,12 +256,12 @@ def tile_aft_full_pb_kernel(tc, x_bytes, x_scale, wq_w, wq_b, r_aft, out_w, out_
                         start=(g == 0),
                         stop=(g == 1),
                     )
-            return q, tiles, sig
 
-        def sigmoids(q, tiles, sig):
+        def sigmoids(b, tiles, tokens):
+            q = held["query", b, tiles[0], tokens.start]
             for place, (f, t) in enumerate(tiles):
                 nc.scalar.activation(
-                    out=sig[:, :, t, :],
+                    out=sig[2 * b + f][:, tokens.start // 4 : tokens.stop // 4, t, :],
                     in_=q[:, place, :].rearrange("p (c i) -> p c i", i=4),
                     func=SIGMOID,
                     bias=query_bias[:, f, t : t + 1],
@@ -301,260 +271,249 @@ def tile_aft_full_pb_kernel(tc, x_bytes, x_scale, wq_w, wq_b, r_aft, out_w, out_
             return [(i // 2, 2 * (i % 2) + s) for s in range(2)]
 
         def query_pair(b, i):
-            sigmoids(*query(b, slice(0, TB), pair_tiles(i), gate_sig[2 * b + i // 2]))
+            query_only(b, pair_tiles(i), slice(0, TB))
 
-        def query_block(b):
-            for i in range(PAIRS):
-                query_pair(b, i)
+        def sigmoid_pair(b, i):
+            sigmoids(b, pair_tiles(i), slice(0, TB))
 
-        def query_last_half(j, f):
-            sigmoids(*query(LAST, slice(P * j, P * (j + 1)), [(f, t) for t in range(4)], last_sig[2 * j + f]))
+        def query(b, i, tokens=slice(0, TB)):
+            query_only(b, pair_tiles(i), tokens)
+            sigmoids(b, pair_tiles(i), tokens)
 
-        def query_last_pair(j, i):
-            sigmoids(*query(LAST, slice(P * j, P * (j + 1)), pair_tiles(i), last_sig[2 * j + i // 2]))
+        def query_half(b, j, f):
+            tiles = [(f, t) for t in range(4)]
+            query_only(b, tiles, slice(P * j, P * (j + 1)))
+            sigmoids(b, tiles, slice(P * j, P * (j + 1)))
 
         def gate(b, f):
             nc.vector.tensor_tensor(
-                out=kin_tile(("y", b))[:, f, :].rearrange("p (c i u e) -> p c u e i", i=4, u=2, e=2),
-                in0=held["r_turned", b, f][:].bitcast(BF16).rearrange("p c u (i e) -> p c u e i", e=2),
-                in1=gate_sig[2 * b + f][:].rearrange("p c (u e) i -> p c u e i", u=2),
+                out=kin(("y", b))[:, f, :].rearrange("p (c i u e) -> p c u e i", i=4, u=2, e=2),
+                in0=held["r_turned", b, f],
+                in1=sig[2 * b + f][:].rearrange("p c (u e) i -> p c u e i", u=2),
                 op=MULT,
             )
 
-        def gate_last(f, j):
-            pairs = slice(j * P // 4, (j + 1) * P // 4)
+        def gate_tile(b, f, j):
+            part = slice(j * P // 4, (j + 1) * P // 4)
+            held["by_tiles", b] = True
             nc.vector.tensor_tensor(
-                out=last_tile(j)[:, HALF * f : HALF * (f + 1)].rearrange("p (c i u e) -> p c u e i", i=4, u=2, e=2),
-                in0=held["r_turned", LAST, f][:, pairs].bitcast(BF16).rearrange("p c u (i e) -> p c u e i", e=2),
-                in1=last_sig[2 * j + f][:].rearrange("p c (u e) i -> p c u e i", u=2),
+                out=kin(("last", j))[:, HALF * f : HALF * (f + 1)].rearrange("p (c i u e) -> p c u e i", i=4, u=2, e=2),
+                in0=held["r_turned", b, f][:, part],
+                in1=sig[2 * b + f][:, part].rearrange("p c (u e) i -> p c u e i", u=2),
                 op=MULT,
             )
 
-        def quantise_last(j):
-            quantise(y_codes[LAST][:, j, :], y_scales[LAST][:, j, :], last_tile(j)[:])
+        def project(b, j, c):
+            sums = bank("flow", [P, HALF], F32)
+            held["sums", b, j, c] = sums
+            for g in range(2):
+                nc.tensor.matmul_mx(
+                    out=sums[:],
+                    lhsT=y_part(y_codes, b, j, g).bitcast(FP8X4),
+                    lhsT_scale=y_part(y_scales, b, j, g),
+                    rhs=ow_codes[c][:, g, :].bitcast(FP8X4),
+                    rhs_scale=ow_scales[c][:, g, :],
+                    start=(g == 0),
+                    stop=(g == 1),
+                )
 
-        def y_part(tiles, b, j, g):
-            if b == LAST:
-                return tiles[b][:, j, g * P : (g + 1) * P]
-            return tiles[b][:, g, j * P : (j + 1) * P]
+        def store(b, j, c):
+            nc.sync.dma_start(out=out_hbm[b][:, j, HALF * c : HALF * (c + 1)], in_=held["result", b, j, c])
 
-        def quantise_y(b):
-            quantise(flat(y_codes[b]), flat(y_scales[b]), flat(held["y", b]))
-
-        def project(*tiles):
-            for n in tiles:
-                b, c, j = n // 4, n // 2 % 2, n % 2
-                held["sums", n] = banks.tile([P, HALF], F32, name="bank")
-                for g in range(2):
-                    nc.tensor.matmul_mx(
-                        out=held["sums", n][:],
-                        lhsT=y_part(y_codes, b, j, g).bitcast(FP8X4),
-                        lhsT_scale=y_part(y_scales, b, j, g),
-                        rhs=ow_codes[c][:, g, :].bitcast(FP8X4),
-                        rhs_scale=ow_scales[c][:, g, :],
-                        start=(g == 0),
-                        stop=(g == 1),
-                    )
-
-        def result_and_bias(n):
-            c = n // 2 % 2
+        def finish(b, j, c):
             result = flow.tile([P, HALF], F32, name="result", align_bytes=64, bufs=RESULT_BUFS)
-            return result[:], out_bias[c][:]
+            held["result", b, j, c] = result[:]
+            nc.vector.tensor_tensor(out=result[:], in0=held["sums", b, j, c][:], in1=out_bias[c][:], op=ADD)
+            store(b, j, c)
 
-        def store(n, result):
-            b, c, j = n // 4, n // 2 % 2, n % 2
-            nc.sync.dma_start(out=out_hbm[b][:, j, HALF * c : HALF * (c + 1)], in_=result)
-
-        def finish_by_halves(n):
-            b, c, j = n // 4, n // 2 % 2, n % 2
+        def finish_by_halves(b, j, c):
             for h in range(2):
                 part = slice(TB * h, TB * (h + 1))
                 result = flow.tile([P, TB], F32, name="result", align_bytes=64, bufs=RESULT_BUFS)
-                nc.vector.tensor_tensor(out=result[:], in0=held["sums", n][:, part], in1=out_bias[c][:, part], op=ADD)
+                nc.vector.tensor_tensor(out=result[:], in0=held["sums", b, j, c][:, part], in1=out_bias[c][:, part], op=ADD)
                 nc.sync.dma_start(out=out_hbm[b][:, j, HALF * c + TB * h : HALF * c + TB * (h + 1)], in_=result[:])
 
-        def finish(*tiles):
-            for n in tiles:
-                result, bias = result_and_bias(n)
-                nc.vector.tensor_tensor(out=result, in0=held["sums", n][:], in1=bias, op=ADD)
-                store(n, result)
+        def empty(b, j, c):
+            result = flow.tile([P, HALF], F32, name="result", align_bytes=64, bufs=RESULT_BUFS)
+            held["emptied", b, j, c] = result[:]
+            nc.scalar.copy(out=result[:], in_=held["sums", b, j, c][:])
 
-        def empty_sums(n):
-            held["emptied", n] = result_and_bias(n)
-            nc.scalar.copy(out=held["emptied", n][0], in_=held["sums", n][:])
-
-        def bias_on_gpsimd(n, result):
-            sums, bias = held["emptied", n]
-            nc.gpsimd.tensor_tensor(out=result, in0=sums, in1=bias, op=ADD)
+        def add_behind(key, *tiles):
+            results = own_tile(key, [P, len(tiles), HALF], F32)
+            for place, (b, j, c) in enumerate(tiles):
+                held["result", b, j, c] = results[:, place, :]
+                nc.gpsimd.tensor_tensor(out=results[:, place, :], in0=held["emptied", b, j, c], in1=out_bias[c][:], op=ADD)
 
         nc.gpsimd.memset(one_column[:], 0.0)
         make_identity(nc, identity[:])
         nc.scalar.activation(out=one_column[:], in_=one_column[:], func=SIGMOID)
 
-        load_x_first(0)
-        load_x_first(1)
-        nc.sync.dma_start(out=x_mult[:], in_=x_scale[0, :, :].rearrange("o (g p t) -> p (o g) t", p=P, t=4))
-        load_wq_first(0, 0)
-        load_x(1)
-        load_wq_first(0, 1)
-        load_wq_first(1, 0)
-        load_wq_first(1, 1)
-        load_wq(2)
-        load_x(2)
-        load_wq(3)
-        load_query_bias()
-        load_x(3)
-        load_r(0)
-        load_ow(0)
-        load_r(1)
-        load_ow(1)
-        load_ow(2)
-        load_ow(3)
-        load_out_bias(0)
-        load_r(2)
-        load_out_bias(1)
-        load_r(3)
+        load(x_first[0], x_hbm[0][:, 0, :])
+        load(x_first[1], x_hbm[0][:, 1, :])
+        load(x_mult, x_scale[0, :, :].rearrange("o (g p t) -> p (o g) t", p=P, t=4))
+        load(wq_first[0], wq_hbm[0][0][:, 0, :])
+        load(x_raw[1], x_hbm[1])
+        load(wq_first[1], wq_hbm[0][0][:, 1, :])
+        load(wq_first[2], wq_hbm[0][1][:, 0, :])
+        load(wq_first[3], wq_hbm[0][1][:, 1, :])
+        load(x_raw[2], x_hbm[2])
+        load(wq_raw[2], wq_hbm[1][0])
+        load(wq_raw[3], wq_hbm[1][1])
+        load(query_bias, wq_b.rearrange("(f p t) -> p f t", p=P, t=4))
+        load(r_raw[0], r_hbm[0])
+        load(x_raw[3], x_hbm[3])
+        load(ow_raw[0], ow_hbm[0])
+        load(r_raw[1], r_hbm[1])
+        load(ow_raw[1], ow_hbm[1])
+        load(ow_raw[2], ow_hbm[2])
+        load(ow_raw[3], ow_hbm[3])
+        load(out_bias[0], out_b[HALF * 0 : HALF * 1].partition_broadcast(P))
+        load(r_raw[2], r_hbm[2])
+        load(out_bias[1], out_b[HALF * 1 : HALF * 2].partition_broadcast(P))
+        load(r_raw[3], r_hbm[3])
 
-        widen_first(0, nc.vector.tensor_copy, HALF)
-        widen_first(1, nc.scalar.copy, D)
+        widen_tile(0, 0, nc.vector.tensor_copy, HALF)
+        widen_tile(0, 1, nc.scalar.copy)
         widen_tile(1, 0, nc.scalar.copy)
-        widen_tile(1, 1, nc.gpsimd.tensor_copy)
-        turn_first(0)
-        scale_first(0)
-        turn_and_empty("wq", 0, 0)
-        turn_first(1)
-        scale_first(1)
-        turn_and_empty("wq", 0, 1)
-        turn_and_empty("wq", 1, 0)
-        turn_and_empty("wq", 1, 1)
+        widen_tile(1, 1, nc.scalar.copy)
+        turn_x(0, 0)
+        scale_x(0, 0)
+        turn_weight("wq", 0, 0)
+        turn_x(0, 1)
+        scale_x(0, 1)
+        turn_weight("wq", 0, 1)
+        turn_weight("wq", 1, 0)
+        turn_weight("wq", 1, 1)
         quantise_x(0)
         quantise_wq(0)
         quantise_wq(1)
+        sort_pair("wq", 3, ("wq", 0))
         widen_tile(2, 0, nc.scalar.copy)
-        widen_tile(2, 1, nc.gpsimd.tensor_copy, ("wq", 0))
-        turn_half("x", 1, 0)
-        turn_half("x", 1, 1)
-        turn("wq", 2, 0)
-        turn("wq", 2, 1)
-        empty("wq", 2, 0)
-        sort_rows("wq", 3, 0)
-        empty("wq", 2, 1)
-        sort_rows("wq", 3, 1)
+        turn_x(1, 0)
+        turn_x(1, 1)
+        turn_only("wq", 2, 0)
+        turn_only("wq", 2, 1)
+        widen_tile(2, 1, nc.scalar.copy)
+        empty_weight("wq", 2, 0)
+        empty_weight("wq", 2, 1)
         scale_x(1, 0)
         scale_x(1, 1)
         quantise_x(1)
         quantise_wq(2)
-        sort_pair(handed_on(("wq", 2), [P, 2, HALF]), "ow", 0)
-        sort_rows("r", 0, 0)
-        sort_rows("r", 0, 1)
-        query_pair(0, 0)
-        waiting = query(0, slice(0, TB), pair_tiles(1), gate_sig[0])
-        turn_half("x", 2, 0)
-        turn_and_empty("wq", 3, 0)
-        turn_and_empty("wq", 3, 1)
-        turn_half("x", 2, 1)
-        turn_half("r", 0, 0)
-        sigmoids(*waiting)
+        query(0, 0)
+        query(0, 1)
+        sort_half(0, 0)
+        turn_x(2, 0)
+        turn_x(2, 1)
+        turn_weight("wq", 3, 0)
+        turn_weight("wq", 3, 1)
+        turn_r(0, 0)
+        sort_half(0, 1)
         scale_x(2, 0)
-        scale_x(2, 1)
         quantise_wq(3)
-        quantise_x(2)
-        sort_pair(handed_on(("wq", 3), [P, 2, HALF]), "ow", 1)
-        widen(3)
-        query_pair(0, 2)
-        query_pair(1, 0)
-        query_pair(1, 1)
-        query_pair(0, 3)
+        sort_pair("ow", 0, ("wq", 3))
+        scale_x(2, 1)
         gate(0, 0)
-        sort_half(1, 1)
-        turn_half("r", 1, 0)
-        turn_half("r", 0, 1)
-        turn_and_empty("ow", 0, 0)
-        turn_and_empty("ow", 0, 1)
-        turn_and_empty("ow", 1, 0)
-        turn_and_empty("ow", 1, 1)
+        quantise_x(2)
+        widen_tile(3, 0, nc.gpsimd.tensor_copy, D, ("x", 2))
+        query(0, 2)
+        query(1, 0)
+        query(1, 1)
+        query(0, 3)
+        widen_tile(3, 1, nc.scalar.copy)
+        turn_r(1, 0)
+        turn_r(0, 1)
+        turn_weight("ow", 1, 0)
+        turn_weight("ow", 1, 1)
+        turn_weight("ow", 0, 0)
+        turn_weight("ow", 0, 1)
+        turn_r(1, 1)
         gate(1, 0)
-        turn_half("r", 1, 1)
         gate(0, 1)
-        quantise_ow(0)
+        quantise_ow_pair(1)
         quantise_y(0)
-        quantise_ow(1)
-
-        sort_pair(handed_on(("y", 0), [P, 2, HALF]), "ow", 2)
-        query_pair(1, 2)
-        query_pair(1, 3)
-        query_pair(2, 0)
-        query_pair(2, 1)
+        quantise_ow_pair(0)
+        sort_pair("ow", 2, ("y", 0))
+        query(1, 2)
+        query(1, 3)
+        query(2, 0)
+        query(2, 1)
         gate(1, 1)
         sort_rows("ow", 3, 0)
-        query_pair(2, 2)
-        project(0, 1)
+        query(2, 2)
+        project(0, 0, 0)
+        project(0, 1, 0)
         sort_rows("ow", 3, 1)
-        empty_sums(1)
-        finish(0)
+        finish(0, 0, 0)
+        finish(0, 1, 0)
         quantise_y(1)
-        first = handed_on(("y", 1), [P, HALF])
-        bias_on_gpsimd(1, first[:])
-        turn_half("x", 3, 0)
-        turn_half("x", 3, 1)
-        turn_and_empty("ow", 2, 0)
-        turn_and_empty("ow", 2, 1)
-        turn_and_empty("ow", 3, 0)
-        turn_and_empty("ow", 3, 1)
+        sort_pair("r", 2, ("y", 1))
+        turn_x(3, 0)
+        turn_x(3, 1)
+        turn_weight("ow", 2, 0)
+        turn_weight("ow", 2, 1)
+        turn_weight("ow", 3, 0)
+        turn_weight("ow", 3, 1)
         scale_x(3, 0)
         scale_x(3, 1)
-        store(1, first[:])
-        quantise_ow(2)
-        quantise_ow(3)
+        quantise_ow_pair(2)
+        quantise_ow_pair(3)
         quantise_x(3)
-        project(4, 5)
-        empty_sums(4)
-        query_pair(2, 3)
-        empty_sums(5)
-        second = handed_on(("ow", 3), [P, 2, HALF])
-        bias_on_gpsimd(4, second[:, 0])
-        bias_on_gpsimd(5, second[:, 1])
+        project(1, 0, 0)
+        project(1, 1, 0)
+        empty(1, 0, 0)
+        query(2, 3)
+        empty(1, 1, 0)
+        add_behind(("ow", 1), (1, 0, 0), (1, 1, 0))
         sort_rows("r", 3, 0)
-        turn_half("r", 2, 0)
-        turn_half("r", 2, 1)
-        project(2, 3)
-        empty_sums(2)
+        turn_r(2, 0)
+        turn_r(2, 1)
+        project(0, 0, 1)
+        project(0, 1, 1)
+        empty(0, 0, 1)
         sort_rows("r", 3, 1)
         gate(2, 0)
-        store(4, second[:, 0])
+        store(1, 0, 0)
         gate(2, 1)
-        store(5, second[:, 1])
-        finish(3)
+        store(1, 1, 0)
+        finish(0, 1, 1)
         quantise_y(2)
-        third = handed_on(("y", 2), [P, HALF])
-        bias_on_gpsimd(2, third[:])
-        query_last_half(0, 0)
-        query_last_half(0, 1)
-        turn_half("r", 3, 0)
-        turn_half("r", 3, 1)
-        project(6, 7, 8, 9)
-        empty_sums(6)
-        gate_last(0, 0)
-        gate_last(1, 0)
-        finish(7)
-        empty_sums(8)
-        quantise_last(0)
-        store(2, third[:])
-        fourth = handed_on(("last", 0), [P, 2, HALF])
-        bias_on_gpsimd(6, fourth[:, 0])
-        bias_on_gpsimd(8, fourth[:, 1])
-        finish(9)
-        for i in range(PAIRS):
-            query_last_pair(1, i)
-        project(10, 11, 12, 14)
-        gate_last(0, 1)
-        store(6, fourth[:, 0])
-        finish(10)
-        gate_last(1, 1)
-        store(8, fourth[:, 1])
-        finish(11)
-        quantise_last(1)
-        finish(12, 14)
-        project(13, 15)
-        finish(13)
-        finish_by_halves(15)
+        add_behind(("y", 2), (0, 0, 1))
+        query_half(3, 0, 0)
+        query_half(3, 0, 1)
+        turn_r(3, 0)
+        turn_r(3, 1)
+        project(1, 0, 1)
+        project(1, 1, 1)
+        project(2, 0, 0)
+        project(2, 1, 0)
+        empty(1, 0, 1)
+        gate_tile(3, 0, 0)
+        gate_tile(3, 1, 0)
+        finish(1, 1, 1)
+        empty(2, 0, 0)
+        quantise_y_tile(3, 0)
+        store(0, 0, 1)
+        add_behind(("last", 0), (1, 0, 1), (2, 0, 0))
+        finish(2, 1, 0)
+        query(3, 0, slice(P * 1, P * 2))
+        query(3, 1, slice(P * 1, P * 2))
+        query(3, 2, slice(P * 1, P * 2))
+        query(3, 3, slice(P * 1, P * 2))
+        project(2, 0, 1)
+        project(2, 1, 1)
+        project(3, 0, 0)
+        project(3, 0, 1)
+        gate_tile(3, 0, 1)
+        store(1, 0, 1)
+        finish(2, 0, 1)
+        gate_tile(3, 1, 1)
+        store(2, 0, 0)
+        finish(2, 1, 1)
+        quantise_y_tile(3, 1)
+        finish(3, 0, 0)
+        finish(3, 0, 1)
+        project(3, 1, 0)
+        project(3, 1, 1)
+        finish(3, 1, 0)
+        finish_by_halves(3, 1, 1)

@@ -51,6 +51,7 @@ def tile_aft_full_pb_kernel(tc, x_bytes, x_scale, wq_w, wq_b, r_aft, out_w, out_
         out_bias = [keep.tile([P, HALF], BF16, name="out_bias%d" % c) for c in range(2)]
         identity = keep.tile([P, P], F32)
         one_column = keep.tile([P, 1], F32)
+        zeros = keep.tile([P, HALF], BF16, align_bytes=64)
 
         def kept(name, count, shape, dtype):
             return [keep.tile(shape, dtype, name="%s%d" % (name, i), align_bytes=64) for i in range(count)]
@@ -95,6 +96,10 @@ def tile_aft_full_pb_kernel(tc, x_bytes, x_scale, wq_w, wq_b, r_aft, out_w, out_
                 else:
                     held[key] = flow.tile(shape, BF16, name="kin", align_bytes=64, bufs=KIN_BUFS)
             return held[key]
+
+        def warm_up(width):
+            place = bank("flow", [P, HALF], F32)
+            nc.tensor.matmul(out=place[:, :width], lhsT=zeros[:, :P], rhs=zeros[:, :width], start=True, stop=True)
 
         def rows_of(name, i, s):
             if name == "x":
@@ -344,6 +349,7 @@ def tile_aft_full_pb_kernel(tc, x_bytes, x_scale, wq_w, wq_b, r_aft, out_w, out_
                 held["result", b, j, c] = results[:, place, :]
                 nc.gpsimd.tensor_tensor(out=results[:, place, :], in0=held["emptied", b, j, c], in1=out_bias[c][:], op=ADD)
 
+        nc.vector.memset(zeros[:], 0.0)
         nc.gpsimd.memset(one_column[:], 0.0)
         make_identity(nc, identity[:])
         nc.scalar.activation(out=one_column[:], in_=one_column[:], func=SIGMOID)
@@ -372,17 +378,23 @@ def tile_aft_full_pb_kernel(tc, x_bytes, x_scale, wq_w, wq_b, r_aft, out_w, out_
         load(out_bias[1], out_b[HALF * 1 : HALF * 2].partition_broadcast(P))
         load(r_raw[3], r_hbm[3])
 
+        warm_up(512)
+        warm_up(512)
+        warm_up(512)
         widen_tile(0, 0, nc.vector.tensor_copy, HALF)
         widen_tile(0, 1, nc.scalar.copy)
         widen_tile(1, 0, nc.scalar.copy)
         widen_tile(1, 1, nc.scalar.copy)
         turn_x(0, 0)
         scale_x(0, 0)
+        warm_up(256)
         turn_weight("wq", 0, 0)
         turn_x(0, 1)
         scale_x(0, 1)
+        warm_up(256)
         turn_weight("wq", 0, 1)
         turn_weight("wq", 1, 0)
+        warm_up(256)
         turn_weight("wq", 1, 1)
         quantise_x(0)
         quantise_wq(0)
@@ -391,6 +403,7 @@ def tile_aft_full_pb_kernel(tc, x_bytes, x_scale, wq_w, wq_b, r_aft, out_w, out_
         widen_tile(2, 0, nc.scalar.copy)
         turn_x(1, 0)
         turn_x(1, 1)
+        warm_up(256)
         turn_only("wq", 2, 0)
         turn_only("wq", 2, 1)
         widen_tile(2, 1, nc.scalar.copy)

@@ -29,7 +29,8 @@ RESULT_BUFS = 9
 SORTED_BUFS = 4
 KIN_BUFS = 4
 LAST = BLOCKS - 1
-OWN = (("wq", 0), ("wq", 3), ("x", 2), ("y", 0), ("y", 1), ("ow", 1), ("y", 2), ("ow", 0), ("last", 0), ("last", 1))
+OWN = (("x", 0), ("wq", 3), ("x", 2), ("y", 0), ("y", 1), ("ow", 3), ("y", 2), ("last", 0), ("last", 1))
+GROUPS = ((("x", 0), ("wq", 0)), (("wq", 1),), (("wq", 2),), (("x", 1),), (("wq", 3),), (("x", 2),), (("ow", 1),), (("y", 0),), (("ow", 0),), (("y", 1),), (("ow", 2),), (("ow", 3),), (("x", 3),), (("y", 2),), (("last", 0),), (("last", 1),))
 
 
 def tile_aft_full_pb_kernel(tc, x_bytes, x_scale, wq_w, wq_b, r_aft, out_w, out_b, out):
@@ -62,19 +63,20 @@ def tile_aft_full_pb_kernel(tc, x_bytes, x_scale, wq_w, wq_b, r_aft, out_w, out_
         wq_first = kept("wq_first", 4, [P, D], BF16)
         wq_raw = [None, None] + kept("wq_raw", PAIRS - 2, [P, 2, D], BF16)
         ow_raw = kept("ow_raw", PAIRS, [P, 2, D], BF16)
-        x_codes = kept("x_codes", BLOCKS, [P, 2, TB], U32)
-        x_scales = kept("x_scales", BLOCKS, [P, 2, TB], U8)
-        wq_codes = kept("wq_codes", PAIRS, [P, 2, 2, P], U32)
-        wq_scales = kept("wq_scales", PAIRS, [P, 2, 2, P], U8)
-        ow_codes = kept("ow_codes", 2, [P, 2, HALF], U32)
-        ow_scales = kept("ow_scales", 2, [P, 2, HALF], U8)
-        y_codes = kept("y_codes", BLOCKS, [P, 2, TB], U32)
-        y_scales = kept("y_scales", BLOCKS, [P, 2, TB], U8)
+        codes, scales = {}, {}
+        for group in GROUPS:
+            width = HALF // 2 if group[0][0] == "last" else HALF
+            group_codes = keep.tile([P, len(group), width], U32, name="%s_codes%d" % group[0], align_bytes=64)
+            group_scales = keep.tile([P, len(group), width], U8, name="%s_scales%d" % group[0], align_bytes=64)
+            codes[group], scales[group] = group_codes, group_scales
+            for place, key in enumerate(group):
+                codes[key], scales[key] = group_codes[:, place, :], group_scales[:, place, :]
         sig = kept("sig", 2 * BLOCKS, [P, TB // 4, 4, 4], F32)
         held = {}
         taken = {"vector": [], "flow": []}
 
         def bank(kind, shape, dtype):
+            kind = held.pop("next_bank", kind)
             count = VECTOR_BANKS if kind == "vector" else FLOW_BANKS
             taken[kind].append(shape)
             return psum.tile(shape, dtype, name="%s%d" % (kind, len(taken[kind]) % count))
@@ -90,11 +92,14 @@ def tile_aft_full_pb_kernel(tc, x_bytes, x_scale, wq_w, wq_b, r_aft, out_w, out_
 
         def kin(key):
             if key not in held:
-                shape = {"ow": [P, 2, 4 * HALF], "last": [P, D]}.get(key[0], [P, 2, 4 * TB])
-                if key in OWN:
-                    held[key] = own_tile(key, shape, BF16)
+                group = [members for members in GROUPS if key in members][0]
+                width = D if key[0] == "last" else 2 * D
+                if group[0] in OWN or len(group) > 1:
+                    held[group] = own_tile(group[0], [P, len(group), width], BF16)
                 else:
-                    held[key] = flow.tile(shape, BF16, name="kin", align_bytes=64, bufs=KIN_BUFS)
+                    held[group] = flow.tile([P, 1, width], BF16, name="kin", align_bytes=64, bufs=KIN_BUFS)
+                for place, member in enumerate(group):
+                    held[member] = held[group][:, place, :].rearrange("p (a c) -> p a c", c=D)
             return held[key]
 
         def warm_up(width):
@@ -140,8 +145,8 @@ def tile_aft_full_pb_kernel(tc, x_bytes, x_scale, wq_w, wq_b, r_aft, out_w, out_
                 in_=rows_of(name, i, s).bitcast(F32).rearrange("p (g c e u) -> p g c u e", g=2, u=2, e=2),
             )
 
-        def sort_tile(name, i, s, copy):
-            ordered = flow.tile([P, HALF], F32, name="ordered", align_bytes=64, bufs=SORTED_BUFS)
+        def sort_tile(name, i, s, copy, key=None):
+            ordered = own_tile(key or ("sorted_" + name, 2 * i + s), [P, HALF], F32)
             for g in range(2):
                 held["sorted", name, i, s, g] = ordered[:, WORDS * g : WORDS * (g + 1)]
             copy(
@@ -157,6 +162,42 @@ def tile_aft_full_pb_kernel(tc, x_bytes, x_scale, wq_w, wq_b, r_aft, out_w, out_
                 out=ordered[:].rearrange("p j (u c e) -> p j c u e", u=2, e=2),
                 in_=r_raw[b][:].bitcast(F32)[:, :, WORDS * f : WORDS * (f + 1)].rearrange("p j (c e u) -> p j c u e", u=2, e=2),
             )
+
+        def sort_half_behind(b, f, key):
+            ordered = own_tile(key, [P, J, WORDS], F32)
+            for j in range(J):
+                held["sorted", "r", b, j, f] = ordered[:, j]
+            nc.gpsimd.tensor_copy(
+                out=ordered[:].bitcast(U32).rearrange("p j (u c) -> p j u c", u=2),
+                in_=r_raw[b][:].bitcast(U32)[:, :, WORDS * f : WORDS * (f + 1)].rearrange("p j (c u) -> p j u c", u=2),
+            )
+
+        def sort_half_on_vector(name, b, f):
+            for j in range(J):
+                if (name, b, f, "ordered") not in held:
+                    held[name, b, f, "ordered"] = own_tile(("ordered_" + name, 2 * b + f), [P, J, WORDS], F32)
+                held["sorted", name, b, j, f] = held[name, b, f, "ordered"][:, j]
+            source = (r_raw[b] if name == "r" else held["wide_block", b])[:].bitcast(F32)
+            nc.vector.tensor_copy(
+                out=held[name, b, f, "ordered"][:].rearrange("p j (u c e) -> p j c u e", u=2, e=2),
+                in_=source[:, :, WORDS * f : WORDS * (f + 1)].rearrange("p j (c e u) -> p j c u e", u=2, e=2),
+            )
+
+        def sort_x(b, key):
+            ordered = own_tile(key, [P, J, HALF], F32)
+            for j in range(J):
+                for g in range(2):
+                    held["sorted", "x", b, j, g] = ordered[:, j, WORDS * g : WORDS * (g + 1)]
+            nc.gpsimd.tensor_copy(
+                out=ordered[:].bitcast(U32).rearrange("p s (g u c) -> p (s g) u c", g=2, u=2),
+                in_=held["wide_block", b][:].bitcast(U32).rearrange("p s (g c u) -> p (s g) u c", g=2, u=2),
+            )
+
+        def widen_part(b, j, copy=nc.scalar.copy):
+            if ("wide_block", b) not in held:
+                held["wide_block", b] = flow.tile([P, J, D], BF16, name="wide_block%d" % b, align_bytes=64)
+            held["wide", b, j] = held["wide_block", b][:, j, :]
+            copy(out=held["wide", b, j], in_=x_raw[b][:, j, :].bitcast(FP8))
 
         def words_of(name, i, s, g, u):
             if ("sorted", name, i, s, g) in held:
@@ -175,8 +216,7 @@ def tile_aft_full_pb_kernel(tc, x_bytes, x_scale, wq_w, wq_b, r_aft, out_w, out_
             if name == "wq":
                 words = kin((name, i))[:, s, :].bitcast(F32).rearrange("p (g w) -> p g w", g=2)
             else:
-                place = 2 * (i % 2) + s
-                words = kin((name, i // 2))[:].bitcast(F32)[:, :, WORDS * place : WORDS * (place + 1)]
+                words = kin((name, i)).bitcast(F32)[:, :, WORDS * s : WORDS * (s + 1)]
             nc.scalar.copy(out=words.rearrange("p g (c i u) -> p g c u i", i=2, u=2), in_=turned[:])
 
         def turn_weight(name, i, s):
@@ -192,6 +232,12 @@ def tile_aft_full_pb_kernel(tc, x_bytes, x_scale, wq_w, wq_b, r_aft, out_w, out_
                         nc.tensor.transpose(turned[:, u, part * P : (part + 1) * P], words_of("x", b, part, g, u), identity[:])
                     else:
                         nc.tensor.transpose(turned[:, part, u * P : (u + 1) * P], words_of("x", 0, g, part, u), identity[:])
+
+        def first_half(g):
+            turned = bank("flow", [P, 2, P], F32)
+            for u in range(2):
+                nc.tensor.transpose(turned[:, u, :], words_of("x", 0, 0, g, u), identity[:])
+            scale(kin(("x", 0))[:, g, :HALF], turned[:], g)
 
         def scale(result, turned, g):
             tokens = turned.shape[2]
@@ -217,34 +263,14 @@ def tile_aft_full_pb_kernel(tc, x_bytes, x_scale, wq_w, wq_b, r_aft, out_w, out_
                 for u in range(2):
                     nc.tensor.transpose(turned[:, j * P // 4 : (j + 1) * P // 4, u, :], words_of("r", b, j, f, u), identity[:])
 
-        def quantise(codes, scales, values):
-            nc.vector.quantize_mx(out=codes.bitcast(FP8X4), scales=scales, in_=values)
-
-        def quantise_x(b):
-            quantise(flat(x_codes[b]), flat(x_scales[b]), flat(held["x", b]))
-
-        def quantise_wq(i):
-            quantise(wq_codes[i][:].rearrange("p s g m -> p (s g m)"), wq_scales[i][:].rearrange("p s g m -> p (s g m)"), flat(held["wq", i]))
-
-        def quantise_ow(c, g):
-            quantise(ow_codes[c][:, g, :], ow_scales[c][:, g, :], held["ow", c][:, g, :])
-
-        def quantise_ow_pair(i):
-            for g in range(2):
-                columns = slice(TB * (i % 2), TB * (i % 2 + 1))
-                values = slice(4 * columns.start, 4 * columns.stop)
-                quantise(ow_codes[i // 2][:, g, columns], ow_scales[i // 2][:, g, columns], held["ow", i // 2][:, g, values])
-
-        def quantise_y(b):
-            quantise(flat(y_codes[b]), flat(y_scales[b]), flat(held["y", b]))
-
-        def quantise_y_tile(b, j):
-            quantise(y_codes[b][:, j, :], y_scales[b][:, j, :], held["last", j][:])
+        def quantise(name, i):
+            group = [members for members in GROUPS if members[0] == (name, i)][0]
+            nc.vector.quantize_mx(out=flat(codes[group]).bitcast(FP8X4), scales=flat(scales[group]), in_=flat(held[group]))
 
         def y_part(tiles, b, j, g):
-            if ("by_tiles", b) in held:
-                return tiles[b][:, j, g * P : (g + 1) * P]
-            return tiles[b][:, g, j * P : (j + 1) * P]
+            if b == LAST:
+                return tiles["last", j][:, g * P : (g + 1) * P]
+            return tiles["y", b][:, g * TB + j * P : g * TB + (j + 1) * P]
 
         def query_only(b, tiles, tokens):
             q = bank("flow", [P, len(tiles), tokens.stop - tokens.start], F32)
@@ -252,12 +278,14 @@ def tile_aft_full_pb_kernel(tc, x_bytes, x_scale, wq_w, wq_b, r_aft, out_w, out_
             for place, (f, t) in enumerate(tiles):
                 i, s = 2 * f + t // 2, t % 2
                 for g in range(2):
+                    stationary = slice((2 * s + g) * P, (2 * s + g + 1) * P)
+                    moving = slice(g * TB + tokens.start, g * TB + tokens.stop)
                     nc.tensor.matmul_mx(
                         out=q[:, place, :],
-                        lhsT=wq_codes[i][:, s, g, :].bitcast(FP8X4),
-                        lhsT_scale=wq_scales[i][:, s, g, :],
-                        rhs=x_codes[b][:, g, tokens].bitcast(FP8X4),
-                        rhs_scale=x_scales[b][:, g, tokens],
+                        lhsT=codes["wq", i][:, stationary].bitcast(FP8X4),
+                        lhsT_scale=scales["wq", i][:, stationary],
+                        rhs=codes["x", b][:, moving].bitcast(FP8X4),
+                        rhs_scale=scales["x", b][:, moving],
                         start=(g == 0),
                         stop=(g == 1),
                     )
@@ -300,9 +328,8 @@ def tile_aft_full_pb_kernel(tc, x_bytes, x_scale, wq_w, wq_b, r_aft, out_w, out_
 
         def gate_tile(b, f, j):
             part = slice(j * P // 4, (j + 1) * P // 4)
-            held["by_tiles", b] = True
             nc.vector.tensor_tensor(
-                out=kin(("last", j))[:, HALF * f : HALF * (f + 1)].rearrange("p (c i u e) -> p c u e i", i=4, u=2, e=2),
+                out=kin(("last", j))[:, 0, HALF * f : HALF * (f + 1)].rearrange("p (c i u e) -> p c u e i", i=4, u=2, e=2),
                 in0=held["r_turned", b, f][:, part],
                 in1=sig[2 * b + f][:, part].rearrange("p c (u e) i -> p c u e i", u=2),
                 op=MULT,
@@ -311,16 +338,17 @@ def tile_aft_full_pb_kernel(tc, x_bytes, x_scale, wq_w, wq_b, r_aft, out_w, out_
         def project(b, j, c):
             sums = bank("flow", [P, HALF], F32)
             held["sums", b, j, c] = sums
-            for g in range(2):
-                nc.tensor.matmul_mx(
-                    out=sums[:],
-                    lhsT=y_part(y_codes, b, j, g).bitcast(FP8X4),
-                    lhsT_scale=y_part(y_scales, b, j, g),
-                    rhs=ow_codes[c][:, g, :].bitcast(FP8X4),
-                    rhs_scale=ow_scales[c][:, g, :],
-                    start=(g == 0),
-                    stop=(g == 1),
-                )
+            for h in range(2):
+                for g in range(2):
+                    nc.tensor.matmul_mx(
+                        out=sums[:, TB * h : TB * (h + 1)],
+                        lhsT=y_part(codes, b, j, g).bitcast(FP8X4),
+                        lhsT_scale=y_part(scales, b, j, g),
+                        rhs=codes["ow", 2 * c + h][:, TB * g : TB * (g + 1)].bitcast(FP8X4),
+                        rhs_scale=scales["ow", 2 * c + h][:, TB * g : TB * (g + 1)],
+                        start=(g == 0),
+                        stop=(g == 1),
+                    )
 
         def store(b, j, c):
             nc.sync.dma_start(out=out_hbm[b][:, j, HALF * c : HALF * (c + 1)], in_=held["result", b, j, c])
@@ -385,8 +413,8 @@ def tile_aft_full_pb_kernel(tc, x_bytes, x_scale, wq_w, wq_b, r_aft, out_w, out_
         widen_tile(0, 1, nc.scalar.copy)
         widen_tile(1, 0, nc.scalar.copy)
         widen_tile(1, 1, nc.scalar.copy)
-        turn_x(0, 0)
-        scale_x(0, 0)
+        first_half(0)
+        first_half(1)
         warm_up(256)
         turn_weight("wq", 0, 0)
         turn_x(0, 1)
@@ -396,10 +424,9 @@ def tile_aft_full_pb_kernel(tc, x_bytes, x_scale, wq_w, wq_b, r_aft, out_w, out_
         turn_weight("wq", 1, 0)
         warm_up(256)
         turn_weight("wq", 1, 1)
-        quantise_x(0)
-        quantise_wq(0)
-        quantise_wq(1)
-        sort_pair("wq", 3, ("wq", 0))
+        quantise("x", 0)
+        quantise("wq", 1)
+        sort_pair("wq", 3, ("x", 0))
         widen_tile(2, 0, nc.scalar.copy)
         turn_x(1, 0)
         turn_x(1, 1)
@@ -411,8 +438,8 @@ def tile_aft_full_pb_kernel(tc, x_bytes, x_scale, wq_w, wq_b, r_aft, out_w, out_
         empty_weight("wq", 2, 1)
         scale_x(1, 0)
         scale_x(1, 1)
-        quantise_x(1)
-        quantise_wq(2)
+        quantise("wq", 2)
+        quantise("x", 1)
         query(0, 0)
         query(0, 1)
         sort_half(0, 0)
@@ -423,11 +450,11 @@ def tile_aft_full_pb_kernel(tc, x_bytes, x_scale, wq_w, wq_b, r_aft, out_w, out_
         turn_r(0, 0)
         sort_half(0, 1)
         scale_x(2, 0)
-        quantise_wq(3)
+        quantise("wq", 3)
         sort_pair("ow", 0, ("wq", 3))
         scale_x(2, 1)
         gate(0, 0)
-        quantise_x(2)
+        quantise("x", 2)
         widen_tile(3, 0, nc.gpsimd.tensor_copy, D, ("x", 2))
         query(0, 2)
         query(1, 0)
@@ -443,9 +470,9 @@ def tile_aft_full_pb_kernel(tc, x_bytes, x_scale, wq_w, wq_b, r_aft, out_w, out_
         turn_r(1, 1)
         gate(1, 0)
         gate(0, 1)
-        quantise_ow_pair(1)
-        quantise_y(0)
-        quantise_ow_pair(0)
+        quantise("ow", 1)
+        quantise("y", 0)
+        quantise("ow", 0)
         sort_pair("ow", 2, ("y", 0))
         query(1, 2)
         query(1, 3)
@@ -456,11 +483,11 @@ def tile_aft_full_pb_kernel(tc, x_bytes, x_scale, wq_w, wq_b, r_aft, out_w, out_
         query(2, 2)
         project(0, 0, 0)
         project(0, 1, 0)
+        empty(0, 1, 0)
         sort_rows("ow", 3, 1)
         finish(0, 0, 0)
-        finish(0, 1, 0)
-        quantise_y(1)
-        sort_pair("r", 2, ("y", 1))
+        quantise("y", 1)
+        add_behind(("y", 1), (0, 1, 0))
         turn_x(3, 0)
         turn_x(3, 1)
         turn_weight("ow", 2, 0)
@@ -469,15 +496,16 @@ def tile_aft_full_pb_kernel(tc, x_bytes, x_scale, wq_w, wq_b, r_aft, out_w, out_
         turn_weight("ow", 3, 1)
         scale_x(3, 0)
         scale_x(3, 1)
-        quantise_ow_pair(2)
-        quantise_ow_pair(3)
-        quantise_x(3)
+        store(0, 1, 0)
+        quantise("ow", 2)
+        quantise("ow", 3)
+        quantise("x", 3)
         project(1, 0, 0)
         project(1, 1, 0)
         empty(1, 0, 0)
         query(2, 3)
         empty(1, 1, 0)
-        add_behind(("ow", 1), (1, 0, 0), (1, 1, 0))
+        add_behind(("ow", 3), (1, 0, 0), (1, 1, 0))
         sort_rows("r", 3, 0)
         turn_r(2, 0)
         turn_r(2, 1)
@@ -490,7 +518,7 @@ def tile_aft_full_pb_kernel(tc, x_bytes, x_scale, wq_w, wq_b, r_aft, out_w, out_
         gate(2, 1)
         store(1, 1, 0)
         finish(0, 1, 1)
-        quantise_y(2)
+        quantise("y", 2)
         add_behind(("y", 2), (0, 0, 1))
         query_half(3, 0, 0)
         query_half(3, 0, 1)
@@ -505,7 +533,7 @@ def tile_aft_full_pb_kernel(tc, x_bytes, x_scale, wq_w, wq_b, r_aft, out_w, out_
         gate_tile(3, 1, 0)
         finish(1, 1, 1)
         empty(2, 0, 0)
-        quantise_y_tile(3, 0)
+        quantise("last", 0)
         store(0, 0, 1)
         add_behind(("last", 0), (1, 0, 1), (2, 0, 0))
         finish(2, 1, 0)
@@ -523,7 +551,7 @@ def tile_aft_full_pb_kernel(tc, x_bytes, x_scale, wq_w, wq_b, r_aft, out_w, out_
         gate_tile(3, 1, 1)
         store(2, 0, 0)
         finish(2, 1, 1)
-        quantise_y_tile(3, 1)
+        quantise("last", 1)
         finish(3, 0, 0)
         finish(3, 0, 1)
         project(3, 1, 0)

@@ -380,11 +380,12 @@ def tile_aft_full_pb_kernel(tc, x_bytes, x_scale, wq_w, wq_b, r_aft, out_w, out_
         nc.vector.memset(zeros[:], 0.0)
         nc.gpsimd.memset(one_column[:], 0.0)
         make_identity(nc, identity[:])
+        nc.scalar.dma_start(out=x_mult[:], in_=x_scale[0, :, :].rearrange("o (g p t) -> p (o g) t", p=P, t=4))
+        nc.scalar.dma_start(out=query_bias[:], in_=wq_b.rearrange("(f p t) -> p f t", p=P, t=4))
         nc.scalar.activation(out=one_column[:], in_=one_column[:], func=SIGMOID)
 
         load(x_first[0], x_hbm[0][:, 0, :])
         load(x_first[1], x_hbm[0][:, 1, :])
-        load(x_mult, x_scale[0, :, :].rearrange("o (g p t) -> p (o g) t", p=P, t=4))
         load(wq_first[0], wq_hbm[0][0][:, 0, :])
         load(x_raw[1], x_hbm[1])
         load(wq_first[1], wq_hbm[0][0][:, 1, :])
@@ -393,7 +394,6 @@ def tile_aft_full_pb_kernel(tc, x_bytes, x_scale, wq_w, wq_b, r_aft, out_w, out_
         load(x_raw[2], x_hbm[2])
         load(wq_raw[2], wq_hbm[1][0])
         load(wq_raw[3], wq_hbm[1][1])
-        load(query_bias, wq_b.rearrange("(f p t) -> p f t", p=P, t=4))
         load(r_raw[0], r_hbm[0])
         load(x_raw[3], x_hbm[3])
         load(ow_raw[0], ow_hbm[0])
@@ -483,11 +483,11 @@ def tile_aft_full_pb_kernel(tc, x_bytes, x_scale, wq_w, wq_b, r_aft, out_w, out_
         query(2, 2)
         project(0, 0, 0)
         project(0, 1, 0)
-        empty(0, 1, 0)
         sort_rows("ow", 3, 1)
         finish(0, 0, 0)
+        finish(0, 1, 0)
         quantise("y", 1)
-        add_behind(("y", 1), (0, 1, 0))
+        sort_pair("r", 2, ("y", 1))
         turn_x(3, 0)
         turn_x(3, 1)
         turn_weight("ow", 2, 0)
@@ -496,7 +496,6 @@ def tile_aft_full_pb_kernel(tc, x_bytes, x_scale, wq_w, wq_b, r_aft, out_w, out_
         turn_weight("ow", 3, 1)
         scale_x(3, 0)
         scale_x(3, 1)
-        store(0, 1, 0)
         quantise("ow", 2)
         quantise("ow", 3)
         quantise("x", 3)
@@ -557,4 +556,4 @@ def tile_aft_full_pb_kernel(tc, x_bytes, x_scale, wq_w, wq_b, r_aft, out_w, out_
         project(3, 1, 0)
         project(3, 1, 1)
         finish(3, 1, 0)
-        finish_by_halves(3, 1, 1)
+        finish(3, 1, 1)

from contextlib import ExitStack

import concourse.mybir as mybir
from concourse.masks import make_identity

F32 = mybir.dt.float32
BF16 = mybir.dt.bfloat16
U32 = mybir.dt.uint32
U8 = mybir.dt.uint8
FP8 = mybir.dt.float8_e4m3fn
FP8X4 = mybir.dt.float8_e4m3fn_x4
MULT = mybir.AluOpType.mult
ADD = mybir.AluOpType.add
SIGMOID = mybir.ActivationFunctionType.Sigmoid

P = 128
TOKENS = 1024
D = 1024
FLOPS = 2 * 2 * TOKENS * D * D
BLOCKS = 4
TB = TOKENS // BLOCKS
J = TB // P
PAIRS = 4
HALF = 512
WORDS = HALF // 2
VECTOR_BANKS = 3
FLOW_BANKS = 5
RESULT_BUFS = 9
SORTED_BUFS = 4
KIN_BUFS = 4
LAST = BLOCKS - 1
OWN = (("x", 0), ("wq", 3), ("x", 2), ("y", 0), ("y", 1), ("ow", 3), ("y", 2), ("last", 0), ("last", 1))
GROUPS = ((("x", 0), ("wq", 0)), (("wq", 1),), (("wq", 2),), (("x", 1),), (("wq", 3),), (("x", 2),), (("ow", 1),), (("y", 0),), (("ow", 0),), (("y", 1),), (("ow", 2),), (("ow", 3),), (("x", 3),), (("y", 2),), (("last", 0),), (("last", 1),))


def tile_aft_full_pb_kernel(tc, x_bytes, x_scale, wq_w, wq_b, r_aft, out_w, out_b, out):
    nc = tc.nc
    x_hbm = x_bytes[0, :, :].rearrange("(b p j) k -> b p j k", b=BLOCKS, p=P)
    r_hbm = r_aft[0, :, :].rearrange("(b p j) k -> b p j k", b=BLOCKS, p=P)
    out_hbm = out[0, :, :].rearrange("(b p j) n -> b p j n", b=BLOCKS, p=P)
    wq_hbm = wq_w.rearrange("(f m h s) k -> f h m s k", f=2, m=P, h=2)
    ow_hbm = out_w.rearrange("(i s m) k -> i m s k", i=PAIRS, m=P)

    with ExitStack() as ctx:
        keep = ctx.enter_context(tc.tile_pool(name="keep", bufs=1))
        flow = ctx.enter_context(tc.tile_pool(name="flow", bufs=1))
        psum = ctx.enter_context(tc.psum_pool(name="psum", bufs=1))
        ctx.enter_context(tc.manual_schedule())

        x_mult = keep.tile([P, 2, 4], F32)
        query_bias = keep.tile([P, 2, 4], BF16)
        out_bias = [keep.tile([P, HALF], BF16, name="out_bias%d" % c) for c in range(2)]
        identity = keep.tile([P, P], F32)
        one_column = keep.tile([P, 1], F32)
        zeros = keep.tile([P, HALF], BF16, align_bytes=64)

        def kept(name, count, shape, dtype):
            return [keep.tile(shape, dtype, name="%s%d" % (name, i), align_bytes=64) for i in range(count)]

        x_first = kept("x_first", J, [P, D], U8)
        x_raw = [None] + kept("x_raw", LAST, [P, J, D], U8)
        r_raw = kept("r_raw", BLOCKS, [P, J, D], BF16)
        wq_first = kept("wq_first", 4, [P, D], BF16)
        wq_raw = [None, None] + kept("wq_raw", PAIRS - 2, [P, 2, D], BF16)
        ow_raw = kept("ow_raw", PAIRS, [P, 2, D], BF16)
        codes, scales = {}, {}
        for group in GROUPS:
            width = HALF // 2 if group[0][0] == "last" else HALF
            group_codes = keep.tile([P, len(group), width], U32, name="%s_codes%d" % group[0], align_bytes=64)
            group_scales = keep.tile([P, len(group), width], U8, name="%s_scales%d" % group[0], align_bytes=64)
            codes[group], scales[group] = group_codes, group_scales
            for place, key in enumerate(group):
                codes[key], scales[key] = group_codes[:, place, :], group_scales[:, place, :]
        sig = kept("sig", 2 * BLOCKS, [P, TB // 4, 4, 4], F32)
        held = {}
        taken = {"vector": [], "flow": []}

        def bank(kind, shape, dtype):
            kind = held.pop("next_bank", kind)
            count = VECTOR_BANKS if kind == "vector" else FLOW_BANKS
            taken[kind].append(shape)
            return psum.tile(shape, dtype, name="%s%d" % (kind, len(taken[kind]) % count))

        def load(tile, source):
            nc.sync.dma_start(out=tile[:], in_=source)

        def flat(tile):
            return tile[:].rearrange("p a c -> p (a c)")

        def own_tile(key, shape, dtype):
            return flow.tile(shape, dtype, name="%s_in%d" % key, align_bytes=64)

        def kin(key):
            if key not in held:
                group = [members for members in GROUPS if key in members][0]
                width = D if key[0] == "last" else 2 * D
                if group[0] in OWN or len(group) > 1:
                    held[group] = own_tile(group[0], [P, len(group), width], BF16)
                else:
                    held[group] = flow.tile([P, 1, width], BF16, name="kin", align_bytes=64, bufs=KIN_BUFS)
                for place, member in enumerate(group):
                    held[member] = held[group][:, place, :].rearrange("p (a c) -> p a c", c=D)
            return held[key]

        def warm_up(width):
            place = bank("flow", [P, HALF], F32)
            nc.tensor.matmul(out=place[:, :width], lhsT=zeros[:, :P], rhs=zeros[:, :width], start=True, stop=True)

        def rows_of(name, i, s):
            if name == "x":
                return held["wide", i, s]
            if name == "wq":
                return wq_raw[i][:, s, :] if i >= 2 else wq_first[2 * i + s][:]
            return (r_raw if name == "r" else ow_raw)[i][:, s, :]

        def widen_tile(b, j, copy, width=D, key=None):
            wide = own_tile(key, [P, D], BF16) if key else flow.tile([P, D], BF16, name="wide%d_%d" % (b, j), align_bytes=64)
            held["wide", b, j] = wide[:]
            source = x_raw[b][:, j, :] if b else x_first[j][:]
            for first in range(0, D, width):
                copy(out=wide[:, first : first + width], in_=source[:, first : first + width].bitcast(FP8))

        def widen_block(b, key=None):
            wide = own_tile(key or ("wide", b), [P, J, D], BF16)
            for j in range(J):
                held["wide", b, j] = wide[:, j, :]
            nc.gpsimd.tensor_copy(out=flat(wide), in_=flat(x_raw[b]).bitcast(FP8))

        def sort_pair(name, i, key):
            ordered = own_tile(key, [P, 2, HALF], F32)
            for s in range(2):
                for g in range(2):
                    held["sorted", name, i, s, g] = ordered[:, s, WORDS * g : WORDS * (g + 1)]
            nc.gpsimd.tensor_copy(
                out=ordered[:].bitcast(U32).rearrange("p s (g u c) -> p (s g) u c", g=2, u=2),
                in_={"r": r_raw, "ow": ow_raw, "wq": wq_raw}[name][i][:].bitcast(U32).rearrange("p s (g c u) -> p (s g) u c", g=2, u=2),
            )

        def sort_rows(name, i, s):
            ordered = flow.tile([P, HALF], F32, name="ordered", align_bytes=64, bufs=SORTED_BUFS)
            for g in range(2):
                held["sorted", name, i, s, g] = ordered[:, WORDS * g : WORDS * (g + 1)]
            nc.scalar.copy(
                out=ordered[:].rearrange("p (g u c e) -> p g c u e", g=2, u=2, e=2),
                in_=rows_of(name, i, s).bitcast(F32).rearrange("p (g c e u) -> p g c u e", g=2, u=2, e=2),
            )

        def sort_tile(name, i, s, copy, key=None):
            ordered = own_tile(key or ("sorted_" + name, 2 * i + s), [P, HALF], F32)
            for g in range(2):
                held["sorted", name, i, s, g] = ordered[:, WORDS * g : WORDS * (g + 1)]
            copy(
                out=ordered[:].bitcast(U32).rearrange("p (g u c) -> p g u c", g=2, u=2),
                in_=rows_of(name, i, s).bitcast(U32).rearrange("p (g c u) -> p g u c", g=2, u=2),
            )

        def sort_half(b, f):
            ordered = flow.tile([P, J, WORDS], F32, name="ordered", align_bytes=64, bufs=SORTED_BUFS)
            for j in range(J):
                held["sorted", "r", b, j, f] = ordered[:, j]
            nc.scalar.copy(
                out=ordered[:].rearrange("p j (u c e) -> p j c u e", u=2, e=2),
                in_=r_raw[b][:].bitcast(F32)[:, :, WORDS * f : WORDS * (f + 1)].rearrange("p j (c e u) -> p j c u e", u=2, e=2),
            )

        def sort_half_behind(b, f, key):
            ordered = own_tile(key, [P, J, WORDS], F32)
            for j in range(J):
                held["sorted", "r", b, j, f] = ordered[:, j]
            nc.gpsimd.tensor_copy(
                out=ordered[:].bitcast(U32).rearrange("p j (u c) -> p j u c", u=2),
                in_=r_raw[b][:].bitcast(U32)[:, :, WORDS * f : WORDS * (f + 1)].rearrange("p j (c u) -> p j u c", u=2),
            )

        def sort_half_on_vector(name, b, f):
            for j in range(J):
                if (name, b, f, "ordered") not in held:
                    held[name, b, f, "ordered"] = own_tile(("ordered_" + name, 2 * b + f), [P, J, WORDS], F32)
                held["sorted", name, b, j, f] = held[name, b, f, "ordered"][:, j]
            source = (r_raw[b] if name == "r" else held["wide_block", b])[:].bitcast(F32)
            nc.vector.tensor_copy(
                out=held[name, b, f, "ordered"][:].rearrange("p j (u c e) -> p j c u e", u=2, e=2),
                in_=source[:, :, WORDS * f : WORDS * (f + 1)].rearrange("p j (c e u) -> p j c u e", u=2, e=2),
            )

        def sort_x(b, key):
            ordered = own_tile(key, [P, J, HALF], F32)
            for j in range(J):
                for g in range(2):
                    held["sorted", "x", b, j, g] = ordered[:, j, WORDS * g : WORDS * (g + 1)]
            nc.gpsimd.tensor_copy(
                out=ordered[:].bitcast(U32).rearrange("p s (g u c) -> p (s g) u c", g=2, u=2),
                in_=held["wide_block", b][:].bitcast(U32).rearrange("p s (g c u) -> p (s g) u c", g=2, u=2),
            )

        def widen_part(b, j, copy=nc.scalar.copy):
            if ("wide_block", b) not in held:
                held["wide_block", b] = flow.tile([P, J, D], BF16, name="wide_block%d" % b, align_bytes=64)
            held["wide", b, j] = held["wide_block", b][:, j, :]
            copy(out=held["wide", b, j], in_=x_raw[b][:, j, :].bitcast(FP8))

        def words_of(name, i, s, g, u):
            if ("sorted", name, i, s, g) in held:
                return held["sorted", name, i, s, g][:, P * u : P * (u + 1)]
            return rows_of(name, i, s).bitcast(F32)[:, WORDS * g + u : WORDS * (g + 1) : 2]

        def turn_only(name, i, s):
            turned = bank("flow", [P, 2, P // 2, 2, 2], F32)
            for g in range(2):
                for u in range(2):
                    nc.tensor.transpose(turned[:, g, :, u, :], words_of(name, i, s, g, u), identity[:])
            held["turned", name, i, s] = turned

        def empty_weight(name, i, s):
            turned = held["turned", name, i, s]
            if name == "wq":
                words = kin((name, i))[:, s, :].bitcast(F32).rearrange("p (g w) -> p g w", g=2)
            else:
                words = kin((name, i)).bitcast(F32)[:, :, WORDS * s : WORDS * (s + 1)]
            nc.scalar.copy(out=words.rearrange("p g (c i u) -> p g c u i", i=2, u=2), in_=turned[:])

        def turn_weight(name, i, s):
            turn_only(name, i, s)
            empty_weight(name, i, s)

        def turn_x(b, g):
            turned = bank("vector", [P, 2, TB], F32)
            held["x_turned", b, g] = turned
            for part in range(2):
                for u in range(2):
                    if b:
                        nc.tensor.transpose(turned[:, u, part * P : (part + 1) * P], words_of("x", b, part, g, u), identity[:])
                    else:
                        nc.tensor.transpose(turned[:, part, u * P : (u + 1) * P], words_of("x", 0, g, part, u), identity[:])

        def first_half(g):
            turned = bank("flow", [P, 2, P], F32)
            for u in range(2):
                nc.tensor.transpose(turned[:, u, :], words_of("x", 0, 0, g, u), identity[:])
            scale(kin(("x", 0))[:, g, :HALF], turned[:], g)

        def scale(result, turned, g):
            tokens = turned.shape[2]
            nc.vector.tensor_tensor(
                out=result.rearrange("p (n u e) -> p n u e", u=2, e=2),
                in0=turned.bitcast(BF16).rearrange("p u (n e) -> p n u e", e=2),
                in1=x_mult[:, g, :].rearrange("p (n u e) -> p n u e", n=1, u=2).to_broadcast([P, tokens, 2, 2]),
                op=MULT,
            )

        def scale_x(b, g):
            turned = held["x_turned", b, g]
            if b:
                scale(kin(("x", b))[:, g, :], turned[:], g)
            else:
                for part in range(2):
                    scale(kin(("x", 0))[:, part, HALF * g : HALF * (g + 1)], turned[:, part, :].rearrange("p (u n) -> p u n", u=2), part)

        def turn_r(b, f):
            turned = bank("vector", [P, TB // 4, 2, 4], F32)
            held["r_turned", b, f] = turned[:].bitcast(BF16).rearrange("p c u (i e) -> p c u e i", e=2)
            for j in range(J):
                for u in range(2):
                    nc.tensor.transpose(turned[:, j * P // 4 : (j + 1) * P // 4, u, :], words_of("r", b, j, f, u), identity[:])

        def quantise(name, i):
            group = [members for members in GROUPS if members[0] == (name, i)][0]
            nc.vector.quantize_mx(out=flat(codes[group]).bitcast(FP8X4), scales=flat(scales[group]), in_=flat(held[group]))

        def y_part(tiles, b, j, g):
            if b == LAST:
                return tiles["last", j][:, g * P : (g + 1) * P]
            return tiles["y", b][:, g * TB + j * P : g * TB + (j + 1) * P]

        def query_only(b, tiles, tokens):
            q = bank("flow", [P, len(tiles), tokens.stop - tokens.start], F32)
            held["query", b, tiles[0], tokens.start] = q
            for place, (f, t) in enumerate(tiles):
                i, s = 2 * f + t // 2, t % 2
                for g in range(2):
                    stationary = slice((2 * s + g) * P, (2 * s + g + 1) * P)
                    moving = slice(g * TB + tokens.start, g * TB + tokens.stop)
                    nc.tensor.matmul_mx(
                        out=q[:, place, :],
                        lhsT=codes["wq", i][:, stationary].bitcast(FP8X4),
                        lhsT_scale=scales["wq", i][:, stationary],
                        rhs=codes["x", b][:, moving].bitcast(FP8X4),
                        rhs_scale=scales["x", b][:, moving],
                        start=(g == 0),
                        stop=(g == 1),
                    )

        def sigmoids(b, tiles, tokens):
            q = held["query", b, tiles[0], tokens.start]
            for place, (f, t) in enumerate(tiles):
                nc.scalar.activation(
                    out=sig[2 * b + f][:, tokens.start // 4 : tokens.stop // 4, t, :],
                    in_=q[:, place, :].rearrange("p (c i) -> p c i", i=4),
                    func=SIGMOID,
                    bias=query_bias[:, f, t : t + 1],
                )

        def pair_tiles(i):
            return [(i // 2, 2 * (i % 2) + s) for s in range(2)]

        def query_pair(b, i):
            query_only(b, pair_tiles(i), slice(0, TB))

        def sigmoid_pair(b, i):
            sigmoids(b, pair_tiles(i), slice(0, TB))

        def query(b, i, tokens=slice(0, TB)):
            query_only(b, pair_tiles(i), tokens)
            sigmoids(b, pair_tiles(i), tokens)

        def query_half(b, j, f):
            tiles = [(f, t) for t in range(4)]
            query_only(b, tiles, slice(P * j, P * (j + 1)))
            sigmoids(b, tiles, slice(P * j, P * (j + 1)))

        def gate(b, f):
            nc.vector.tensor_tensor(
                out=kin(("y", b))[:, f, :].rearrange("p (c i u e) -> p c u e i", i=4, u=2, e=2),
                in0=held["r_turned", b, f],
                in1=sig[2 * b + f][:].rearrange("p c (u e) i -> p c u e i", u=2),
                op=MULT,
            )

        def gate_tile(b, f, j):
            part = slice(j * P // 4, (j + 1) * P // 4)
            nc.vector.tensor_tensor(
                out=kin(("last", j))[:, 0, HALF * f : HALF * (f + 1)].rearrange("p (c i u e) -> p c u e i", i=4, u=2, e=2),
                in0=held["r_turned", b, f][:, part],
                in1=sig[2 * b + f][:, part].rearrange("p c (u e) i -> p c u e i", u=2),
                op=MULT,
            )

        def project(b, j, c):
            sums = bank("flow", [P, HALF], F32)
            held["sums", b, j, c] = sums
            for h in range(2):
                for g in range(2):
                    nc.tensor.matmul_mx(
                        out=sums[:, TB * h : TB * (h + 1)],
                        lhsT=y_part(codes, b, j, g).bitcast(FP8X4),
                        lhsT_scale=y_part(scales, b, j, g),
                        rhs=codes["ow", 2 * c + h][:, TB * g : TB * (g + 1)].bitcast(FP8X4),
                        rhs_scale=scales["ow", 2 * c + h][:, TB * g : TB * (g + 1)],
                        start=(g == 0),
                        stop=(g == 1),
                    )

        def store(b, j, c):
            nc.sync.dma_start(out=out_hbm[b][:, j, HALF * c : HALF * (c + 1)], in_=held["result", b, j, c])

        def finish(b, j, c):
            result = flow.tile([P, HALF], F32, name="result", align_bytes=64, bufs=RESULT_BUFS)
            held["result", b, j, c] = result[:]
            nc.vector.tensor_tensor(out=result[:], in0=held["sums", b, j, c][:], in1=out_bias[c][:], op=ADD)
            store(b, j, c)

        def finish_by_halves(b, j, c):
            for h in range(2):
                part = slice(TB * h, TB * (h + 1))
                result = flow.tile([P, TB], F32, name="result", align_bytes=64, bufs=RESULT_BUFS)
                nc.vector.tensor_tensor(out=result[:], in0=held["sums", b, j, c][:, part], in1=out_bias[c][:, part], op=ADD)
                nc.sync.dma_start(out=out_hbm[b][:, j, HALF * c + TB * h : HALF * c + TB * (h + 1)], in_=result[:])

        def empty(b, j, c):
            result = flow.tile([P, HALF], F32, name="result", align_bytes=64, bufs=RESULT_BUFS)
            held["emptied", b, j, c] = result[:]
            nc.scalar.copy(out=result[:], in_=held["sums", b, j, c][:])

        def add_behind(key, *tiles):
            results = own_tile(key, [P, len(tiles), HALF], F32)
            for place, (b, j, c) in enumerate(tiles):
                held["result", b, j, c] = results[:, place, :]
                nc.gpsimd.tensor_tensor(out=results[:, place, :], in0=held["emptied", b, j, c], in1=out_bias[c][:], op=ADD)

        nc.vector.memset(zeros[:], 0.0)
        nc.gpsimd.memset(one_column[:], 0.0)
        make_identity(nc, identity[:])
        nc.scalar.dma_start(out=x_mult[:], in_=x_scale[0, :, :].rearrange("o (g p t) -> p (o g) t", p=P, t=4))
        nc.scalar.dma_start(out=query_bias[:], in_=wq_b.rearrange("(f p t) -> p f t", p=P, t=4))
        nc.scalar.activation(out=one_column[:], in_=one_column[:], func=SIGMOID)

        load(x_first[0], x_hbm[0][:, 0, :])
        load(x_first[1], x_hbm[0][:, 1, :])
        load(wq_first[0], wq_hbm[0][0][:, 0, :])
        load(x_raw[1], x_hbm[1])
        load(wq_first[1], wq_hbm[0][0][:, 1, :])
        load(wq_first[2], wq_hbm[0][1][:, 0, :])
        load(wq_first[3], wq_hbm[0][1][:, 1, :])
        load(x_raw[2], x_hbm[2])
        load(wq_raw[2], wq_hbm[1][0])
        load(wq_raw[3], wq_hbm[1][1])
        load(r_raw[0], r_hbm[0])
        load(x_raw[3], x_hbm[3])
        load(ow_raw[0], ow_hbm[0])
        load(r_raw[1], r_hbm[1])
        load(ow_raw[1], ow_hbm[1])
        load(ow_raw[2], ow_hbm[2])
        load(ow_raw[3], ow_hbm[3])
        load(out_bias[0], out_b[HALF * 0 : HALF * 1].partition_broadcast(P))
        load(r_raw[2], r_hbm[2])
        load(out_bias[1], out_b[HALF * 1 : HALF * 2].partition_broadcast(P))
        load(r_raw[3], r_hbm[3])

        warm_up(512)
        warm_up(512)
        warm_up(512)
        widen_tile(0, 0, nc.vector.tensor_copy, HALF)
        widen_tile(0, 1, nc.scalar.copy)
        widen_tile(1, 0, nc.scalar.copy)
        widen_tile(1, 1, nc.scalar.copy)
        first_half(0)
        first_half(1)
        warm_up(256)
        turn_weight("wq", 0, 0)
        turn_x(0, 1)
        scale_x(0, 1)
        warm_up(256)
        turn_weight("wq", 0, 1)
        turn_weight("wq", 1, 0)
        warm_up(256)
        turn_weight("wq", 1, 1)
        quantise("x", 0)
        quantise("wq", 1)
        sort_pair("wq", 3, ("x", 0))
        widen_tile(2, 0, nc.scalar.copy)
        turn_x(1, 0)
        turn_x(1, 1)
        warm_up(256)
        turn_only("wq", 2, 0)
        turn_only("wq", 2, 1)
        widen_tile(2, 1, nc.scalar.copy)
        empty_weight("wq", 2, 0)
        empty_weight("wq", 2, 1)
        scale_x(1, 0)
        scale_x(1, 1)
        quantise("wq", 2)
        quantise("x", 1)
        query(0, 0)
        query(0, 1)
        sort_half(0, 0)
        turn_x(2, 0)
        turn_x(2, 1)
        turn_weight("wq", 3, 0)
        turn_weight("wq", 3, 1)
        turn_r(0, 0)
        sort_half(0, 1)
        scale_x(2, 0)
        quantise("wq", 3)
        sort_pair("ow", 0, ("wq", 3))
        scale_x(2, 1)
        gate(0, 0)
        quantise("x", 2)
        widen_tile(3, 0, nc.gpsimd.tensor_copy, D, ("x", 2))
        query(0, 2)
        query(1, 0)
        query(1, 1)
        query(0, 3)
        widen_tile(3, 1, nc.scalar.copy)
        turn_r(1, 0)
        turn_r(0, 1)
        turn_weight("ow", 1, 0)
        turn_weight("ow", 1, 1)
        turn_weight("ow", 0, 0)
        turn_weight("ow", 0, 1)
        turn_r(1, 1)
        gate(1, 0)
        gate(0, 1)
        quantise("ow", 1)
        quantise("y", 0)
        quantise("ow", 0)
        sort_pair("ow", 2, ("y", 0))
        query(1, 2)
        query(1, 3)
        query(2, 0)
        query(2, 1)
        gate(1, 1)
        sort_rows("ow", 3, 0)
        query(2, 2)
        project(0, 0, 0)
        project(0, 1, 0)
        sort_rows("ow", 3, 1)
        finish(0, 0, 0)
        finish(0, 1, 0)
        quantise("y", 1)
        sort_pair("r", 2, ("y", 1))
        turn_x(3, 0)
        turn_x(3, 1)
        turn_weight("ow", 2, 0)
        turn_weight("ow", 2, 1)
        turn_weight("ow", 3, 0)
        turn_weight("ow", 3, 1)
        scale_x(3, 0)
        scale_x(3, 1)
        quantise("ow", 2)
        quantise("ow", 3)
        quantise("x", 3)
        project(1, 0, 0)
        project(1, 1, 0)
        empty(1, 0, 0)
        query(2, 3)
        empty(1, 1, 0)
        add_behind(("ow", 3), (1, 0, 0), (1, 1, 0))
        sort_rows("r", 3, 0)
        turn_r(2, 0)
        turn_r(2, 1)
        project(0, 0, 1)
        project(0, 1, 1)
        empty(0, 0, 1)
        sort_rows("r", 3, 1)
        gate(2, 0)
        store(1, 0, 0)
        gate(2, 1)
        store(1, 1, 0)
        finish(0, 1, 1)
        quantise("y", 2)
        add_behind(("y", 2), (0, 0, 1))
        query_half(3, 0, 0)
        query_half(3, 0, 1)
        turn_r(3, 0)
        turn_r(3, 1)
        project(1, 0, 1)
        project(1, 1, 1)
        project(2, 0, 0)
        project(2, 1, 0)
        empty(1, 0, 1)
        gate_tile(3, 0, 0)
        gate_tile(3, 1, 0)
        finish(1, 1, 1)
        empty(2, 0, 0)
        quantise("last", 0)
        store(0, 0, 1)
        add_behind(("last", 0), (1, 0, 1), (2, 0, 0))
        finish(2, 1, 0)
        query(3, 0, slice(P * 1, P * 2))
        query(3, 1, slice(P * 1, P * 2))
        query(3, 2, slice(P * 1, P * 2))
        query(3, 3, slice(P * 1, P * 2))
        project(2, 0, 1)
        project(2, 1, 1)
        project(3, 0, 0)
        project(3, 0, 1)
        gate_tile(3, 0, 1)
        store(1, 0, 1)
        finish(2, 0, 1)
        gate_tile(3, 1, 1)
        store(2, 0, 0)
        finish(2, 1, 1)
        quantise("last", 1)
        finish(3, 0, 0)
        finish(3, 0, 1)
        project(3, 1, 0)
        project(3, 1, 1)
        finish(3, 1, 0)
        finish(3, 1, 1)
